import numpy as np
import ml_dtypes


def mxq(x, axis, fmt="e4m3"):
    dtype, down = {"e4m3": (ml_dtypes.float8_e4m3fn, 7), "e5m2": (ml_dtypes.float8_e5m2, 14)}[fmt]
    v = np.moveaxis(np.asarray(x, np.float32).astype(ml_dtypes.bfloat16).astype(np.float64), axis, -1)
    blocks = v.reshape(v.shape[:-1] + (-1, 32))
    amax = np.abs(blocks).max(-1, keepdims=True)
    byte = np.maximum(np.where(amax > 0, np.frexp(amax)[1] - 1 + 127, 0) - down, 1)
    scale = np.exp2(byte - 127.0)
    codes = (blocks / scale).astype(np.float32).astype(dtype).astype(np.float64)
    return np.moveaxis((codes * scale).reshape(v.shape), -1, axis)


WIDE = False


def mx_kscale(k):
    if not WIDE:
        return np.ones(k)
    levels = np.array([10, -10, 5, -5, 0])
    if k % 512:
        return np.exp2(np.random.permutation(np.resize(levels, k // 32))).repeat(32)
    a = np.empty((k // 512, 16))
    for p in range(k // 512):
        a[p, :8] = np.random.permutation(np.resize(levels, 8))
        for g in range(8):
            far = levels[np.abs(levels - a[p, g]) >= 10]
            a[p, g + 8] = far[np.random.randint(len(far))]
    return np.exp2(a.ravel()).repeat(32)


BF16 = ml_dtypes.bfloat16


def bf(x):
    return np.asarray(x, np.float32).astype(BF16)


def f64(x):
    return np.asarray(x).astype(np.float64)


E2M1 = np.array([0.0, 0.5, 1.0, 1.5, 2.0, 3.0, 4.0, 6.0, -0.0, -0.5, -1.0, -1.5, -2.0, -3.0, -4.0, -6.0])


def pack_weight(w, fmt):
    k, n = w.shape
    w = f64(bf(w)).reshape(k // 32, 32, n)
    amax = np.abs(w).max(1)
    if fmt == "e4m3":
        byte = np.frexp(amax)[1] - 1 + 127 - 7
    else:
        mant, ex = np.frexp(amax / 6.0)
        byte = np.where(mant > 0.5, ex, ex - 1) + 127
    byte = np.clip(np.where(amax > 0, byte, 1), 1, 254)
    scaled = (w * np.exp2(127.0 - byte)[:, None, :]).reshape(k, n).astype(np.float32)
    by_word = np.ascontiguousarray(scaled.reshape(k // 512, 128, 4, n).transpose(0, 1, 3, 2))
    if fmt == "e4m3":
        words = by_word.astype(ml_dtypes.float8_e4m3fn).view(np.uint8)
    else:
        c = by_word.astype(ml_dtypes.float4_e2m1fn).view(np.uint8) & 0xF
        words = c[..., 0::2] | (c[..., 1::2] << 4)
    return np.ascontiguousarray(words), np.ascontiguousarray(byte.astype(np.uint8).reshape(k // 512, 16, n))


def unpack_weight(words, scales, fmt):
    g, p, n, _ = words.shape
    if fmt == "e4m3":
        vals = np.ascontiguousarray(words).view(ml_dtypes.float8_e4m3fn).astype(np.float64)
    else:
        nib = np.empty((g, p, n, 4), np.uint8)
        nib[..., 0::2] = words & 0xF
        nib[..., 1::2] = words >> 4
        vals = E2M1[nib]
    vals = vals * np.repeat(np.exp2(scales.astype(np.float64) - 127.0), 8, axis=1)[..., None]
    return vals.transpose(0, 1, 3, 2).reshape(g * 512, n)
def pack4(w):
    words, scales = pack_weight(w, "e2m1")
    return words.reshape(words.shape[0], 128, -1), scales


def unpack4(words, scales):
    return unpack_weight(words.reshape(words.shape[0], 128, -1, 2), scales, "e2m1")


B, N, D, H, S = 2, 512, 512, 1024, 128
QS = 2.3 / N ** 0.25


def silu(z):
    return z / (1.0 + np.exp(-z))


def draw0():
    t = np.exp2(np.round(np.log2(mx_kscale(N)) / 2))
    r = mx_kscale(H)
    q = bf(np.random.standard_normal((B, N, S)) * QS)
    k = bf(np.random.standard_normal((B, N, S)) * QS * t[:, None])
    u = bf(silu(0.7 * np.random.standard_normal((B, N, H))) * r)
    v = bf(silu(0.7 * np.random.standard_normal((B, N, H))) / (t * t)[:, None])
    W_o_words, W_o_scales = pack4(np.random.standard_normal((H, D)) / np.sqrt(H) / r[:, None])
    return {"q": q,
            "k": k,
            "u": u,
            "v": v,
            "W_o_words": W_o_words,
            "W_o_scales": W_o_scales,
            "b_o": bf(0.1 * np.random.standard_normal(D))}


def core(q, k, u, v, W_o_words, W_o_scales, b_o):
    qk = f64(q) @ f64(k).transpose(0, 2, 1) * (1.0 / np.sqrt(S))
    attn = np.square(np.maximum(qk, 0.0))
    av = mxq(attn, 2, "e4m3") @ mxq(f64(v), 1, "e4m3")
    gated = f64(u) * av
    return (mxq(gated, 2, "e4m3") @ unpack4(W_o_words, W_o_scales)) + f64(b_o)


def e4m3fn_bytes(y):
    return np.clip(np.asarray(y, np.float64), -448.0, 448.0).astype(np.float32).astype(ml_dtypes.float8_e4m3fn).view(np.uint8)


def e4m3fn_values(b):
    return np.asarray(b, np.uint8).view(ml_dtypes.float8_e4m3fn).astype(np.float64)


def setup_inputs():
    d = draw0()
    x0 = np.asarray(d['v']).astype(np.float64)
    s = (np.max(np.abs(x0), axis=(0, 2), keepdims=True) / 448.0).astype(np.float32)
    out = {}
    for k, v in d.items():
        if k == 'v':
            out['v_bytes'] = e4m3fn_bytes(x0 / s.astype(np.float64))
            out['v_scale'] = s
        else:
            out[k] = v
    return out


def reference(q, k, u, v_bytes, v_scale, W_o_words, W_o_scales, b_o):
    return core(q, k, u, e4m3fn_values(v_bytes) * v_scale.astype(np.float64), W_o_words, W_o_scales, b_o)

@@ -1,0 +1,255 @@
+import math
+from contextlib import ExitStack
+
+import concourse.mybir as mybir
+from concourse.masks import make_identity
+
+B, N, D, H, S = 2, 512, 512, 1024, 128
+FLOPS = B * (2 * N * N * S + 2 * N * N * H + 2 * N * H * D)
+
+F32 = mybir.dt.float32
+BF16 = mybir.dt.bfloat16
+U32 = mybir.dt.uint32
+I32 = mybir.dt.int32
+U8 = mybir.dt.uint8
+FP8 = mybir.dt.float8_e4m3fn
+FP8X4 = mybir.dt.float8_e4m3fn_x4
+FP4X4 = mybir.dt.float4_e2m1fn_x4
+ACT = mybir.ActivationFunctionType
+ALU = mybir.AluOpType
+
+P = 128
+T = 4
+NT = N // P
+G = H // 512
+QK_SCALE = 1.0 / math.sqrt(S)
+
+ORDER = """
+SW00 VW01 PTq0 PTk0 VW02 SW03 VCQ0 PTU00 SCK0 VIL000 SIL010 VIL001 PQK00 VQV00 PTU01 SRL00 VW11 SSQ00 PQK01
+VCU00 VQA00 SCU01 PQK02 VIL011 PAV000 SRL01 PTq1 VW13 SRL02 PQK03 VQV01 PTU02 SCQ1 SRL03 PAV001 VCU02 SSQ01
+PTU03 VW12 PTk1 SCU03 VQA01 VGT000 SCK1 SSQ02 VGT001 PAV010 SSQ03 VGT010 PAV011 SW10 VQA02 VQG00 PAV020 VQA03
+VGT011 SIL101 VGT020 PAV021 PPJ00 VIL111 PQK10 SIL100 VBI00 PQK11 PAV030 VQG01 PTU10 VGT021 PPJ01 SCU10 VGT030
+PTU11 SIL110 VQV10 PAV031 PTU12 VQG02 VGT031 PPJ02 SRL10 VQV11 SSQ10 PQK12 VBI02 SRL11 VQG03 VQA10 SSQ11 VBI01
+PAV100 SRL12 PAV101 VGT100 PPJ03 SSQ12 VGT101 PQK13 SRL13 VQG10 VBI03 PPJ10 SSQ13 VQA11 VQA12 SCU11 VQA13
+PAV110 VBI10 PAV111 SCU12 PTU13 VGT110 VGT111 SCU13 PAV120 VQG11 PAV121 VGT120 PPJ11 VGT121 PAV130 VQG12
+PAV131 VGT130 PPJ12 VGT131 VQY13 VBI12 VQX13 VBI11 PPX13 VBX13 PPY13 VBY13
+"""
+
+
+def tile_gatedattentionunit_pb_w4_kernel(tc, q, k, u, v_bytes, v_scale, W_o_words, W_o_scales, b_o, out):
+    nc = tc.nc
+    with ExitStack() as ctx:
+        keep = ctx.enter_context(tc.tile_pool(name="keep", bufs=1))
+        ps_tr = ctx.enter_context(tc.psum_pool(name="ps_tr", bufs=2))
+        ps_qk = ctx.enter_context(tc.psum_pool(name="ps_qk", bufs=2))
+        ps_av = ctx.enter_context(tc.psum_pool(name="ps_av", bufs=2))
+        ps_o = ctx.enter_context(tc.psum_pool(name="ps_o", bufs=2))
+
+        def kt(shape, dt, name):
+            return keep.tile(shape, dt, name=name, align_bytes=64)
+
+        k_sb = [kt([P, T, S], BF16, "k_sb%d" % b) for b in range(B)]
+        q_sb = [kt([P, NT, S], BF16, "q_sb%d" % b) for b in range(B)]
+        kT = [kt([P, T, P], BF16, "kT%d" % b) for b in range(B)]
+        qT = [kt([P, NT, P], BF16, "qT%d" % b) for b in range(B)]
+        vb = [kt([P, T, H], U8, "vb%d" % b) for b in range(B)]
+        v_bf = [kt([P, T, H], BF16, "v_bf%d" % b) for b in range(B)]
+        v_il = [[kt([P, T, P, T], BF16, "v_il%d_%d" % (b, g)) for g in range(G)] for b in range(B)]
+        v_c = [[kt([P, 512], U32, "v_c%d_%d" % (b, g)) for g in range(G)] for b in range(B)]
+        v_s = [[kt([P, 512], U8, "v_s%d_%d" % (b, g)) for g in range(G)] for b in range(B)]
+        u_sb = [[kt([P, 2, H], BF16, "u_sb%d_%d" % (b, c)) for c in range(2)] for b in range(B)]
+        uT = [[kt([P, G, P, T], BF16, "uT%d_%d" % (b, i)) for i in range(NT)] for b in range(B)]
+        at_il = [[kt([P, P, T], BF16, "at_il%d_%d" % (b, i)) for i in range(NT)] for b in range(B)]
+        at_c = [[kt([P, P], U32, "at_c%d_%d" % (b, i)) for i in range(NT)] for b in range(B)]
+        at_s = [[kt([P, P], U8, "at_s%d_%d" % (b, i)) for i in range(NT)] for b in range(B)]
+        r_sb = [[kt([P, P, T], F32, "r_sb%d_%d" % (b, i)) for i in range(NT)] for b in range(B)]
+        gt = [[kt([P, G, P, T], BF16, "gt%d_%d" % (b, i)) for i in range(NT)] for b in range(B)]
+        gc = [[kt([P, G, P], U32, "gc%d_%d" % (b, i)) for i in range(NT)] for b in range(B)]
+        gs = [[kt([P, G, P], U8, "gs%d_%d" % (b, i)) for i in range(NT)] for b in range(B)]
+        o_sb = [[kt([P, D], F32, "o_sb%d_%d" % (b, i)) for i in range(NT)] for b in range(B)]
+        vs = kt([P, T], F32, "vs")
+        w_sb = kt([P, G, 2 * D], U8, "w_sb")
+        ws_sb = kt([P, G, D], U8, "ws_sb")
+        b_bc = kt([P, D], BF16, "b_bc")
+        id_bf = kt([P, P], BF16, "id_bf")
+        id_f = kt([P, P], F32, "id_f")
+        dummy = kt([P, 1], F32, "dummy")
+
+        banks = {}
+
+        def load_kq(b):
+            nc.sync.dma_start(out=k_sb[b][:], in_=k[b].rearrange("(p t) s -> p t s", t=T))
+            nc.sync.dma_start(out=q_sb[b][:], in_=q[b].rearrange("(p i) s -> p i s", i=NT))
+
+        def load_v(b, t0, t1):
+            rows = v_bytes[b].rearrange("(p t) h -> p t h", t=T)
+            nc.sync.dma_start(out=vb[b][:, t0:t1, :], in_=rows[:, t0:t1, :])
+
+        def load_u(b, c):
+            rows = u[b].rearrange("(p i) h -> p i h", i=NT)
+            nc.sync.dma_start(out=u_sb[b][c][:], in_=rows[:, 2 * c : 2 * c + 2, :])
+
+        def load_w():
+            nc.sync.dma_start(out=w_sb[:], in_=W_o_words.rearrange("g p n -> p g n"))
+            rows = W_o_scales.bitcast(I32).rearrange("g (q r) n -> r q g n", r=4)
+            ws_i = ws_sb[:].bitcast(I32)
+            for r in range(4):
+                nc.sync.dma_start(out=ws_i[r:P:32, :, :], in_=rows[r])
+            nc.sync.dma_start(out=b_bc[:], in_=b_o.partition_broadcast(P))
+
+        def copy(eng, out, in_):
+            if eng == "V":
+                nc.vector.tensor_copy(out=out, in_=in_)
+            else:
+                nc.scalar.copy(out=out, in_=in_)
+
+        def Tk(e, b):
+            bank = banks["Tk", b] = ps_tr.tile([P, T, P], BF16, name="tr_bank")
+            for t in range(T):
+                nc.tensor.transpose(bank[:, t, :], k_sb[b][:, t, :], id_bf[:])
+
+        def Tq(e, b):
+            bank = banks["Tq", b] = ps_tr.tile([P, T, P], BF16, name="tr_bank")
+            for t in range(T):
+                nc.tensor.transpose(bank[:, t, :], q_sb[b][:, t, :], id_bf[:])
+
+        def CK(e, b):
+            copy(e, kT[b][:], banks["Tk", b][:])
+
+        def CQ(e, b):
+            copy(e, qT[b][:], banks["Tq", b][:])
+
+        def QK(e, b, i):
+            bank = banks["QK", b, i] = ps_qk.tile([P, T, P], F32, name="qk_bank")
+            for t in range(T):
+                nc.tensor.matmul(bank[:, t, :], lhsT=kT[b][:, t, :], rhs=qT[b][:, i, :], start=True, stop=True)
+
+        def RL(e, b, i):
+            nc.scalar.activation(r_sb[b][i][:], banks["QK", b, i][:].rearrange("p t n -> p n t"), ACT.Relu)
+
+        def SQ(e, b, i):
+            nc.scalar.activation(at_il[b][i][:], r_sb[b][i][:], ACT.Square, scale=QK_SCALE)
+
+        def QA(e, b, i):
+            nc.vector.quantize_mx(out=at_c[b][i][:].bitcast(FP8X4), scales=at_s[b][i][:], in_=at_il[b][i][:].rearrange("p n t -> p (n t)"))
+
+        def W(e, b, t):
+            src = vb[b][:, t, :].bitcast(FP8)
+            if e == "V":
+                nc.vector.tensor_scalar(out=v_bf[b][:, t, :], in0=src, scalar1=vs[:, t : t + 1], scalar2=None, op0=ALU.mult)
+            else:
+                nc.scalar.activation(v_bf[b][:, t, :], src, ACT.Copy, scale=vs[:, t : t + 1])
+
+        def IL(e, b, g, h):
+            dst = v_il[b][g][:, 2 * h : 2 * h + 2]
+            src = v_bf[b][:, :, 512 * g : 512 * (g + 1)].rearrange("p t (m c) -> p c m t", c=T)[:, 2 * h : 2 * h + 2]
+            copy(e, dst, src)
+
+        def QV(e, b, g):
+            nc.vector.quantize_mx(out=v_c[b][g][:].bitcast(FP8X4), scales=v_s[b][g][:], in_=v_il[b][g][:].rearrange("p c m t -> p (c m t)"))
+
+        def TU(e, b, i):
+            bank = banks["TU", b, i] = ps_tr.tile([P, G, 2, P], F32, name="tr_bank")
+            words = u_sb[b][i // 2][:, i % 2, :].bitcast(F32)
+            for g in range(G):
+                for w in range(2):
+                    nc.tensor.transpose(bank[:, g, w, :], words[:, 256 * g + w : 256 * (g + 1) : 2], id_f[:])
+
+        def CU(e, b, i):
+            copy(e, uT[b][i][:].bitcast(F32), banks["TU", b, i][:].rearrange("p g w n -> p g n w"))
+
+        def AV(e, b, i, g):
+            bank = banks["AV", b, i, g] = ps_av.tile([P, T, P], F32, name="av_bank")
+            for t in range(T):
+                cols = slice(P * t, P * (t + 1))
+                nc.tensor.matmul_mx(
+                    out=bank[:, t, :],
+                    lhsT=v_c[b][g][:, cols].bitcast(FP8X4),
+                    lhsT_scale=v_s[b][g][:, cols],
+                    rhs=at_c[b][i][:].bitcast(FP8X4),
+                    rhs_scale=at_s[b][i][:],
+                    start=True,
+                    stop=True,
+                )
+
+        def GT(e, b, i, g):
+            src = banks["AV", b, i, g][:].rearrange("p t n -> p n t")
+            nc.vector.tensor_tensor(out=gt[b][i][:, g], in0=src, in1=uT[b][i][:, g], op=ALU.mult)
+
+        def quant_gated(b, i, g0, g1):
+            nc.vector.quantize_mx(
+                out=gc[b][i][:, g0:g1].rearrange("p g n -> p (g n)").bitcast(FP8X4),
+                scales=gs[b][i][:, g0:g1].rearrange("p g n -> p (g n)"),
+                in_=gt[b][i][:, g0:g1].rearrange("p g n t -> p (g n t)"),
+            )
+
+        def QG(e, b, i):
+            quant_gated(b, i, 0, G)
+
+        def QX(e, b, i):
+            quant_gated(b, i, 0, 1)
+
+        def QY(e, b, i):
+            quant_gated(b, i, 1, 2)
+
+        def project(b, i, d0, d1, n):
+            bank = banks["PJ", b, i, d0] = ps_o.tile([P, D], F32, name="o_bank")
+            for c in range(d0, d1, n):
+                for g in range(G):
+                    nc.tensor.matmul_mx(
+                        out=bank[:, c - d0 : c - d0 + n],
+                        lhsT=gc[b][i][:, g, :].bitcast(FP8X4),
+                        lhsT_scale=gs[b][i][:, g, :],
+                        rhs=w_sb[:, g, 2 * c : 2 * (c + n)].bitcast(FP4X4),
+                        rhs_scale=ws_sb[:, g, c : c + n],
+                        start=(g == 0),
+                        stop=(g == G - 1),
+                    )
+
+        def finish(b, i, d0, d1):
+            o = o_sb[b][i][:, d0:d1]
+            nc.vector.tensor_tensor(out=o, in0=banks["PJ", b, i, d0][:, : d1 - d0], in1=b_bc[:, d0:d1], op=ALU.add)
+            nc.sync.dma_start(out=out[b].rearrange("(p i) d -> p i d", i=NT)[:, i, d0:d1], in_=o)
+
+        def PJ(e, b, i):
+            project(b, i, 0, D, D)
+
+        def PX(e, b, i):
+            project(b, i, 0, D // 2, 128)
+
+        def PY(e, b, i):
+            project(b, i, D // 2, D, 128)
+
+        def BI(e, b, i):
+            finish(b, i, 0, D)
+
+        def BX(e, b, i):
+            finish(b, i, 0, D // 2)
+
+        def BY(e, b, i):
+            finish(b, i, D // 2, D)
+
+        make_identity(nc, id_bf[:])
+        make_identity(nc, id_f[:])
+        with tc.manual_schedule():
+            nc.vector.memset(ws_sb[:].bitcast(I32), 0)
+            nc.vector.memset(dummy[:], 0.0)
+            nc.scalar.activation(dummy[:], dummy[:], ACT.Relu)
+
+            nc.sync.dma_start(out=vs[:], in_=v_scale.rearrange("o (p t) x -> p (o t x)", t=T))
+            load_v(0, 0, 1)
+            load_v(0, 1, 2)
+            load_kq(0)
+            load_v(0, 2, 4)
+            load_u(0, 0)
+            load_u(0, 1)
+            load_kq(1)
+            load_v(1, 0, 2)
+            load_v(1, 2, 4)
+            load_w()
+            load_u(1, 0)
+            load_u(1, 1)
+            table = dict(Tk=Tk, Tq=Tq, CK=CK, CQ=CQ, QK=QK, RL=RL, SQ=SQ, QA=QA, W=W, IL=IL, QV=QV, TU=TU, CU=CU, AV=AV, GT=GT, QG=QG, QX=QX, QY=QY, PJ=PJ, PX=PX, PY=PY, BI=BI, BX=BX, BY=BY)
+            for step in ORDER.split():
+                name = step[1 : 2 if step[1] == "W" else 3]
+                table[name](step[0], *[int(c) for c in step[1 + len(name) :]])

@@ -21,19 +21,10 @@ ALU = mybir.AluOpType
 P = 128
 T = 4
 NT = N // P
-G = H // 512
+TILES = B * NT
+KP = P * T
+G = H // KP
 QK_SCALE = 1.0 / math.sqrt(S)
-
-ORDER = """
-SW00 VW01 PTq0 PTk0 VW02 SW03 VCQ0 PTU00 SCK0 VIL000 SIL010 VIL001 PQK00 VQV00 PTU01 SRL00 VW11 SSQ00 PQK01
-VCU00 VQA00 SCU01 PQK02 VIL011 PAV000 SRL01 PTq1 VW13 SRL02 PQK03 VQV01 PTU02 SCQ1 SRL03 PAV001 VCU02 SSQ01
-PTU03 VW12 PTk1 SCU03 VQA01 VGT000 SCK1 SSQ02 VGT001 PAV010 SSQ03 VGT010 PAV011 SW10 VQA02 VQG00 PAV020 VQA03
-VGT011 SIL101 VGT020 PAV021 PPJ00 VIL111 PQK10 SIL100 VBI00 PQK11 PAV030 VQG01 PTU10 VGT021 PPJ01 SCU10 VGT030
-PTU11 SIL110 VQV10 PAV031 PTU12 VQG02 VGT031 PPJ02 SRL10 VQV11 SSQ10 PQK12 VBI02 SRL11 VQG03 VQA10 SSQ11 VBI01
-PAV100 SRL12 PAV101 VGT100 PPJ03 SSQ12 VGT101 PQK13 SRL13 VQG10 VBI03 PPJ10 SSQ13 VQA11 VQA12 SCU11 VQA13
-PAV110 VBI10 PAV111 SCU12 PTU13 VGT110 VGT111 SCU13 PAV120 VQG11 PAV121 VGT120 PPJ11 VGT121 PAV130 VQG12
-PAV131 VGT130 PPJ12 VGT131 VQY13 VBI12 VQX13 VBI11 PPX13 VBX13 PPY13 VBY13
-"""
 
 
 def tile_gatedattentionunit_pb_w4_kernel(tc, q, k, u, v_bytes, v_scale, W_o_words, W_o_scales, b_o, out):
@@ -42,8 +33,8 @@ def tile_gatedattentionunit_pb_w4_kernel(tc, q, k, u, v_bytes, v_scale, W_o_word
         keep = ctx.enter_context(tc.tile_pool(name="keep", bufs=1))
         ps_tr = ctx.enter_context(tc.psum_pool(name="ps_tr", bufs=2))
         ps_qk = ctx.enter_context(tc.psum_pool(name="ps_qk", bufs=2))
-        ps_av = ctx.enter_context(tc.psum_pool(name="ps_av", bufs=2))
-        ps_o = ctx.enter_context(tc.psum_pool(name="ps_o", bufs=2))
+        ps_av = ctx.enter_context(tc.psum_pool(name="ps_av", bufs=3))
+        ps_o = ctx.enter_context(tc.psum_pool(name="ps_o", bufs=1))
 
         def kt(shape, dt, name):
             return keep.tile(shape, dt, name=name, align_bytes=64)
@@ -52,28 +43,27 @@ def tile_gatedattentionunit_pb_w4_kernel(tc, q, k, u, v_bytes, v_scale, W_o_word
         q_sb = [kt([P, NT, S], BF16, "q_sb%d" % b) for b in range(B)]
         kT = [kt([P, T, P], BF16, "kT%d" % b) for b in range(B)]
         qT = [kt([P, NT, P], BF16, "qT%d" % b) for b in range(B)]
-        vb = [kt([P, T, H], U8, "vb%d" % b) for b in range(B)]
-        v_bf = [kt([P, T, H], BF16, "v_bf%d" % b) for b in range(B)]
-        v_il = [[kt([P, T, P, T], BF16, "v_il%d_%d" % (b, g)) for g in range(G)] for b in range(B)]
-        v_c = [[kt([P, 512], U32, "v_c%d_%d" % (b, g)) for g in range(G)] for b in range(B)]
-        v_s = [[kt([P, 512], U8, "v_s%d_%d" % (b, g)) for g in range(G)] for b in range(B)]
-        u_sb = [[kt([P, 2, H], BF16, "u_sb%d_%d" % (b, c)) for c in range(2)] for b in range(B)]
-        uT = [[kt([P, G, P, T], BF16, "uT%d_%d" % (b, i)) for i in range(NT)] for b in range(B)]
-        at_il = [[kt([P, P, T], BF16, "at_il%d_%d" % (b, i)) for i in range(NT)] for b in range(B)]
-        at_c = [[kt([P, P], U32, "at_c%d_%d" % (b, i)) for i in range(NT)] for b in range(B)]
-        at_s = [[kt([P, P], U8, "at_s%d_%d" % (b, i)) for i in range(NT)] for b in range(B)]
-        r_sb = [[kt([P, P, T], F32, "r_sb%d_%d" % (b, i)) for i in range(NT)] for b in range(B)]
-        gt = [[kt([P, G, P, T], BF16, "gt%d_%d" % (b, i)) for i in range(NT)] for b in range(B)]
-        gc = [[kt([P, G, P], U32, "gc%d_%d" % (b, i)) for i in range(NT)] for b in range(B)]
-        gs = [[kt([P, G, P], U8, "gs%d_%d" % (b, i)) for i in range(NT)] for b in range(B)]
-        o_sb = [[kt([P, D], F32, "o_sb%d_%d" % (b, i)) for i in range(NT)] for b in range(B)]
+        vb = [[kt([P, 2, H], U8, "vb%d_%d" % (b, c)) for c in range(2)] for b in range(B)]
+        v_bf = [[kt([P, T, KP], BF16, "v_bf%d_%d" % (b, g)) for g in range(G)] for b in range(B)]
+        v_il = [[kt([P, KP, T], BF16, "v_il%d_%d" % (b, g)) for g in range(G)] for b in range(B)]
+        v_c = [[kt([P, KP], U32, "v_c%d_%d" % (b, g)) for g in range(G)] for b in range(B)]
+        v_s = [[kt([P, KP], U8, "v_s%d_%d" % (b, g)) for g in range(G)] for b in range(B)]
+        u_sb = [kt([P, 2, H], BF16, "u_sb%d" % c) for c in range(TILES // 2)]
+        r_sb = [kt([P, P, T], F32, "r_sb%d" % j) for j in range(TILES)]
+        at_il = [kt([P, P, T], BF16, "at_il%d" % j) for j in range(TILES)]
+        at_c = [kt([P, P], U32, "at_c%d" % j) for j in range(TILES)]
+        at_s = [kt([P, P], U8, "at_s%d" % j) for j in range(TILES)]
+        gt = [[kt([P, KP], BF16, "gt%d_%d" % (j, g)) for g in range(G)] for j in range(TILES)]
+        gT = [kt([P, G, P, T], BF16, "gT%d" % j) for j in range(TILES)]
+        gc = [kt([P, G, P], U32, "gc%d" % j) for j in range(TILES)]
+        gs = [kt([P, G, P], U8, "gs%d" % j) for j in range(TILES)]
+        o_sb = [kt([P, D], F32, "o_sb%d" % j) for j in range(TILES)]
         vs = kt([P, T], F32, "vs")
         w_sb = kt([P, G, 2 * D], U8, "w_sb")
         ws_sb = kt([P, G, D], U8, "ws_sb")
         b_bc = kt([P, D], BF16, "b_bc")
         id_bf = kt([P, P], BF16, "id_bf")
         id_f = kt([P, P], F32, "id_f")
-        dummy = kt([P, 1], F32, "dummy")
 
         banks = {}
 
@@ -81,13 +71,13 @@ def tile_gatedattentionunit_pb_w4_kernel(tc, q, k, u, v_bytes, v_scale, W_o_word
             nc.sync.dma_start(out=k_sb[b][:], in_=k[b].rearrange("(p t) s -> p t s", t=T))
             nc.sync.dma_start(out=q_sb[b][:], in_=q[b].rearrange("(p i) s -> p i s", i=NT))
 
-        def load_v(b, t0, t1):
+        def load_v(b, c):
             rows = v_bytes[b].rearrange("(p t) h -> p t h", t=T)
-            nc.sync.dma_start(out=vb[b][:, t0:t1, :], in_=rows[:, t0:t1, :])
+            nc.sync.dma_start(out=vb[b][c][:], in_=rows[:, 2 * c : 2 * c + 2, :])
 
         def load_u(b, c):
             rows = u[b].rearrange("(p i) h -> p i h", i=NT)
-            nc.sync.dma_start(out=u_sb[b][c][:], in_=rows[:, 2 * c : 2 * c + 2, :])
+            nc.sync.dma_start(out=u_sb[2 * b + c][:], in_=rows[:, 2 * c : 2 * c + 2, :])
 
         def load_w():
             nc.sync.dma_start(out=w_sb[:], in_=W_o_words.rearrange("g p n -> p g n"))
@@ -95,161 +85,201 @@ def tile_gatedattentionunit_pb_w4_kernel(tc, q, k, u, v_bytes, v_scale, W_o_word
             ws_i = ws_sb[:].bitcast(I32)
             for r in range(4):
                 nc.sync.dma_start(out=ws_i[r:P:32, :, :], in_=rows[r])
-            nc.sync.dma_start(out=b_bc[:], in_=b_o.partition_broadcast(P))
 
-        def copy(eng, out, in_):
-            if eng == "V":
-                nc.vector.tensor_copy(out=out, in_=in_)
-            else:
-                nc.scalar.copy(out=out, in_=in_)
-
-        def Tk(e, b):
-            bank = banks["Tk", b] = ps_tr.tile([P, T, P], BF16, name="tr_bank")
+        def turn(name, b):
+            src = {"k": k_sb, "q": q_sb}[name][b]
+            bank = banks[name, b] = ps_tr.tile([P, T, P], BF16, name="tr_bank")
             for t in range(T):
-                nc.tensor.transpose(bank[:, t, :], k_sb[b][:, t, :], id_bf[:])
+                nc.tensor.transpose(bank[:, t, :], src[:, t, :], id_bf[:])
 
-        def Tq(e, b):
-            bank = banks["Tq", b] = ps_tr.tile([P, T, P], BF16, name="tr_bank")
-            for t in range(T):
-                nc.tensor.transpose(bank[:, t, :], q_sb[b][:, t, :], id_bf[:])
+        def copy_turned(name, b):
+            nc.scalar.copy(out={"k": kT, "q": qT}[name][b][:], in_=banks[name, b][:])
 
-        def CK(e, b):
-            copy(e, kT[b][:], banks["Tk", b][:])
+        def widen_v(b, g, t):
+            src = vb[b][t // 2][:, t % 2, KP * g : KP * (g + 1)].bitcast(FP8)
+            nc.vector.tensor_scalar(out=v_bf[b][g][:, t, :], in0=src, scalar1=vs[:, t : t + 1], scalar2=None, op0=ALU.mult)
 
-        def CQ(e, b):
-            copy(e, qT[b][:], banks["Tq", b][:])
+        def widen_s(b, g, t):
+            src = vb[b][t // 2][:, t % 2, KP * g : KP * (g + 1)].bitcast(FP8)
+            nc.scalar.activation(v_bf[b][g][:, t, :], src, ACT.Copy, scale=vs[:, t : t + 1])
 
-        def QK(e, b, i):
-            bank = banks["QK", b, i] = ps_qk.tile([P, T, P], F32, name="qk_bank")
+        def interleave(b, g):
+            dst = v_il[b][g][:].rearrange("p (c i) t -> p c t i", i=4)
+            src = v_bf[b][g][:].rearrange("p t (c i) -> p c t i", i=4)
+            nc.vector.tensor_copy(out=dst, in_=src)
+
+        def quant_v(b, g):
+            nc.vector.quantize_mx(out=v_c[b][g][:].bitcast(FP8X4), scales=v_s[b][g][:], in_=v_il[b][g][:].rearrange("p c t -> p (c t)"))
+
+        def scores(j):
+            b, i = divmod(j, NT)
+            bank = banks["qk", j] = ps_qk.tile([P, T, P], F32, name="qk_bank")
             for t in range(T):
                 nc.tensor.matmul(bank[:, t, :], lhsT=kT[b][:, t, :], rhs=qT[b][:, i, :], start=True, stop=True)
 
-        def RL(e, b, i):
-            nc.scalar.activation(r_sb[b][i][:], banks["QK", b, i][:].rearrange("p t n -> p n t"), ACT.Relu)
+        def relu(j):
+            nc.scalar.activation(r_sb[j][:], banks["qk", j][:].rearrange("p t n -> p n t"), ACT.Relu)
 
-        def SQ(e, b, i):
-            nc.scalar.activation(at_il[b][i][:], r_sb[b][i][:], ACT.Square, scale=QK_SCALE)
+        def square(j):
+            nc.scalar.activation(at_il[j][:], r_sb[j][:], ACT.Square, scale=QK_SCALE)
 
-        def QA(e, b, i):
-            nc.vector.quantize_mx(out=at_c[b][i][:].bitcast(FP8X4), scales=at_s[b][i][:], in_=at_il[b][i][:].rearrange("p n t -> p (n t)"))
+        def quant_attn(j):
+            nc.vector.quantize_mx(out=at_c[j][:].bitcast(FP8X4), scales=at_s[j][:], in_=at_il[j][:].rearrange("p n t -> p (n t)"))
 
-        def W(e, b, t):
-            src = vb[b][:, t, :].bitcast(FP8)
-            if e == "V":
-                nc.vector.tensor_scalar(out=v_bf[b][:, t, :], in0=src, scalar1=vs[:, t : t + 1], scalar2=None, op0=ALU.mult)
-            else:
-                nc.scalar.activation(v_bf[b][:, t, :], src, ACT.Copy, scale=vs[:, t : t + 1])
-
-        def IL(e, b, g, h):
-            dst = v_il[b][g][:, 2 * h : 2 * h + 2]
-            src = v_bf[b][:, :, 512 * g : 512 * (g + 1)].rearrange("p t (m c) -> p c m t", c=T)[:, 2 * h : 2 * h + 2]
-            copy(e, dst, src)
-
-        def QV(e, b, g):
-            nc.vector.quantize_mx(out=v_c[b][g][:].bitcast(FP8X4), scales=v_s[b][g][:], in_=v_il[b][g][:].rearrange("p c m t -> p (c m t)"))
-
-        def TU(e, b, i):
-            bank = banks["TU", b, i] = ps_tr.tile([P, G, 2, P], F32, name="tr_bank")
-            words = u_sb[b][i // 2][:, i % 2, :].bitcast(F32)
-            for g in range(G):
-                for w in range(2):
-                    nc.tensor.transpose(bank[:, g, w, :], words[:, 256 * g + w : 256 * (g + 1) : 2], id_f[:])
-
-        def CU(e, b, i):
-            copy(e, uT[b][i][:].bitcast(F32), banks["TU", b, i][:].rearrange("p g w n -> p g n w"))
-
-        def AV(e, b, i, g):
-            bank = banks["AV", b, i, g] = ps_av.tile([P, T, P], F32, name="av_bank")
-            for t in range(T):
-                cols = slice(P * t, P * (t + 1))
-                nc.tensor.matmul_mx(
-                    out=bank[:, t, :],
-                    lhsT=v_c[b][g][:, cols].bitcast(FP8X4),
-                    lhsT_scale=v_s[b][g][:, cols],
-                    rhs=at_c[b][i][:].bitcast(FP8X4),
-                    rhs_scale=at_s[b][i][:],
-                    start=True,
-                    stop=True,
-                )
-
-        def GT(e, b, i, g):
-            src = banks["AV", b, i, g][:].rearrange("p t n -> p n t")
-            nc.vector.tensor_tensor(out=gt[b][i][:, g], in0=src, in1=uT[b][i][:, g], op=ALU.mult)
-
-        def quant_gated(b, i, g0, g1):
-            nc.vector.quantize_mx(
-                out=gc[b][i][:, g0:g1].rearrange("p g n -> p (g n)").bitcast(FP8X4),
-                scales=gs[b][i][:, g0:g1].rearrange("p g n -> p (g n)"),
-                in_=gt[b][i][:, g0:g1].rearrange("p g n t -> p (g n t)"),
+        def mix(j, g):
+            b = j // NT
+            bank = banks["av", j, g] = ps_av.tile([P, KP], F32, name="av_bank")
+            nc.tensor.matmul_mx(
+                out=bank[:],
+                lhsT=at_c[j][:].bitcast(FP8X4),
+                lhsT_scale=at_s[j][:],
+                rhs=v_c[b][g][:].bitcast(FP8X4),
+                rhs_scale=v_s[b][g][:],
+                start=True,
+                stop=True,
             )
 
-        def QG(e, b, i):
-            quant_gated(b, i, 0, G)
+        def gate(j, g):
+            av = banks["av", j, g][:].rearrange("n (p w e) -> n w p e", w=2, e=2)
+            gate_in = u_sb[j // 2][:, j % 2, KP * g : KP * (g + 1)].rearrange("n (p w e) -> n w p e", w=2, e=2)
+            nc.vector.tensor_tensor(out=gt[j][g][:].rearrange("n (w p e) -> n w p e", w=2, e=2), in0=av, in1=gate_in, op=ALU.mult)
 
-        def QX(e, b, i):
-            quant_gated(b, i, 0, 1)
+        def turn_gated(j, g0, g1):
+            bank = banks["tg", j, g0] = ps_tr.tile([P, g1 - g0, 2, P], F32, name="tr_bank")
+            for g in range(g0, g1):
+                words = gt[j][g][:].bitcast(F32)
+                for w in range(2):
+                    nc.tensor.transpose(bank[:, g - g0, w, :], words[:, P * w : P * (w + 1)], id_f[:])
 
-        def QY(e, b, i):
-            quant_gated(b, i, 1, 2)
+        def copy_gated(j, g0, g1):
+            nc.scalar.copy(out=gT[j][:, g0:g1].bitcast(F32), in_=banks["tg", j, g0][:].rearrange("p g w n -> p g n w"))
 
-        def project(b, i, d0, d1, n):
-            bank = banks["PJ", b, i, d0] = ps_o.tile([P, D], F32, name="o_bank")
-            for c in range(d0, d1, n):
-                for g in range(G):
-                    nc.tensor.matmul_mx(
-                        out=bank[:, c - d0 : c - d0 + n],
-                        lhsT=gc[b][i][:, g, :].bitcast(FP8X4),
-                        lhsT_scale=gs[b][i][:, g, :],
-                        rhs=w_sb[:, g, 2 * c : 2 * (c + n)].bitcast(FP4X4),
-                        rhs_scale=ws_sb[:, g, c : c + n],
-                        start=(g == 0),
-                        stop=(g == G - 1),
-                    )
+        def quant_gated(j, g0, g1):
+            nc.vector.quantize_mx(
+                out=gc[j][:, g0:g1].rearrange("p g n -> p (g n)").bitcast(FP8X4),
+                scales=gs[j][:, g0:g1].rearrange("p g n -> p (g n)"),
+                in_=gT[j][:, g0:g1].rearrange("p g n t -> p (g n t)"),
+            )
 
-        def finish(b, i, d0, d1):
-            o = o_sb[b][i][:, d0:d1]
-            nc.vector.tensor_tensor(out=o, in0=banks["PJ", b, i, d0][:, : d1 - d0], in1=b_bc[:, d0:d1], op=ALU.add)
-            nc.sync.dma_start(out=out[b].rearrange("(p i) d -> p i d", i=NT)[:, i, d0:d1], in_=o)
+        def project(j, g0, g1):
+            if g0 == 0:
+                if j < TILES - 2:
+                    banks["o", j] = ps_o.tile([P, D], F32, name="o_bank")
+                else:
+                    banks["o", j] = ps_qk.tile([P, D], F32, name="qk_bank")
+            for g in range(g0, g1):
+                nc.tensor.matmul_mx(
+                    out=banks["o", j][:],
+                    lhsT=gc[j][:, g, :].bitcast(FP8X4),
+                    lhsT_scale=gs[j][:, g, :],
+                    rhs=w_sb[:, g, :].bitcast(FP4X4),
+                    rhs_scale=ws_sb[:, g, :],
+                    start=(g == 0),
+                    stop=(g == G - 1),
+                )
 
-        def PJ(e, b, i):
-            project(b, i, 0, D, D)
-
-        def PX(e, b, i):
-            project(b, i, 0, D // 2, 128)
-
-        def PY(e, b, i):
-            project(b, i, D // 2, D, 128)
-
-        def BI(e, b, i):
-            finish(b, i, 0, D)
-
-        def BX(e, b, i):
-            finish(b, i, 0, D // 2)
-
-        def BY(e, b, i):
-            finish(b, i, D // 2, D)
+        def finish(j):
+            b, i = divmod(j, NT)
+            nc.vector.tensor_tensor(out=o_sb[j][:], in0=banks["o", j][:], in1=b_bc[:], op=ALU.add)
+            nc.sync.dma_start(out=out[b].rearrange("(p i) d -> p i d", i=NT)[:, i, :], in_=o_sb[j][:])
 
         make_identity(nc, id_bf[:])
-        make_identity(nc, id_f[:])
         with tc.manual_schedule():
             nc.vector.memset(ws_sb[:].bitcast(I32), 0)
-            nc.vector.memset(dummy[:], 0.0)
-            nc.scalar.activation(dummy[:], dummy[:], ACT.Relu)
+            nc.scalar.activation(id_f[:], id_bf[:], ACT.Copy)
 
             nc.sync.dma_start(out=vs[:], in_=v_scale.rearrange("o (p t) x -> p (o t x)", t=T))
-            load_v(0, 0, 1)
-            load_v(0, 1, 2)
+            load_v(0, 0)
+            load_v(0, 1)
             load_kq(0)
-            load_v(0, 2, 4)
+            load_v(1, 0)
+            load_v(1, 1)
             load_u(0, 0)
-            load_u(0, 1)
             load_kq(1)
-            load_v(1, 0, 2)
-            load_v(1, 2, 4)
             load_w()
+            load_u(0, 1)
+            nc.sync.dma_start(out=b_bc[:], in_=b_o.partition_broadcast(P))
             load_u(1, 0)
             load_u(1, 1)
-            table = dict(Tk=Tk, Tq=Tq, CK=CK, CQ=CQ, QK=QK, RL=RL, SQ=SQ, QA=QA, W=W, IL=IL, QV=QV, TU=TU, CU=CU, AV=AV, GT=GT, QG=QG, QX=QX, QY=QY, PJ=PJ, PX=PX, PY=PY, BI=BI, BX=BX, BY=BY)
-            for step in ORDER.split():
-                name = step[1 : 2 if step[1] == "W" else 3]
-                table[name](step[0], *[int(c) for c in step[1 + len(name) :]])
+
+            for t in range(T):
+                widen_v(0, 0, t)
+            for t in range(T - 1):
+                widen_s(0, 1, t)
+            widen_v(0, 1, T - 1)
+            for name in "kq":
+                turn(name, 0)
+                copy_turned(name, 0)
+            scores(0)
+            scores(1)
+            interleave(0, 0)
+            interleave(0, 1)
+            quant_v(0, 0)
+            quant_v(0, 1)
+            widen_s(1, 0, 0)
+            widen_s(1, 0, 1)
+            relu(0)
+            widen_s(1, 0, 2)
+            square(0)
+            widen_v(1, 0, 3)
+            relu(1)
+            scores(2)
+            for name in "kq":
+                turn(name, 1)
+            quant_attn(0)
+            mix(0, 0)
+            mix(0, 1)
+            interleave(1, 0)
+            copy_turned("k", 1)
+            square(1)
+            relu(2)
+            copy_turned("q", 1)
+
+            last = TILES - 1
+            for j in range(TILES):
+                gate(j, 0)
+                if j + 1 < TILES:
+                    quant_attn(j + 1)
+                    mix(j + 1, 0)
+                if j == NT - 1:
+                    quant_v(1, 1)
+                if j + 1 < TILES:
+                    mix(j + 1, 1)
+                if j < 3:
+                    widen_s(1, 1, j)
+                if j + 2 < TILES:
+                    square(j + 2)
+                if j == last:
+                    turn_gated(j, 0, 1)
+                    copy_gated(j, 0, 1)
+                gate(j, 1)
+                if j < last:
+                    turn_gated(j, 0, G)
+                else:
+                    turn_gated(j, 1, G)
+                if j + 3 < TILES:
+                    scores(j + 3)
+                if j == 0:
+                    widen_s(1, 1, T - 1)
+                if j < last:
+                    copy_gated(j, 0, G)
+                else:
+                    copy_gated(j, 1, G)
+                if j + 3 < TILES:
+                    relu(j + 3)
+                if j >= 1:
+                    quant_gated(j - 1, 0, G)
+                if 2 <= j:
+                    finish(j - 2)
+                if j >= 1:
+                    project(j - 1, 0, G)
+                if j == 0:
+                    quant_v(1, 0)
+                if j == 2:
+                    interleave(1, 1)
+            quant_gated(last, 0, 1)
+            project(last, 0, 1)
+            quant_gated(last, 1, G)
+            finish(last - 1)
+            project(last, 1, G)
+            finish(last)

@@ -41,8 +41,8 @@ def tile_gatedattentionunit_pb_w4_kernel(tc, q, k, u, v_bytes, v_scale, W_o_word
 
         k_sb = [kt([P, T, S], BF16, "k_sb%d" % b) for b in range(B)]
         q_sb = [kt([P, NT, S], BF16, "q_sb%d" % b) for b in range(B)]
-        kT = [kt([P, T, P], BF16, "kT%d" % b) for b in range(B)]
-        qT = [kt([P, NT, P], BF16, "qT%d" % b) for b in range(B)]
+        kqT = [kt([P, T + 1, P], BF16, "kqT%d" % b) for b in range(B)]
+        qT = [kt([P, NT - 1, P], BF16, "qT%d" % b) for b in range(B)]
         vb = [[kt([P, 2, H], U8, "vb%d_%d" % (b, c)) for c in range(2)] for b in range(B)]
         v_bf = [[kt([P, T, KP], BF16, "v_bf%d_%d" % (b, g)) for g in range(G)] for b in range(B)]
         v_il = [[kt([P, KP, T], BF16, "v_il%d_%d" % (b, g)) for g in range(G)] for b in range(B)]
@@ -87,13 +87,19 @@ def tile_gatedattentionunit_pb_w4_kernel(tc, q, k, u, v_bytes, v_scale, W_o_word
                 nc.sync.dma_start(out=ws_i[r:P:32, :, :], in_=rows[r])
 
         def turn(name, b):
-            src = {"k": k_sb, "q": q_sb}[name][b]
-            bank = banks[name, b] = ps_tr.tile([P, T, P], BF16, name="tr_bank")
-            for t in range(T):
-                nc.tensor.transpose(bank[:, t, :], src[:, t, :], id_bf[:])
+            if name == "k":
+                srcs = [k_sb[b][:, t, :] for t in range(T)] + [q_sb[b][:, 0, :]]
+            else:
+                srcs = [q_sb[b][:, i, :] for i in range(1, NT)]
+            if b == 0:
+                bank = banks[name, b] = ps_tr.tile([P, len(srcs), P], BF16, name="tr_bank")
+            else:
+                bank = banks[name, b] = ps_qk.tile([P, len(srcs), P], BF16, name="qk_bank")
+            for n, src in enumerate(srcs):
+                nc.tensor.transpose(bank[:, n, :], src, id_bf[:])
 
         def copy_turned(name, b):
-            nc.scalar.copy(out={"k": kT, "q": qT}[name][b][:], in_=banks[name, b][:])
+            nc.scalar.copy(out={"k": kqT, "q": qT}[name][b][:], in_=banks[name, b][:])
 
         def widen_v(b, g, t):
             src = vb[b][t // 2][:, t % 2, KP * g : KP * (g + 1)].bitcast(FP8)
@@ -115,13 +121,14 @@ def tile_gatedattentionunit_pb_w4_kernel(tc, q, k, u, v_bytes, v_scale, W_o_word
             b, i = divmod(j, NT)
             bank = banks["qk", j] = ps_qk.tile([P, T, P], F32, name="qk_bank")
             for t in range(T):
-                nc.tensor.matmul(bank[:, t, :], lhsT=kT[b][:, t, :], rhs=qT[b][:, i, :], start=True, stop=True)
+                rhs = kqT[b][:, T, :] if i == 0 else qT[b][:, i - 1, :]
+                nc.tensor.matmul(bank[:, t, :], lhsT=kqT[b][:, t, :], rhs=rhs, start=True, stop=True)
 
-        def relu(j):
-            nc.scalar.activation(r_sb[j][:], banks["qk", j][:].rearrange("p t n -> p n t"), ACT.Relu)
+        def relu(j, n0=0, n1=P):
+            nc.scalar.activation(r_sb[j][:, n0:n1], banks["qk", j][:, :, n0:n1].rearrange("p t n -> p n t"), ACT.Relu)
 
-        def square(j):
-            nc.scalar.activation(at_il[j][:], r_sb[j][:], ACT.Square, scale=QK_SCALE)
+        def square(j, n0=0, n1=P):
+            nc.scalar.activation(at_il[j][:, n0:n1], r_sb[j][:, n0:n1], ACT.Square, scale=QK_SCALE)
 
         def quant_attn(j):
             nc.vector.quantize_mx(out=at_c[j][:].bitcast(FP8X4), scales=at_s[j][:], in_=at_il[j][:].rearrange("p n t -> p (n t)"))
@@ -178,10 +185,94 @@ def tile_gatedattentionunit_pb_w4_kernel(tc, q, k, u, v_bytes, v_scale, W_o_word
                     stop=(g == G - 1),
                 )
 
-        def finish(j):
+        def finish(j, d0=0, d1=D):
             b, i = divmod(j, NT)
-            nc.vector.tensor_tensor(out=o_sb[j][:], in0=banks["o", j][:], in1=b_bc[:], op=ALU.add)
-            nc.sync.dma_start(out=out[b].rearrange("(p i) d -> p i d", i=NT)[:, i, :], in_=o_sb[j][:])
+            nc.vector.tensor_tensor(out=o_sb[j][:, d0:d1], in0=banks["o", j][:, d0:d1], in1=b_bc[:, d0:d1], op=ALU.add)
+            nc.sync.dma_start(out=out[b].rearrange("(p i) d -> p i d", i=NT)[:, i, d0:d1], in_=o_sb[j][:, d0:d1])
+
+
+        last = TILES - 1
+
+        def needs(step):
+            f, a = step[0], step[1:]
+            if f is copy_turned:
+                return [(turn,) + a]
+            if f is interleave:
+                return [("widen",) + a + (t,) for t in range(T)]
+            if f is quant_v:
+                return [(interleave,) + a]
+            if f is scores:
+                return [(copy_turned, "k", a[0] // NT)] + [(copy_turned, "q", a[0] // NT)] * (a[0] % NT > 0)
+            if f is relu:
+                return [(scores, a[0])]
+            if f is square:
+                return [(relu,) + a]
+            if f is quant_attn:
+                return [(square,) + a]
+            if f is mix:
+                return [(quant_attn, a[0]), (quant_v, a[0] // NT, a[1])]
+            if f is gate:
+                return [(mix,) + a]
+            if f is turn_gated:
+                return [(gate, a[0], g) for g in range(a[1], a[2])]
+            if f is copy_gated:
+                return [(turn_gated,) + a]
+            if f is quant_gated:
+                return [("copied", a[0], g) for g in range(a[1], a[2])]
+            if f is project:
+                return [("quantised", a[0], g) for g in range(a[1], a[2])]
+            if f is finish:
+                return [("projected", a[0])]
+            return []
+
+        def gives(step):
+            f, a = step[0], step[1:]
+            if (f is relu or f is square) and a[1:] == (P // 2, P):
+                return [step, (f, a[0])]
+            if f is widen_v or f is widen_s:
+                return [("widen",) + a]
+            if f is copy_gated:
+                return [step] + [("copied", a[0], g) for g in range(a[1], a[2])]
+            if f is quant_gated:
+                return [("quantised", a[0], g) for g in range(a[1], a[2])]
+            if f is project and a[2] == G:
+                return [("projected", a[0])]
+            return [step]
+
+        def bank_of(step):
+            f, a = step[0], step[1:]
+            if f is turn:
+                return ("qk" if a[1] else "tr", 2, (copy_turned,) + a)
+            if f is turn_gated:
+                return ("tr", 2, (copy_gated,) + a)
+            if f is scores:
+                return ("qk", 2, (relu,) + a)
+            if f is mix:
+                return ("av", 3, (gate,) + a)
+            if f is project and a[1] == 0:
+                return ("o", 1, (finish, a[0])) if a[0] < TILES - 2 else ("qk", 2, (finish, a[0]))
+            return None
+
+        def issue(queues):
+            done, taken = set(), {}
+            heads = [0] * len(queues)
+            for sweep in range(sum(len(x) for x in queues)):
+                for e, queue in enumerate(queues):
+                    if heads[e] == len(queue):
+                        continue
+                    step = queue[heads[e]]
+                    wait = needs(step)
+                    bank = bank_of(step)
+                    if bank and len(taken.get(bank[0], [])) >= bank[1]:
+                        wait = wait + [taken[bank[0]][-bank[1]]]
+                    if all(w in done for w in wait):
+                        step[0](*step[1:])
+                        for w in gives(step):
+                            done.add(w)
+                        if bank:
+                            taken.setdefault(bank[0], []).append(bank[2])
+                        heads[e] = heads[e] + 1
+            assert heads == [len(x) for x in queues], [x[h] for x, h in zip(queues, heads) if h < len(x)]
 
         make_identity(nc, id_bf[:])
         with tc.manual_schedule():
@@ -202,84 +293,30 @@ def tile_gatedattentionunit_pb_w4_kernel(tc, q, k, u, v_bytes, v_scale, W_o_word
             load_u(1, 0)
             load_u(1, 1)
 
-            for t in range(T):
-                widen_v(0, 0, t)
-            for t in range(T - 1):
-                widen_s(0, 1, t)
-            widen_v(0, 1, T - 1)
-            for name in "kq":
-                turn(name, 0)
-                copy_turned(name, 0)
-            scores(0)
-            scores(1)
-            interleave(0, 0)
-            interleave(0, 1)
-            quant_v(0, 0)
-            quant_v(0, 1)
-            widen_s(1, 0, 0)
-            widen_s(1, 0, 1)
-            relu(0)
-            widen_s(1, 0, 2)
-            square(0)
-            widen_v(1, 0, 3)
-            relu(1)
-            scores(2)
-            for name in "kq":
-                turn(name, 1)
-            quant_attn(0)
-            mix(0, 0)
-            mix(0, 1)
-            interleave(1, 0)
-            copy_turned("k", 1)
-            square(1)
-            relu(2)
-            copy_turned("q", 1)
-
-            last = TILES - 1
+            vector = [(widen_v, 0, 0, t) for t in range(T)] + [(widen_v, 0, 1, 3)]
+            vector += [(interleave, 0, 0), (interleave, 0, 1), (quant_v, 0, 0), (quant_v, 0, 1)]
+            vector += [(widen_v, 1, 0, 3), (quant_attn, 0), (interleave, 1, 0)]
             for j in range(TILES):
-                gate(j, 0)
-                if j + 1 < TILES:
-                    quant_attn(j + 1)
-                    mix(j + 1, 0)
-                if j == NT - 1:
-                    quant_v(1, 1)
-                if j + 1 < TILES:
-                    mix(j + 1, 1)
-                if j < 3:
-                    widen_s(1, 1, j)
-                if j + 2 < TILES:
-                    square(j + 2)
-                if j == last:
-                    turn_gated(j, 0, 1)
-                    copy_gated(j, 0, 1)
-                gate(j, 1)
-                if j < last:
-                    turn_gated(j, 0, G)
-                else:
-                    turn_gated(j, 1, G)
-                if j + 3 < TILES:
-                    scores(j + 3)
-                if j == 0:
-                    widen_s(1, 1, T - 1)
-                if j < last:
-                    copy_gated(j, 0, G)
-                else:
-                    copy_gated(j, 1, G)
-                if j + 3 < TILES:
-                    relu(j + 3)
+                vector += [(gate, j, 0)] + [(quant_attn, j + 1)] * (j < last) + [(quant_v, 1, 1)] * (j == NT - 1) + [(gate, j, 1)]
+                vector += [(widen_v, 1, 1, 3)] * (j == 1)
                 if j >= 1:
-                    quant_gated(j - 1, 0, G)
-                if 2 <= j:
-                    finish(j - 2)
-                if j >= 1:
-                    project(j - 1, 0, G)
-                if j == 0:
-                    quant_v(1, 0)
-                if j == 2:
-                    interleave(1, 1)
-            quant_gated(last, 0, 1)
-            project(last, 0, 1)
-            quant_gated(last, 1, G)
-            finish(last - 1)
-            project(last, 1, G)
-            finish(last)
+                    vector += [(quant_gated, j - 1, 0, G)]
+                if j >= 2:
+                    vector += [(finish, j - 2)]
+                vector += {0: [(quant_v, 1, 0)], 2: [(interleave, 1, 1)]}.get(j, [])
+            vector += [(quant_gated, last, 0, 1), (quant_gated, last, 1, G), (finish, last - 1), (finish, last, 0, D // 2), (finish, last, D // 2, D)]
+
+            scalar = [(widen_s, 0, 1, t) for t in range(3)] + [(copy_turned, "k", 0), (copy_turned, "q", 0)]
+            scalar += [(widen_s, 1, 0, 0), (widen_s, 1, 0, 1), (relu, 0, 0, P // 2), (relu, 0, P // 2, P), (square, 0, 0, P // 2), (square, 0, P // 2, P)]
+            scalar += [(widen_s, 1, 0, 2), (relu, 1), (widen_s, 1, 1, 0), (square, 1), (relu, 2), (widen_s, 1, 1, 1), (square, 2)]
+            scalar += [(relu, 3), (copy_gated, 0, 0, G), (square, 3), (copy_turned, "k", 1), (copy_turned, "q", 1), (copy_gated, 1, 0, G), (widen_s, 1, 1, 2), (relu, 4)]
+            for j in range(2, last):
+                scalar += [(relu, j + 3)] * (j + 3 < TILES) + [(square, j + 2)] * (j + 2 < TILES) + [(copy_gated, j, 0, G)]
+            scalar += [(copy_gated, last, 0, 1), (copy_gated, last, 1, G)]
+
+            tensor = [(turn, "k", 0), (turn, "q", 0), (scores, 0), (scores, 1), (scores, 2), (mix, 0, 0), (mix, 0, 1), (scores, 3)]
+            tensor += [(mix, 1, 0), (mix, 1, 1), (turn_gated, 0, 0, G), (turn, "k", 1), (mix, 2, 0), (mix, 2, 1), (turn, "q", 1), (turn_gated, 1, 0, G), (project, 0, 0, G), (scores, 4), (scores, 5)]
+            for j in range(2, last):
+                tensor += [(mix, j + 1, 0), (mix, j + 1, 1), (turn_gated, j, 0, G)] + [(scores, j + 4)] * (j + 4 < TILES) + [(project, j - 1, 0, G)]
+            tensor += [(turn_gated, last, 0, 1), (turn_gated, last, 1, G), (project, last - 1, 0, G), (project, last, 0, 1), (project, last, 1, G)]
+            issue([tensor, scalar, vector])

@@ -24,6 +24,7 @@ NT = N // P
 TILES = B * NT
 KP = P * T
 G = H // KP
+HELPED = {1: 3, 3: 5}
 QK_SCALE = 1.0 / math.sqrt(S)
 
 
@@ -58,6 +59,7 @@ def tile_gatedattentionunit_pb_w4_kernel(tc, q, k, u, v_bytes, v_scale, W_o_word
         gc = [kt([P, G, P], U32, "gc%d" % j) for j in range(TILES)]
         gs = [kt([P, G, P], U8, "gs%d" % j) for j in range(TILES)]
         o_sb = [kt([P, D], F32, "o_sb%d" % j) for j in range(TILES)]
+        o_raw = {j: kt([P, D], F32, "o_raw%d" % j) for j in HELPED}
         vs = kt([P, T], F32, "vs")
         w_sb = kt([P, G, 2 * D], U8, "w_sb")
         ws_sb = kt([P, G, D], U8, "ws_sb")
@@ -170,7 +172,7 @@ def tile_gatedattentionunit_pb_w4_kernel(tc, q, k, u, v_bytes, v_scale, W_o_word
 
         def project(j, g0, g1):
             if g0 == 0:
-                if j < TILES - 2:
+                if j < NT:
                     banks["o", j] = ps_o.tile([P, D], F32, name="o_bank")
                 else:
                     banks["o", j] = ps_qk.tile([P, D], F32, name="qk_bank")
@@ -185,10 +187,20 @@ def tile_gatedattentionunit_pb_w4_kernel(tc, q, k, u, v_bytes, v_scale, W_o_word
                     stop=(g == G - 1),
                 )
 
-        def finish(j, d0=0, d1=D):
+        def store(j, d0=0, d1=D):
             b, i = divmod(j, NT)
+            src = gT[HELPED[j]][:].rearrange("p g n t -> p (g n t)").bitcast(F32) if j in HELPED else o_sb[j][:]
+            nc.sync.dma_start(out=out[b].rearrange("(p i) d -> p i d", i=NT)[:, i, d0:d1], in_=src[:, d0:d1])
+
+        def finish(j, d0=0, d1=D):
             nc.vector.tensor_tensor(out=o_sb[j][:, d0:d1], in0=banks["o", j][:, d0:d1], in1=b_bc[:, d0:d1], op=ALU.add)
-            nc.sync.dma_start(out=out[b].rearrange("(p i) d -> p i d", i=NT)[:, i, d0:d1], in_=o_sb[j][:, d0:d1])
+
+        def evacuate(j):
+            nc.scalar.copy(out=o_raw[j][:], in_=banks["o", j][:])
+
+        def add_bias(j):
+            dst = gT[HELPED[j]][:].rearrange("p g n t -> p (g n t)").bitcast(F32)
+            nc.gpsimd.tensor_tensor(out=dst, in0=o_raw[j][:], in1=b_bc[:], op=ALU.add)
 
 
         last = TILES - 1
@@ -221,7 +233,11 @@ def tile_gatedattentionunit_pb_w4_kernel(tc, q, k, u, v_bytes, v_scale, W_o_word
                 return [("copied", a[0], g) for g in range(a[1], a[2])]
             if f is project:
                 return [("quantised", a[0], g) for g in range(a[1], a[2])]
-            if f is finish:
+            if f is store:
+                return [(add_bias if a[0] in HELPED else finish,) + a]
+            if f is add_bias:
+                return [(evacuate, a[0])] + [("quantised", HELPED[a[0]], g) for g in range(G)]
+            if f is finish or f is evacuate:
                 return [("projected", a[0])]
             return []
 
@@ -250,7 +266,8 @@ def tile_gatedattentionunit_pb_w4_kernel(tc, q, k, u, v_bytes, v_scale, W_o_word
             if f is mix:
                 return ("av", 3, (gate,) + a)
             if f is project and a[1] == 0:
-                return ("o", 1, (finish, a[0])) if a[0] < TILES - 2 else ("qk", 2, (finish, a[0]))
+                reader = (evacuate if a[0] in HELPED else finish, a[0])
+                return ("o", 1, reader) if a[0] < NT else ("qk", 2, reader)
             return None
 
         def issue(queues):
@@ -297,11 +314,12 @@ def tile_gatedattentionunit_pb_w4_kernel(tc, q, k, u, v_bytes, v_scale, W_o_word
             vector += [(interleave, 0, 0), (interleave, 0, 1), (quant_v, 0, 0), (quant_v, 0, 1)]
             vector += [(widen_v, 1, 0, 3), (quant_attn, 0), (interleave, 1, 0)]
             for j in range(TILES):
-                vector += [(gate, j, 0)] + [(quant_attn, j + 1)] * (j < last) + [(quant_v, 1, 1)] * (j == NT - 1) + [(gate, j, 1)]
+                vector += [(gate, j, 0)] + [(quant_attn, j + 1)] * (j < NT) + [(quant_v, 1, 1)] * (j == NT - 1) + [(gate, j, 1)]
+                vector += [(quant_attn, j + 2)] * (NT - 1 <= j < TILES - 2)
                 vector += [(widen_v, 1, 1, 3)] * (j == 1)
                 if j >= 1:
                     vector += [(quant_gated, j - 1, 0, G)]
-                if j >= 2:
+                if j >= 2 and j - 2 not in HELPED:
                     vector += [(finish, j - 2)]
                 vector += {0: [(quant_v, 1, 0)], 2: [(interleave, 1, 1)]}.get(j, [])
             vector += [(quant_gated, last, 0, 1), (quant_gated, last, 1, G), (finish, last - 1), (finish, last, 0, D // 2), (finish, last, D // 2, D)]
@@ -310,13 +328,15 @@ def tile_gatedattentionunit_pb_w4_kernel(tc, q, k, u, v_bytes, v_scale, W_o_word
             scalar += [(widen_s, 1, 0, 0), (widen_s, 1, 0, 1), (relu, 0, 0, P // 2), (relu, 0, P // 2, P), (square, 0, 0, P // 2), (square, 0, P // 2, P)]
             scalar += [(widen_s, 1, 0, 2), (relu, 1), (widen_s, 1, 1, 0), (square, 1), (relu, 2), (widen_s, 1, 1, 1), (square, 2)]
             scalar += [(relu, 3), (copy_gated, 0, 0, G), (square, 3), (copy_turned, "k", 1), (copy_turned, "q", 1), (copy_gated, 1, 0, G), (widen_s, 1, 1, 2), (relu, 4)]
-            for j in range(2, last):
-                scalar += [(relu, j + 3)] * (j + 3 < TILES) + [(square, j + 2)] * (j + 2 < TILES) + [(copy_gated, j, 0, G)]
+            scalar += [(relu, 5), (square, 4), (copy_gated, 2, 0, G), (square, 5), (relu, 6), (evacuate, 1), (square, 6), (copy_gated, 3, 0, G), (relu, 7)]
+            scalar += [(square, 7), (copy_gated, 4, 0, G), (evacuate, 3), (copy_gated, 5, 0, G), (copy_gated, 6, 0, G)]
             scalar += [(copy_gated, last, 0, 1), (copy_gated, last, 1, G)]
 
             tensor = [(turn, "k", 0), (turn, "q", 0), (scores, 0), (scores, 1), (scores, 2), (mix, 0, 0), (mix, 0, 1), (scores, 3)]
             tensor += [(mix, 1, 0), (mix, 1, 1), (turn_gated, 0, 0, G), (turn, "k", 1), (mix, 2, 0), (mix, 2, 1), (turn, "q", 1), (turn_gated, 1, 0, G), (project, 0, 0, G), (scores, 4), (scores, 5)]
             for j in range(2, last):
-                tensor += [(mix, j + 1, 0), (mix, j + 1, 1), (turn_gated, j, 0, G)] + [(scores, j + 4)] * (j + 4 < TILES) + [(project, j - 1, 0, G)]
+                tensor += [(mix, j + 1, 0), (mix, j + 1, 1), (turn_gated, j, 0, G)] + [(scores, 6)] * (j == 2) + [(project, j - 1, 0, G)] + [(scores, 7)] * (j == 2)
             tensor += [(turn_gated, last, 0, 1), (turn_gated, last, 1, G), (project, last - 1, 0, G), (project, last, 0, 1), (project, last, 1, G)]
-            issue([tensor, scalar, vector])
+            gpsimd = [(add_bias, j) for j in HELPED]
+            sync = [(store, j) for j in (0, 2, 1, 4, 3, 5, 6)] + [(store, last, 0, D // 2), (store, last, D // 2, D)]
+            issue([tensor, scalar, gpsimd, vector, sync])

@@ -172,7 +172,7 @@ def tile_gatedattentionunit_pb_w4_kernel(tc, q, k, u, v_bytes, v_scale, W_o_word
 
         def project(j, g0, g1):
             if g0 == 0:
-                if j < NT:
+                if j < NT - 1:
                     banks["o", j] = ps_o.tile([P, D], F32, name="o_bank")
                 else:
                     banks["o", j] = ps_qk.tile([P, D], F32, name="qk_bank")
@@ -195,6 +195,21 @@ def tile_gatedattentionunit_pb_w4_kernel(tc, q, k, u, v_bytes, v_scale, W_o_word
         def finish(j, d0=0, d1=D):
             nc.vector.tensor_tensor(out=o_sb[j][:, d0:d1], in0=banks["o", j][:, d0:d1], in1=b_bc[:, d0:d1], op=ALU.add)
 
+        def interleave_low():
+            dst = v_il[1][1][:, : KP // 2].rearrange("p (c i) t -> p c t i", i=4)
+            src = v_bf[1][1][:, :, : KP // 2].rearrange("p t (c i) -> p c t i", i=4)
+            nc.vector.tensor_copy(out=dst, in_=src)
+
+        def interleave_high():
+            dst = gT[1][:].rearrange("p g n t -> p (g n) t")
+            src = v_bf[1][1][:, :, KP // 2 :].rearrange("p t c -> p c t")
+            nc.gpsimd.tensor_scalar(out=dst, in0=src, scalar1=1.0, scalar2=0.0, op0=ALU.mult, op1=ALU.add)
+
+        def quant_half(h):
+            cols = slice(h * KP // 2, (h + 1) * KP // 2)
+            src = gT[1][:].rearrange("p g n t -> p (g n t)") if h else v_il[1][1][:, cols].rearrange("p c t -> p (c t)")
+            nc.vector.quantize_mx(out=v_c[1][1][:, cols].bitcast(FP8X4), scales=v_s[1][1][:, cols], in_=src)
+
         def evacuate(j):
             nc.scalar.copy(out=o_raw[j][:], in_=banks["o", j][:])
 
@@ -209,6 +224,12 @@ def tile_gatedattentionunit_pb_w4_kernel(tc, q, k, u, v_bytes, v_scale, W_o_word
             f, a = step[0], step[1:]
             if f is copy_turned:
                 return [(turn,) + a]
+            if f is interleave_low or f is interleave_high:
+                return [("widen", 1, 1, t) for t in range(T)] + [("quantised", 1, 1)] * (f is interleave_high)
+            if f is quant_half:
+                return [(interleave_high if a[0] else interleave_low,)]
+            if f is mix and a[0] >= NT and a[1] == 1:
+                return [(quant_attn, a[0]), (quant_half, 0), (quant_half, 1)]
             if f is interleave:
                 return [("widen",) + a + (t,) for t in range(T)]
             if f is quant_v:
@@ -267,7 +288,7 @@ def tile_gatedattentionunit_pb_w4_kernel(tc, q, k, u, v_bytes, v_scale, W_o_word
                 return ("av", 3, (gate,) + a)
             if f is project and a[1] == 0:
                 reader = (evacuate if a[0] in HELPED else finish, a[0])
-                return ("o", 1, reader) if a[0] < NT else ("qk", 2, reader)
+                return ("o", 1, reader) if a[0] < NT - 1 else ("qk", 2, reader)
             return None
 
         def issue(queues):
@@ -314,29 +335,33 @@ def tile_gatedattentionunit_pb_w4_kernel(tc, q, k, u, v_bytes, v_scale, W_o_word
             vector += [(interleave, 0, 0), (interleave, 0, 1), (quant_v, 0, 0), (quant_v, 0, 1)]
             vector += [(widen_v, 1, 0, 3), (quant_attn, 0), (interleave, 1, 0)]
             for j in range(TILES):
-                vector += [(gate, j, 0)] + [(quant_attn, j + 1)] * (j < NT) + [(quant_v, 1, 1)] * (j == NT - 1) + [(gate, j, 1)]
-                vector += [(quant_attn, j + 2)] * (NT - 1 <= j < TILES - 2)
-                vector += [(widen_v, 1, 1, 3)] * (j == 1)
+                vector += [(gate, j, 0)] + [(quant_attn, j + 1)] * (j < NT - 1) + [(gate, j, 1)]
+                if j == NT - 1:
+                    vector += [(interleave_low,), (quant_attn, NT), (quant_half, 1), (quant_half, 0), (quant_gated, j - 1, 0, G), (quant_attn, NT + 1)]
+                    continue
+                vector += [(finish, 2)] * (j == 5) + [(quant_attn, 6)] * (j == 4) + [(widen_v, 1, 1, 3)] * (j == 1)
                 if j >= 1:
                     vector += [(quant_gated, j - 1, 0, G)]
-                if j >= 2 and j - 2 not in HELPED:
+                vector += [(quant_attn, 7)] * (j == 5)
+                if j >= 2 and j - 2 not in HELPED and j != 4:
                     vector += [(finish, j - 2)]
-                vector += {0: [(quant_v, 1, 0)], 2: [(interleave, 1, 1)]}.get(j, [])
+                vector += [(quant_v, 1, 0)] * (j == 0)
             vector += [(quant_gated, last, 0, 1), (quant_gated, last, 1, G), (finish, last - 1), (finish, last, 0, D // 2), (finish, last, D // 2, D)]
 
             scalar = [(widen_s, 0, 1, t) for t in range(3)] + [(copy_turned, "k", 0), (copy_turned, "q", 0)]
             scalar += [(widen_s, 1, 0, 0), (widen_s, 1, 0, 1), (relu, 0, 0, P // 2), (relu, 0, P // 2, P), (square, 0, 0, P // 2), (square, 0, P // 2, P)]
             scalar += [(widen_s, 1, 0, 2), (relu, 1), (widen_s, 1, 1, 0), (square, 1), (relu, 2), (widen_s, 1, 1, 1), (square, 2)]
             scalar += [(relu, 3), (copy_gated, 0, 0, G), (square, 3), (copy_turned, "k", 1), (copy_turned, "q", 1), (copy_gated, 1, 0, G), (widen_s, 1, 1, 2), (relu, 4)]
-            scalar += [(relu, 5), (square, 4), (copy_gated, 2, 0, G), (square, 5), (relu, 6), (evacuate, 1), (square, 6), (copy_gated, 3, 0, G), (relu, 7)]
-            scalar += [(square, 7), (copy_gated, 4, 0, G), (evacuate, 3), (copy_gated, 5, 0, G), (copy_gated, 6, 0, G)]
+            scalar += [(relu, 5), (square, 4), (copy_gated, 2, 0, G), (square, 5), (relu, 6), (copy_gated, 3, 0, G), (square, 6), (evacuate, 1), (relu, 7)]
+            scalar += [(copy_gated, 4, 0, G), (square, 7), (copy_gated, 5, 0, G), (evacuate, 3), (copy_gated, 6, 0, G)]
             scalar += [(copy_gated, last, 0, 1), (copy_gated, last, 1, G)]
 
             tensor = [(turn, "k", 0), (turn, "q", 0), (scores, 0), (scores, 1), (scores, 2), (mix, 0, 0), (mix, 0, 1), (scores, 3)]
             tensor += [(mix, 1, 0), (mix, 1, 1), (turn_gated, 0, 0, G), (turn, "k", 1), (mix, 2, 0), (mix, 2, 1), (turn, "q", 1), (turn_gated, 1, 0, G), (project, 0, 0, G), (scores, 4), (scores, 5)]
-            for j in range(2, last):
-                tensor += [(mix, j + 1, 0), (mix, j + 1, 1), (turn_gated, j, 0, G)] + [(scores, 6)] * (j == 2) + [(project, j - 1, 0, G)] + [(scores, 7)] * (j == 2)
+            tensor += [(mix, 3, 0), (mix, 3, 1), (turn_gated, 2, 0, G), (scores, 6), (project, 1, 0, G), (scores, 7), (turn_gated, 3, 0, G)]
+            tensor += [(mix, 4, 0), (mix, 4, 1), (mix, 5, 0), (mix, 5, 1), (turn_gated, 4, 0, G), (project, 2, 0, G), (mix, 6, 0), (mix, 6, 1), (turn_gated, 5, 0, G), (project, 3, 0, G)]
+            tensor += [(project, 4, 0, G), (mix, 7, 0), (mix, 7, 1), (turn_gated, 6, 0, G), (project, 5, 0, G)]
             tensor += [(turn_gated, last, 0, 1), (turn_gated, last, 1, G), (project, last - 1, 0, G), (project, last, 0, 1), (project, last, 1, G)]
-            gpsimd = [(add_bias, j) for j in HELPED]
-            sync = [(store, j) for j in (0, 2, 1, 4, 3, 5, 6)] + [(store, last, 0, D // 2), (store, last, D // 2, D)]
+            gpsimd = [(interleave_high,)] + [(add_bias, j) for j in HELPED]
+            sync = [(store, j) for j in (0, 1, 2, 4, 3, 5, 6)] + [(store, last, 0, D // 2), (store, last, D // 2, D)]
             issue([tensor, scalar, gpsimd, vector, sync])

@@ -24,7 +24,7 @@ NT = N // P
 TILES = B * NT
 KP = P * T
 G = H // KP
-HELPED = {1: 3, 3: 5}
+HELPED = (1, 3)
 QK_SCALE = 1.0 / math.sqrt(S)
 
 
@@ -49,7 +49,7 @@ def tile_gatedattentionunit_pb_w4_kernel(tc, q, k, u, v_bytes, v_scale, W_o_word
         v_il = [[kt([P, KP, T], BF16, "v_il%d_%d" % (b, g)) for g in range(G)] for b in range(B)]
         v_c = [[kt([P, KP], U32, "v_c%d_%d" % (b, g)) for g in range(G)] for b in range(B)]
         v_s = [[kt([P, KP], U8, "v_s%d_%d" % (b, g)) for g in range(G)] for b in range(B)]
-        u_sb = [kt([P, 2, H], BF16, "u_sb%d" % c) for c in range(TILES // 2)]
+        u_sb = [kt([P, H], BF16, "u_sb%d" % j) for j in range(TILES)]
         r_sb = [kt([P, P, T], F32, "r_sb%d" % j) for j in range(TILES)]
         at_il = [kt([P, P, T], BF16, "at_il%d" % j) for j in range(TILES)]
         at_c = [kt([P, P], U32, "at_c%d" % j) for j in range(TILES)]
@@ -68,6 +68,7 @@ def tile_gatedattentionunit_pb_w4_kernel(tc, q, k, u, v_bytes, v_scale, W_o_word
         id_f = kt([P, P], F32, "id_f")
 
         banks = {}
+        summed = {1: gT[3][:].rearrange("p g n t -> p (g n t)").bitcast(F32), 3: u_sb[6][:].bitcast(F32)}
 
         def load_kq(b):
             nc.sync.dma_start(out=k_sb[b][:], in_=k[b].rearrange("(p t) s -> p t s", t=T))
@@ -79,7 +80,8 @@ def tile_gatedattentionunit_pb_w4_kernel(tc, q, k, u, v_bytes, v_scale, W_o_word
 
         def load_u(b, c):
             rows = u[b].rearrange("(p i) h -> p i h", i=NT)
-            nc.sync.dma_start(out=u_sb[2 * b + c][:], in_=rows[:, 2 * c : 2 * c + 2, :])
+            for i in (2 * c, 2 * c + 1):
+                nc.sync.dma_start(out=u_sb[NT * b + i][:], in_=rows[:, i, :])
 
         def load_w():
             nc.sync.dma_start(out=w_sb[:], in_=W_o_words.rearrange("g p n -> p g n"))
@@ -150,7 +152,7 @@ def tile_gatedattentionunit_pb_w4_kernel(tc, q, k, u, v_bytes, v_scale, W_o_word
 
         def gate(j, g):
             av = banks["av", j, g][:].rearrange("n (p w e) -> n w p e", w=2, e=2)
-            gate_in = u_sb[j // 2][:, j % 2, KP * g : KP * (g + 1)].rearrange("n (p w e) -> n w p e", w=2, e=2)
+            gate_in = u_sb[j][:, KP * g : KP * (g + 1)].rearrange("n (p w e) -> n w p e", w=2, e=2)
             nc.vector.tensor_tensor(out=gt[j][g][:].rearrange("n (w p e) -> n w p e", w=2, e=2), in0=av, in1=gate_in, op=ALU.mult)
 
         def turn_gated(j, g0, g1):
@@ -189,33 +191,57 @@ def tile_gatedattentionunit_pb_w4_kernel(tc, q, k, u, v_bytes, v_scale, W_o_word
 
         def store(j, d0=0, d1=D):
             b, i = divmod(j, NT)
-            src = gT[HELPED[j]][:].rearrange("p g n t -> p (g n t)").bitcast(F32) if j in HELPED else o_sb[j][:]
+            src = summed[j] if j in HELPED else o_sb[j][:]
             nc.sync.dma_start(out=out[b].rearrange("(p i) d -> p i d", i=NT)[:, i, d0:d1], in_=src[:, d0:d1])
 
         def finish(j, d0=0, d1=D):
             nc.vector.tensor_tensor(out=o_sb[j][:, d0:d1], in0=banks["o", j][:, d0:d1], in1=b_bc[:, d0:d1], op=ALU.add)
 
         def interleave_low():
-            dst = v_il[1][1][:, : KP // 2].rearrange("p (c i) t -> p c t i", i=4)
-            src = v_bf[1][1][:, :, : KP // 2].rearrange("p t (c i) -> p c t i", i=4)
+            dst = v_il[1][1][:, : KP // 4].rearrange("p (c i) t -> p c t i", i=4)
+            src = v_bf[1][1][:, :, : KP // 4].rearrange("p t (c i) -> p c t i", i=4)
             nc.vector.tensor_copy(out=dst, in_=src)
 
+        def interleave_mid():
+            src = v_bf[1][1][:, :, KP // 4 : KP // 2].rearrange("p t c -> p c t")
+            nc.gpsimd.tensor_scalar(out=v_il[1][1][:, KP // 4 : KP // 2], in0=src, scalar1=1.0, scalar2=0.0, op0=ALU.mult, op1=ALU.add)
+
         def interleave_high():
-            dst = gT[1][:].rearrange("p g n t -> p (g n) t")
+            dst = u_sb[2][:].rearrange("p (c t) -> p c t", t=T)
             src = v_bf[1][1][:, :, KP // 2 :].rearrange("p t c -> p c t")
             nc.gpsimd.tensor_scalar(out=dst, in0=src, scalar1=1.0, scalar2=0.0, op0=ALU.mult, op1=ALU.add)
 
         def quant_half(h):
             cols = slice(h * KP // 2, (h + 1) * KP // 2)
-            src = gT[1][:].rearrange("p g n t -> p (g n t)") if h else v_il[1][1][:, cols].rearrange("p c t -> p (c t)")
+            src = u_sb[2][:] if h else v_il[1][1][:, cols].rearrange("p c t -> p (c t)")
             nc.vector.quantize_mx(out=v_c[1][1][:, cols].bitcast(FP8X4), scales=v_s[1][1][:, cols], in_=src)
+
+        def project_last(g):
+            for c in range(D // P):
+                if g == 0:
+                    if c < 3:
+                        banks["last", c] = ps_av.tile([P, P], F32, name="av_bank")
+                    else:
+                        banks["last", c] = ps_o.tile([P, P], F32, name="o_bank")
+                nc.tensor.matmul_mx(
+                    out=banks["last", c][:],
+                    lhsT=gc[last][:, g, :].bitcast(FP8X4),
+                    lhsT_scale=gs[last][:, g, :],
+                    rhs=w_sb[:, g, 2 * P * c : 2 * P * (c + 1)].bitcast(FP4X4),
+                    rhs_scale=ws_sb[:, g, P * c : P * (c + 1)],
+                    start=(g == 0),
+                    stop=(g == G - 1),
+                )
+
+        def finish_last(c):
+            cols = slice(P * c, P * (c + 1))
+            nc.vector.tensor_tensor(out=o_sb[last][:, cols], in0=banks["last", c][:], in1=b_bc[:, cols], op=ALU.add)
 
         def evacuate(j):
             nc.scalar.copy(out=o_raw[j][:], in_=banks["o", j][:])
 
         def add_bias(j):
-            dst = gT[HELPED[j]][:].rearrange("p g n t -> p (g n t)").bitcast(F32)
-            nc.gpsimd.tensor_tensor(out=dst, in0=o_raw[j][:], in1=b_bc[:], op=ALU.add)
+            nc.gpsimd.tensor_tensor(out=summed[j], in0=o_raw[j][:], in1=b_bc[:], op=ALU.add)
 
 
         last = TILES - 1
@@ -224,10 +250,10 @@ def tile_gatedattentionunit_pb_w4_kernel(tc, q, k, u, v_bytes, v_scale, W_o_word
             f, a = step[0], step[1:]
             if f is copy_turned:
                 return [(turn,) + a]
-            if f is interleave_low or f is interleave_high:
-                return [("widen", 1, 1, t) for t in range(T)] + [("quantised", 1, 1)] * (f is interleave_high)
+            if f is interleave_low or f is interleave_high or f is interleave_mid:
+                return [("widen", 1, 1, t) for t in range(T)] + [(gate, 2, 1)] * (f is interleave_high)
             if f is quant_half:
-                return [(interleave_high if a[0] else interleave_low,)]
+                return [(interleave_high,)] if a[0] else [(interleave_low,), (interleave_mid,)]
             if f is mix and a[0] >= NT and a[1] == 1:
                 return [(quant_attn, a[0]), (quant_half, 0), (quant_half, 1)]
             if f is interleave:
@@ -254,10 +280,16 @@ def tile_gatedattentionunit_pb_w4_kernel(tc, q, k, u, v_bytes, v_scale, W_o_word
                 return [("copied", a[0], g) for g in range(a[1], a[2])]
             if f is project:
                 return [("quantised", a[0], g) for g in range(a[1], a[2])]
+            if f is project_last:
+                return [("quantised", last, a[0])]
+            if f is finish_last:
+                return [(project_last, 1)]
+            if f is store and a[0] == last:
+                return [(finish_last, a[2] // P - 1)]
             if f is store:
                 return [(add_bias if a[0] in HELPED else finish,) + a]
             if f is add_bias:
-                return [(evacuate, a[0])] + [("quantised", HELPED[a[0]], g) for g in range(G)]
+                return [(evacuate, a[0])] + [("quantised", 3, 1) if a[0] == 1 else (gate, 6, 1)]
             if f is finish or f is evacuate:
                 return [("projected", a[0])]
             return []
@@ -335,33 +367,33 @@ def tile_gatedattentionunit_pb_w4_kernel(tc, q, k, u, v_bytes, v_scale, W_o_word
             vector += [(interleave, 0, 0), (interleave, 0, 1), (quant_v, 0, 0), (quant_v, 0, 1)]
             vector += [(widen_v, 1, 0, 3), (quant_attn, 0), (interleave, 1, 0)]
             for j in range(TILES):
-                vector += [(gate, j, 0)] + [(quant_attn, j + 1)] * (j < NT - 1) + [(gate, j, 1)]
+                vector += [(gate, j, 0)] + [(quant_attn, j + 1)] * (j < NT - 2) + [(gate, j, 1)] + [(quant_attn, j + 1)] * (j == NT - 2)
                 if j == NT - 1:
                     vector += [(interleave_low,), (quant_attn, NT), (quant_half, 1), (quant_half, 0), (quant_gated, j - 1, 0, G), (quant_attn, NT + 1)]
                     continue
-                vector += [(finish, 2)] * (j == 5) + [(quant_attn, 6)] * (j == 4) + [(widen_v, 1, 1, 3)] * (j == 1)
+                vector += [(finish, 2)] * (j == 5) + [(quant_attn, 6)] * (j == 4) + [(widen_v, 1, 1, 2), (widen_v, 1, 1, 3)] * (j == 1)
                 if j >= 1:
                     vector += [(quant_gated, j - 1, 0, G)]
                 vector += [(quant_attn, 7)] * (j == 5)
                 if j >= 2 and j - 2 not in HELPED and j != 4:
                     vector += [(finish, j - 2)]
                 vector += [(quant_v, 1, 0)] * (j == 0)
-            vector += [(quant_gated, last, 0, 1), (quant_gated, last, 1, G), (finish, last - 1), (finish, last, 0, D // 2), (finish, last, D // 2, D)]
+            vector += [(quant_gated, last, 0, 1), (quant_gated, last, 1, G), (finish, last - 1, 0, D // 2), (finish, last - 1, D // 2, D)] + [(finish_last, c) for c in range(D // P)]
 
             scalar = [(widen_s, 0, 1, t) for t in range(3)] + [(copy_turned, "k", 0), (copy_turned, "q", 0)]
             scalar += [(widen_s, 1, 0, 0), (widen_s, 1, 0, 1), (relu, 0, 0, P // 2), (relu, 0, P // 2, P), (square, 0, 0, P // 2), (square, 0, P // 2, P)]
             scalar += [(widen_s, 1, 0, 2), (relu, 1), (widen_s, 1, 1, 0), (square, 1), (relu, 2), (widen_s, 1, 1, 1), (square, 2)]
-            scalar += [(relu, 3), (copy_gated, 0, 0, G), (square, 3), (copy_turned, "k", 1), (copy_turned, "q", 1), (copy_gated, 1, 0, G), (widen_s, 1, 1, 2), (relu, 4)]
-            scalar += [(relu, 5), (square, 4), (copy_gated, 2, 0, G), (square, 5), (relu, 6), (copy_gated, 3, 0, G), (square, 6), (evacuate, 1), (relu, 7)]
+            scalar += [(relu, 3), (copy_gated, 0, 0, G), (square, 3), (copy_turned, "k", 1), (copy_gated, 1, 0, G), (copy_turned, "q", 1), (relu, 4), (relu, 5), (square, 4), (copy_gated, 2, 0, G)]
+            scalar += [(square, 5), (relu, 6), (copy_gated, 3, 0, G), (square, 6), (evacuate, 1), (relu, 7)]
             scalar += [(copy_gated, 4, 0, G), (square, 7), (copy_gated, 5, 0, G), (evacuate, 3), (copy_gated, 6, 0, G)]
             scalar += [(copy_gated, last, 0, 1), (copy_gated, last, 1, G)]
 
             tensor = [(turn, "k", 0), (turn, "q", 0), (scores, 0), (scores, 1), (scores, 2), (mix, 0, 0), (mix, 0, 1), (scores, 3)]
-            tensor += [(mix, 1, 0), (mix, 1, 1), (turn_gated, 0, 0, G), (turn, "k", 1), (mix, 2, 0), (mix, 2, 1), (turn, "q", 1), (turn_gated, 1, 0, G), (project, 0, 0, G), (scores, 4), (scores, 5)]
-            tensor += [(mix, 3, 0), (mix, 3, 1), (turn_gated, 2, 0, G), (scores, 6), (project, 1, 0, G), (scores, 7), (turn_gated, 3, 0, G)]
+            tensor += [(mix, 1, 0), (mix, 1, 1), (turn_gated, 0, 0, G), (turn, "k", 1), (mix, 2, 0), (mix, 2, 1), (turn_gated, 1, 0, G), (turn, "q", 1), (scores, 4), (project, 0, 0, G), (scores, 5)]
+            tensor += [(mix, 3, 0), (mix, 3, 1), (turn_gated, 2, 0, G), (scores, 6), (project, 1, 0, G), (turn_gated, 3, 0, G), (scores, 7)]
             tensor += [(mix, 4, 0), (mix, 4, 1), (mix, 5, 0), (mix, 5, 1), (turn_gated, 4, 0, G), (project, 2, 0, G), (mix, 6, 0), (mix, 6, 1), (turn_gated, 5, 0, G), (project, 3, 0, G)]
             tensor += [(project, 4, 0, G), (mix, 7, 0), (mix, 7, 1), (turn_gated, 6, 0, G), (project, 5, 0, G)]
-            tensor += [(turn_gated, last, 0, 1), (turn_gated, last, 1, G), (project, last - 1, 0, G), (project, last, 0, 1), (project, last, 1, G)]
-            gpsimd = [(interleave_high,)] + [(add_bias, j) for j in HELPED]
-            sync = [(store, j) for j in (0, 1, 2, 4, 3, 5, 6)] + [(store, last, 0, D // 2), (store, last, D // 2, D)]
+            tensor += [(turn_gated, last, 0, 1), (turn_gated, last, 1, G), (project, last - 1, 0, G), (project_last, 0), (project_last, 1)]
+            gpsimd = [(interleave_mid,), (interleave_high,)] + [(add_bias, j) for j in HELPED]
+            sync = [(store, j) for j in (0, 1, 2, 4, 3, 5)] + [(store, j, d, d + D // 2) for j in (last - 1, last) for d in (0, D // 2)]
             issue([tensor, scalar, gpsimd, vector, sync])

@@ -68,7 +68,7 @@ def tile_gatedattentionunit_pb_w4_kernel(tc, q, k, u, v_bytes, v_scale, W_o_word
         id_f = kt([P, P], F32, "id_f")
 
         banks = {}
-        summed = {1: gT[3][:].rearrange("p g n t -> p (g n t)").bitcast(F32), 3: u_sb[6][:].bitcast(F32)}
+        summed = {1: u_sb[4][:].bitcast(F32), 3: u_sb[6][:].bitcast(F32)}
 
         def load_kq(b):
             nc.sync.dma_start(out=k_sb[b][:], in_=k[b].rearrange("(p t) s -> p t s", t=T))
@@ -95,10 +95,7 @@ def tile_gatedattentionunit_pb_w4_kernel(tc, q, k, u, v_bytes, v_scale, W_o_word
                 srcs = [k_sb[b][:, t, :] for t in range(T)] + [q_sb[b][:, 0, :]]
             else:
                 srcs = [q_sb[b][:, i, :] for i in range(1, NT)]
-            if b == 0:
-                bank = banks[name, b] = ps_tr.tile([P, len(srcs), P], BF16, name="tr_bank")
-            else:
-                bank = banks[name, b] = ps_qk.tile([P, len(srcs), P], BF16, name="qk_bank")
+            bank = banks[name, b] = ps_tr.tile([P, len(srcs), P], BF16, name="tr_bank")
             for n, src in enumerate(srcs):
                 nc.tensor.transpose(bank[:, n, :], src, id_bf[:])
 
@@ -197,24 +194,31 @@ def tile_gatedattentionunit_pb_w4_kernel(tc, q, k, u, v_bytes, v_scale, W_o_word
         def finish(j, d0=0, d1=D):
             nc.vector.tensor_tensor(out=o_sb[j][:, d0:d1], in0=banks["o", j][:, d0:d1], in1=b_bc[:, d0:d1], op=ALU.add)
 
-        def interleave_low():
-            dst = v_il[1][1][:, : KP // 4].rearrange("p (c i) t -> p c t i", i=4)
-            src = v_bf[1][1][:, :, : KP // 4].rearrange("p t (c i) -> p c t i", i=4)
+        spare = {
+            (0, 0): v_il[1][0][:].rearrange("p c t -> p (c t)"),
+            (0, 2): v_il[0][1][:].rearrange("p c t -> p (c t)")[:, : 2 * P * T],
+            (1, 0): v_il[1][1][:].rearrange("p c t -> p (c t)")[:, : P * T],
+            (1, 1): gT[0][:].rearrange("p g n t -> p (g n t)")[:, : P * T],
+            (1, 2): u_sb[2][:],
+        }
+
+        def home(g, q0, q1):
+            start = max(s for (h, s) in spare if h == g and s <= q0)
+            return spare[g, start][:, (q0 - start) * P * T : (q1 - start) * P * T]
+
+        def weave_v(g, q0, q1):
+            dst = home(g, q0, q1).rearrange("p (c i t) -> p c t i", i=4, t=T)
+            src = v_bf[1][g][:, :, P * q0 : P * q1].rearrange("p t (c i) -> p c t i", i=4)
             nc.vector.tensor_copy(out=dst, in_=src)
 
-        def interleave_mid():
-            src = v_bf[1][1][:, :, KP // 4 : KP // 2].rearrange("p t c -> p c t")
-            nc.gpsimd.tensor_scalar(out=v_il[1][1][:, KP // 4 : KP // 2], in0=src, scalar1=1.0, scalar2=0.0, op0=ALU.mult, op1=ALU.add)
-
-        def interleave_high():
-            dst = u_sb[2][:].rearrange("p (c t) -> p c t", t=T)
-            src = v_bf[1][1][:, :, KP // 2 :].rearrange("p t c -> p c t")
+        def weave_g(g, q0, q1):
+            dst = home(g, q0, q1).rearrange("p (c t) -> p c t", t=T)
+            src = v_bf[1][g][:, :, P * q0 : P * q1].rearrange("p t c -> p c t")
             nc.gpsimd.tensor_scalar(out=dst, in0=src, scalar1=1.0, scalar2=0.0, op0=ALU.mult, op1=ALU.add)
 
-        def quant_half(h):
-            cols = slice(h * KP // 2, (h + 1) * KP // 2)
-            src = u_sb[2][:] if h else v_il[1][1][:, cols].rearrange("p c t -> p (c t)")
-            nc.vector.quantize_mx(out=v_c[1][1][:, cols].bitcast(FP8X4), scales=v_s[1][1][:, cols], in_=src)
+        def quant_part(g, q0, q1):
+            cols = slice(P * q0, P * q1)
+            nc.vector.quantize_mx(out=v_c[1][g][:, cols].bitcast(FP8X4), scales=v_s[1][g][:, cols], in_=home(g, q0, q1))
 
         def project_last(g):
             for c in range(D // P):
@@ -250,12 +254,13 @@ def tile_gatedattentionunit_pb_w4_kernel(tc, q, k, u, v_bytes, v_scale, W_o_word
             f, a = step[0], step[1:]
             if f is copy_turned:
                 return [(turn,) + a]
-            if f is interleave_low or f is interleave_high or f is interleave_mid:
-                return [("widen", 1, 1, t) for t in range(T)] + [(gate, 2, 1)] * (f is interleave_high)
-            if f is quant_half:
-                return [(interleave_high,)] if a[0] else [(interleave_low,), (interleave_mid,)]
-            if f is mix and a[0] >= NT and a[1] == 1:
-                return [(quant_attn, a[0]), (quant_half, 0), (quant_half, 1)]
+            if f is weave_v or f is weave_g:
+                after = {(0, 2): [(quant_v, 0, 1)], (0, 3): [(quant_v, 0, 1)], (1, 1): [("quantised", 0, 1)], (1, 2): [(gate, 2, 1)]}
+                return [("widen", 1, a[0], t) for t in range(T)] + after.get(a[:2], [])
+            if f is quant_part:
+                return [("woven", a[0], n) for n in range(a[1], a[2])]
+            if f is mix and a[0] >= NT:
+                return [(quant_attn, a[0])] + [("coded", a[1], n) for n in range(T)]
             if f is interleave:
                 return [("widen",) + a + (t,) for t in range(T)]
             if f is quant_v:
@@ -289,7 +294,7 @@ def tile_gatedattentionunit_pb_w4_kernel(tc, q, k, u, v_bytes, v_scale, W_o_word
             if f is store:
                 return [(add_bias if a[0] in HELPED else finish,) + a]
             if f is add_bias:
-                return [(evacuate, a[0])] + [("quantised", 3, 1) if a[0] == 1 else (gate, 6, 1)]
+                return [(evacuate, a[0])] + [(gate, a[0] + 3, 1)]
             if f is finish or f is evacuate:
                 return [("projected", a[0])]
             return []
@@ -298,6 +303,10 @@ def tile_gatedattentionunit_pb_w4_kernel(tc, q, k, u, v_bytes, v_scale, W_o_word
             f, a = step[0], step[1:]
             if (f is relu or f is square) and a[1:] == (P // 2, P):
                 return [step, (f, a[0])]
+            if f is weave_v or f is weave_g:
+                return [("woven", a[0], n) for n in range(a[1], a[2])]
+            if f is quant_part:
+                return [("coded", a[0], n) for n in range(a[1], a[2])]
             if f is widen_v or f is widen_s:
                 return [("widen",) + a]
             if f is copy_gated:
@@ -311,7 +320,7 @@ def tile_gatedattentionunit_pb_w4_kernel(tc, q, k, u, v_bytes, v_scale, W_o_word
         def bank_of(step):
             f, a = step[0], step[1:]
             if f is turn:
-                return ("qk" if a[1] else "tr", 2, (copy_turned,) + a)
+                return ("tr", 2, (copy_turned,) + a)
             if f is turn_gated:
                 return ("tr", 2, (copy_gated,) + a)
             if f is scores:
@@ -355,8 +364,8 @@ def tile_gatedattentionunit_pb_w4_kernel(tc, q, k, u, v_bytes, v_scale, W_o_word
             load_kq(0)
             load_v(1, 0)
             load_v(1, 1)
-            load_u(0, 0)
             load_kq(1)
+            load_u(0, 0)
             load_w()
             load_u(0, 1)
             nc.sync.dma_start(out=b_bc[:], in_=b_o.partition_broadcast(P))
@@ -364,36 +373,36 @@ def tile_gatedattentionunit_pb_w4_kernel(tc, q, k, u, v_bytes, v_scale, W_o_word
             load_u(1, 1)
 
             vector = [(widen_v, 0, 0, t) for t in range(T)] + [(widen_v, 0, 1, 3)]
-            vector += [(interleave, 0, 0), (interleave, 0, 1), (quant_v, 0, 0), (quant_v, 0, 1)]
-            vector += [(widen_v, 1, 0, 3), (quant_attn, 0), (interleave, 1, 0)]
+            vector += [(interleave, 0, 0), (interleave, 0, 1), (quant_v, 0, 0), (widen_v, 1, 0, 2), (widen_v, 1, 0, 3)]
+            vector += [(quant_attn, 0), (quant_v, 0, 1), (weave_v, 0, 0, 2)]
+            blocks = [
+                [(quant_attn, 1), (widen_v, 1, 1, 2), (widen_v, 1, 1, 3), (quant_part, 0, 0, 2)],
+                [(quant_attn, 2), (weave_v, 0, 3, 4), (quant_gated, 0, 0, G), (quant_part, 0, 2, 4)],
+                [(quant_attn, 3), (quant_gated, 1, 0, G), (finish, 0)],
+                [(quant_attn, 4), (quant_part, 1, 0, 1), (quant_part, 1, 1, 2), (quant_part, 1, 2, 4), (quant_gated, 2, 0, G), (quant_attn, 5)],
+                [(quant_gated, 3, 0, G)],
+                [(finish, 2), (quant_gated, 4, 0, G), (quant_attn, 7)],
+                [(quant_gated, 5, 0, G), (finish, 4)],
+                [(quant_gated, 6, 0, G), (finish, 5)],
+            ]
             for j in range(TILES):
-                vector += [(gate, j, 0)] + [(quant_attn, j + 1)] * (j < NT - 2) + [(gate, j, 1)] + [(quant_attn, j + 1)] * (j == NT - 2)
-                if j == NT - 1:
-                    vector += [(interleave_low,), (quant_attn, NT), (quant_half, 1), (quant_half, 0), (quant_gated, j - 1, 0, G), (quant_attn, NT + 1)]
-                    continue
-                vector += [(finish, 2)] * (j == 5) + [(quant_attn, 6)] * (j == 4) + [(widen_v, 1, 1, 2), (widen_v, 1, 1, 3)] * (j == 1)
-                if j >= 1:
-                    vector += [(quant_gated, j - 1, 0, G)]
-                vector += [(quant_attn, 7)] * (j == 5)
-                if j >= 2 and j - 2 not in HELPED and j != 4:
-                    vector += [(finish, j - 2)]
-                vector += [(quant_v, 1, 0)] * (j == 0)
+                vector += [(gate, j, 0)] + [(quant_attn, 6)] * (j == 4) + [(gate, j, 1)] + blocks[j]
             vector += [(quant_gated, last, 0, 1), (quant_gated, last, 1, G), (finish, last - 1, 0, D // 2), (finish, last - 1, D // 2, D)] + [(finish_last, c) for c in range(D // P)]
 
             scalar = [(widen_s, 0, 1, t) for t in range(3)] + [(copy_turned, "k", 0), (copy_turned, "q", 0)]
             scalar += [(widen_s, 1, 0, 0), (widen_s, 1, 0, 1), (relu, 0, 0, P // 2), (relu, 0, P // 2, P), (square, 0, 0, P // 2), (square, 0, P // 2, P)]
-            scalar += [(widen_s, 1, 0, 2), (relu, 1), (widen_s, 1, 1, 0), (square, 1), (relu, 2), (widen_s, 1, 1, 1), (square, 2)]
-            scalar += [(relu, 3), (copy_gated, 0, 0, G), (square, 3), (copy_turned, "k", 1), (copy_gated, 1, 0, G), (copy_turned, "q", 1), (relu, 4), (relu, 5), (square, 4), (copy_gated, 2, 0, G)]
-            scalar += [(square, 5), (relu, 6), (copy_gated, 3, 0, G), (square, 6), (evacuate, 1), (relu, 7)]
+            scalar += [(widen_s, 1, 1, 0), (relu, 1), (widen_s, 1, 1, 1), (square, 1), (relu, 2), (copy_turned, "k", 1), (relu, 3), (copy_turned, "q", 1), (square, 2)]
+            scalar += [(copy_gated, 0, 0, G), (square, 3), (copy_gated, 1, 0, G), (relu, 4), (relu, 5), (square, 4), (square, 5), (copy_gated, 2, 0, G)]
+            scalar += [(relu, 6), (square, 6), (copy_gated, 3, 0, G), (evacuate, 1), (relu, 7)]
             scalar += [(copy_gated, 4, 0, G), (square, 7), (copy_gated, 5, 0, G), (evacuate, 3), (copy_gated, 6, 0, G)]
             scalar += [(copy_gated, last, 0, 1), (copy_gated, last, 1, G)]
 
-            tensor = [(turn, "k", 0), (turn, "q", 0), (scores, 0), (scores, 1), (scores, 2), (mix, 0, 0), (mix, 0, 1), (scores, 3)]
-            tensor += [(mix, 1, 0), (mix, 1, 1), (turn_gated, 0, 0, G), (turn, "k", 1), (mix, 2, 0), (mix, 2, 1), (turn_gated, 1, 0, G), (turn, "q", 1), (scores, 4), (project, 0, 0, G), (scores, 5)]
-            tensor += [(mix, 3, 0), (mix, 3, 1), (turn_gated, 2, 0, G), (scores, 6), (project, 1, 0, G), (turn_gated, 3, 0, G), (scores, 7)]
-            tensor += [(mix, 4, 0), (mix, 4, 1), (mix, 5, 0), (mix, 5, 1), (turn_gated, 4, 0, G), (project, 2, 0, G), (mix, 6, 0), (mix, 6, 1), (turn_gated, 5, 0, G), (project, 3, 0, G)]
+            tensor = [(turn, "k", 0), (turn, "q", 0), (scores, 0), (scores, 1), (turn, "k", 1), (turn, "q", 1), (scores, 2), (mix, 0, 0), (mix, 0, 1), (scores, 3)]
+            tensor += [(mix, 1, 0), (mix, 1, 1), (turn_gated, 0, 0, G), (scores, 4), (scores, 5), (turn_gated, 1, 0, G), (mix, 2, 0), (mix, 2, 1), (project, 0, 0, G), (mix, 3, 0), (mix, 3, 1)]
+            tensor += [(turn_gated, 2, 0, G), (scores, 6), (project, 1, 0, G), (turn_gated, 3, 0, G)]
+            tensor += [(mix, 4, 0), (mix, 4, 1), (scores, 7), (mix, 5, 0), (mix, 5, 1), (turn_gated, 4, 0, G), (project, 2, 0, G), (mix, 6, 0), (mix, 6, 1), (turn_gated, 5, 0, G), (project, 3, 0, G)]
             tensor += [(project, 4, 0, G), (mix, 7, 0), (mix, 7, 1), (turn_gated, 6, 0, G), (project, 5, 0, G)]
             tensor += [(turn_gated, last, 0, 1), (turn_gated, last, 1, G), (project, last - 1, 0, G), (project_last, 0), (project_last, 1)]
-            gpsimd = [(interleave_mid,), (interleave_high,)] + [(add_bias, j) for j in HELPED]
+            gpsimd = [(weave_g, 0, 2, 3), (weave_g, 1, 0, 1), (weave_g, 1, 1, 2), (weave_g, 1, 2, 4)] + [(add_bias, j) for j in HELPED]
             sync = [(store, j) for j in (0, 1, 2, 4, 3, 5)] + [(store, j, d, d + D // 2) for j in (last - 1, last) for d in (0, D // 2)]
             issue([tensor, scalar, gpsimd, vector, sync])

@@ -22,9 +22,11 @@ P = 128
 T = 4
 NT = N // P
 TILES = B * NT
+LAST = TILES - 1
 KP = P * T
 G = H // KP
 HELPED = (1, 3)
+HELP_LAG = 3
 QK_SCALE = 1.0 / math.sqrt(S)
 
 
@@ -68,20 +70,31 @@ def tile_gatedattentionunit_pb_w4_kernel(tc, q, k, u, v_bytes, v_scale, W_o_word
         id_f = kt([P, P], F32, "id_f")
 
         banks = {}
-        summed = {1: u_sb[4][:].bitcast(F32), 3: u_sb[6][:].bitcast(F32)}
+        result = {j: u_sb[j + HELP_LAG][:].bitcast(F32) if j in HELPED else o_sb[j][:] for j in range(TILES)}
+        woven = {
+            (0, 0): v_il[1][0][:].rearrange("p c t -> p (c t)"),
+            (0, 2): v_il[0][1][:].rearrange("p c t -> p (c t)"),
+            (1, 0): v_il[1][1][:].rearrange("p c t -> p (c t)"),
+            (1, 1): gT[0][:].rearrange("p g n t -> p (g n t)"),
+            (1, 2): u_sb[2][:],
+        }
+
+        def quarters(g, q0, q1):
+            first = max(s for (h, s) in woven if h == g and s <= q0)
+            return woven[g, first][:, (q0 - first) * P * T : (q1 - first) * P * T]
 
         def load_kq(b):
             nc.sync.dma_start(out=k_sb[b][:], in_=k[b].rearrange("(p t) s -> p t s", t=T))
             nc.sync.dma_start(out=q_sb[b][:], in_=q[b].rearrange("(p i) s -> p i s", i=NT))
 
-        def load_v(b, c):
+        def load_v(b):
             rows = v_bytes[b].rearrange("(p t) h -> p t h", t=T)
-            nc.sync.dma_start(out=vb[b][c][:], in_=rows[:, 2 * c : 2 * c + 2, :])
+            for c in range(2):
+                nc.sync.dma_start(out=vb[b][c][:], in_=rows[:, 2 * c : 2 * c + 2, :])
 
-        def load_u(b, c):
-            rows = u[b].rearrange("(p i) h -> p i h", i=NT)
-            for i in (2 * c, 2 * c + 1):
-                nc.sync.dma_start(out=u_sb[NT * b + i][:], in_=rows[:, i, :])
+        def load_u(j0, j1):
+            for j in range(j0, j1):
+                nc.sync.dma_start(out=u_sb[j][:], in_=u[j // NT].rearrange("(p i) h -> p i h", i=NT)[:, j % NT, :])
 
         def load_w():
             nc.sync.dma_start(out=w_sb[:], in_=W_o_words.rearrange("g p n -> p g n"))
@@ -90,40 +103,56 @@ def tile_gatedattentionunit_pb_w4_kernel(tc, q, k, u, v_bytes, v_scale, W_o_word
             for r in range(4):
                 nc.sync.dma_start(out=ws_i[r:P:32, :, :], in_=rows[r])
 
-        def turn(name, b):
-            if name == "k":
-                srcs = [k_sb[b][:, t, :] for t in range(T)] + [q_sb[b][:, 0, :]]
-            else:
-                srcs = [q_sb[b][:, i, :] for i in range(1, NT)]
-            bank = banks[name, b] = ps_tr.tile([P, len(srcs), P], BF16, name="tr_bank")
+        def turn(name, srcs):
+            bank = banks[name] = ps_tr.tile([P, len(srcs), P], BF16, name="tr_bank")
             for n, src in enumerate(srcs):
                 nc.tensor.transpose(bank[:, n, :], src, id_bf[:])
 
-        def copy_turned(name, b):
-            nc.scalar.copy(out={"k": kqT, "q": qT}[name][b][:], in_=banks[name, b][:])
+        def turn_kq(b):
+            turn(("kq", b), [k_sb[b][:, t, :] for t in range(T)] + [q_sb[b][:, 0, :]])
+            turn(("q", b), [q_sb[b][:, i, :] for i in range(1, NT)])
 
-        def widen_v(b, g, t):
+        def copy_kq(b):
+            nc.scalar.copy(out=kqT[b][:], in_=banks["kq", b][:])
+
+        def copy_q(b):
+            nc.scalar.copy(out=qT[b][:], in_=banks["q", b][:])
+
+        def widen_on_vector(b, g, t):
             src = vb[b][t // 2][:, t % 2, KP * g : KP * (g + 1)].bitcast(FP8)
             nc.vector.tensor_scalar(out=v_bf[b][g][:, t, :], in0=src, scalar1=vs[:, t : t + 1], scalar2=None, op0=ALU.mult)
 
-        def widen_s(b, g, t):
+        def widen_on_scalar(b, g, t):
             src = vb[b][t // 2][:, t % 2, KP * g : KP * (g + 1)].bitcast(FP8)
             nc.scalar.activation(v_bf[b][g][:, t, :], src, ACT.Copy, scale=vs[:, t : t + 1])
 
-        def interleave(b, g):
-            dst = v_il[b][g][:].rearrange("p (c i) t -> p c t i", i=4)
-            src = v_bf[b][g][:].rearrange("p t (c i) -> p c t i", i=4)
-            nc.vector.tensor_copy(out=dst, in_=src)
+        def weave(dst, src):
+            nc.vector.tensor_copy(out=dst.rearrange("p (c i t) -> p c t i", i=4, t=T), in_=src.rearrange("p t (c i) -> p c t i", i=4))
 
-        def quant_v(b, g):
-            nc.vector.quantize_mx(out=v_c[b][g][:].bitcast(FP8X4), scales=v_s[b][g][:], in_=v_il[b][g][:].rearrange("p c t -> p (c t)"))
+        def weave_first(g):
+            weave(v_il[0][g][:].rearrange("p c t -> p (c t)"), v_bf[0][g][:])
+
+        def quant_first(g):
+            nc.vector.quantize_mx(out=v_c[0][g][:].bitcast(FP8X4), scales=v_s[0][g][:], in_=v_il[0][g][:].rearrange("p c t -> p (c t)"))
+
+        def weave_second(g, q0, q1):
+            weave(quarters(g, q0, q1), v_bf[1][g][:, :, P * q0 : P * q1])
+
+        def weave_second_on_gpsimd(g, q0, q1):
+            dst = quarters(g, q0, q1).rearrange("p (c t) -> p c t", t=T)
+            src = v_bf[1][g][:, :, P * q0 : P * q1].rearrange("p t c -> p c t")
+            nc.gpsimd.tensor_scalar(out=dst, in0=src, scalar1=1.0, scalar2=0.0, op0=ALU.mult, op1=ALU.add)
+
+        def quant_second(g, q0, q1):
+            cols = slice(P * q0, P * q1)
+            nc.vector.quantize_mx(out=v_c[1][g][:, cols].bitcast(FP8X4), scales=v_s[1][g][:, cols], in_=quarters(g, q0, q1))
 
         def scores(j):
             b, i = divmod(j, NT)
             bank = banks["qk", j] = ps_qk.tile([P, T, P], F32, name="qk_bank")
+            queries = kqT[b][:, T, :] if i == 0 else qT[b][:, i - 1, :]
             for t in range(T):
-                rhs = kqT[b][:, T, :] if i == 0 else qT[b][:, i - 1, :]
-                nc.tensor.matmul(bank[:, t, :], lhsT=kqT[b][:, t, :], rhs=rhs, start=True, stop=True)
+                nc.tensor.matmul(bank[:, t, :], lhsT=kqT[b][:, t, :], rhs=queries, start=True, stop=True)
 
         def relu(j, n0=0, n1=P):
             nc.scalar.activation(r_sb[j][:, n0:n1], banks["qk", j][:, :, n0:n1].rearrange("p t n -> p n t"), ACT.Relu)
@@ -152,206 +181,66 @@ def tile_gatedattentionunit_pb_w4_kernel(tc, q, k, u, v_bytes, v_scale, W_o_word
             gate_in = u_sb[j][:, KP * g : KP * (g + 1)].rearrange("n (p w e) -> n w p e", w=2, e=2)
             nc.vector.tensor_tensor(out=gt[j][g][:].rearrange("n (w p e) -> n w p e", w=2, e=2), in0=av, in1=gate_in, op=ALU.mult)
 
-        def turn_gated(j, g0, g1):
+        def turn_gated(j, g0=0, g1=G):
             bank = banks["tg", j, g0] = ps_tr.tile([P, g1 - g0, 2, P], F32, name="tr_bank")
             for g in range(g0, g1):
                 words = gt[j][g][:].bitcast(F32)
                 for w in range(2):
                     nc.tensor.transpose(bank[:, g - g0, w, :], words[:, P * w : P * (w + 1)], id_f[:])
 
-        def copy_gated(j, g0, g1):
+        def copy_gated(j, g0=0, g1=G):
             nc.scalar.copy(out=gT[j][:, g0:g1].bitcast(F32), in_=banks["tg", j, g0][:].rearrange("p g w n -> p g n w"))
 
-        def quant_gated(j, g0, g1):
+        def quant_gated(j, g0=0, g1=G):
             nc.vector.quantize_mx(
                 out=gc[j][:, g0:g1].rearrange("p g n -> p (g n)").bitcast(FP8X4),
                 scales=gs[j][:, g0:g1].rearrange("p g n -> p (g n)"),
                 in_=gT[j][:, g0:g1].rearrange("p g n t -> p (g n t)"),
             )
 
-        def project(j, g0, g1):
-            if g0 == 0:
-                if j < NT - 1:
-                    banks["o", j] = ps_o.tile([P, D], F32, name="o_bank")
-                else:
-                    banks["o", j] = ps_qk.tile([P, D], F32, name="qk_bank")
-            for g in range(g0, g1):
-                nc.tensor.matmul_mx(
-                    out=banks["o", j][:],
-                    lhsT=gc[j][:, g, :].bitcast(FP8X4),
-                    lhsT_scale=gs[j][:, g, :],
-                    rhs=w_sb[:, g, :].bitcast(FP4X4),
-                    rhs_scale=ws_sb[:, g, :],
-                    start=(g == 0),
-                    stop=(g == G - 1),
-                )
+        def project_pass(bank, j, g, d0, d1):
+            nc.tensor.matmul_mx(
+                out=bank[:],
+                lhsT=gc[j][:, g, :].bitcast(FP8X4),
+                lhsT_scale=gs[j][:, g, :],
+                rhs=w_sb[:, g, 2 * d0 : 2 * d1].bitcast(FP4X4),
+                rhs_scale=ws_sb[:, g, d0:d1],
+                start=(g == 0),
+                stop=(g == G - 1),
+            )
 
-        def store(j, d0=0, d1=D):
-            b, i = divmod(j, NT)
-            src = summed[j] if j in HELPED else o_sb[j][:]
-            nc.sync.dma_start(out=out[b].rearrange("(p i) d -> p i d", i=NT)[:, i, d0:d1], in_=src[:, d0:d1])
-
-        def finish(j, d0=0, d1=D):
-            nc.vector.tensor_tensor(out=o_sb[j][:, d0:d1], in0=banks["o", j][:, d0:d1], in1=b_bc[:, d0:d1], op=ALU.add)
-
-        spare = {
-            (0, 0): v_il[1][0][:].rearrange("p c t -> p (c t)"),
-            (0, 2): v_il[0][1][:].rearrange("p c t -> p (c t)")[:, : 2 * P * T],
-            (1, 0): v_il[1][1][:].rearrange("p c t -> p (c t)")[:, : P * T],
-            (1, 1): gT[0][:].rearrange("p g n t -> p (g n t)")[:, : P * T],
-            (1, 2): u_sb[2][:],
-        }
-
-        def home(g, q0, q1):
-            start = max(s for (h, s) in spare if h == g and s <= q0)
-            return spare[g, start][:, (q0 - start) * P * T : (q1 - start) * P * T]
-
-        def weave_v(g, q0, q1):
-            dst = home(g, q0, q1).rearrange("p (c i t) -> p c t i", i=4, t=T)
-            src = v_bf[1][g][:, :, P * q0 : P * q1].rearrange("p t (c i) -> p c t i", i=4)
-            nc.vector.tensor_copy(out=dst, in_=src)
-
-        def weave_g(g, q0, q1):
-            dst = home(g, q0, q1).rearrange("p (c t) -> p c t", t=T)
-            src = v_bf[1][g][:, :, P * q0 : P * q1].rearrange("p t c -> p c t")
-            nc.gpsimd.tensor_scalar(out=dst, in0=src, scalar1=1.0, scalar2=0.0, op0=ALU.mult, op1=ALU.add)
-
-        def quant_part(g, q0, q1):
-            cols = slice(P * q0, P * q1)
-            nc.vector.quantize_mx(out=v_c[1][g][:, cols].bitcast(FP8X4), scales=v_s[1][g][:, cols], in_=home(g, q0, q1))
+        def project(j):
+            if j < 2 or j == LAST - 1:
+                banks["o", j] = ps_o.tile([P, D], F32, name="o_bank")
+            else:
+                banks["o", j] = ps_qk.tile([P, D], F32, name="qk_bank")
+            for g in range(G):
+                project_pass(banks["o", j], j, g, 0, D)
 
         def project_last(g):
             for c in range(D // P):
-                if g == 0:
-                    if c < 3:
-                        banks["last", c] = ps_av.tile([P, P], F32, name="av_bank")
-                    else:
-                        banks["last", c] = ps_o.tile([P, P], F32, name="o_bank")
-                nc.tensor.matmul_mx(
-                    out=banks["last", c][:],
-                    lhsT=gc[last][:, g, :].bitcast(FP8X4),
-                    lhsT_scale=gs[last][:, g, :],
-                    rhs=w_sb[:, g, 2 * P * c : 2 * P * (c + 1)].bitcast(FP4X4),
-                    rhs_scale=ws_sb[:, g, P * c : P * (c + 1)],
-                    start=(g == 0),
-                    stop=(g == G - 1),
-                )
+                if g == 0 and c < D // P - 1:
+                    banks["last", c] = ps_av.tile([P, P], F32, name="av_bank")
+                elif g == 0:
+                    banks["last", c] = ps_qk.tile([P, P], F32, name="qk_bank")
+                project_pass(banks["last", c], LAST, g, P * c, P * (c + 1))
 
-        def finish_last(c):
-            cols = slice(P * c, P * (c + 1))
-            nc.vector.tensor_tensor(out=o_sb[last][:, cols], in0=banks["last", c][:], in1=b_bc[:, cols], op=ALU.add)
+        def add_bias(bank, j, d0=0, d1=D):
+            nc.vector.tensor_tensor(out=result[j][:, d0:d1], in0=bank, in1=b_bc[:, d0:d1], op=ALU.add)
 
         def evacuate(j):
             nc.scalar.copy(out=o_raw[j][:], in_=banks["o", j][:])
 
-        def add_bias(j):
-            nc.gpsimd.tensor_tensor(out=summed[j], in0=o_raw[j][:], in1=b_bc[:], op=ALU.add)
+        def add_bias_on_gpsimd(j):
+            nc.gpsimd.tensor_tensor(out=result[j], in0=o_raw[j][:], in1=b_bc[:], op=ALU.add)
 
+        def store(j, d0=0, d1=D):
+            b, i = divmod(j, NT)
+            nc.sync.dma_start(out=out[b].rearrange("(p i) d -> p i d", i=NT)[:, i, d0:d1], in_=result[j][:, d0:d1])
 
-        last = TILES - 1
-
-        def needs(step):
-            f, a = step[0], step[1:]
-            if f is copy_turned:
-                return [(turn,) + a]
-            if f is weave_v or f is weave_g:
-                after = {(0, 2): [(quant_v, 0, 1)], (0, 3): [(quant_v, 0, 1)], (1, 1): [("quantised", 0, 1)], (1, 2): [(gate, 2, 1)]}
-                return [("widen", 1, a[0], t) for t in range(T)] + after.get(a[:2], [])
-            if f is quant_part:
-                return [("woven", a[0], n) for n in range(a[1], a[2])]
-            if f is mix and a[0] >= NT:
-                return [(quant_attn, a[0])] + [("coded", a[1], n) for n in range(T)]
-            if f is interleave:
-                return [("widen",) + a + (t,) for t in range(T)]
-            if f is quant_v:
-                return [(interleave,) + a]
-            if f is scores:
-                return [(copy_turned, "k", a[0] // NT)] + [(copy_turned, "q", a[0] // NT)] * (a[0] % NT > 0)
-            if f is relu:
-                return [(scores, a[0])]
-            if f is square:
-                return [(relu,) + a]
-            if f is quant_attn:
-                return [(square,) + a]
-            if f is mix:
-                return [(quant_attn, a[0]), (quant_v, a[0] // NT, a[1])]
-            if f is gate:
-                return [(mix,) + a]
-            if f is turn_gated:
-                return [(gate, a[0], g) for g in range(a[1], a[2])]
-            if f is copy_gated:
-                return [(turn_gated,) + a]
-            if f is quant_gated:
-                return [("copied", a[0], g) for g in range(a[1], a[2])]
-            if f is project:
-                return [("quantised", a[0], g) for g in range(a[1], a[2])]
-            if f is project_last:
-                return [("quantised", last, a[0])]
-            if f is finish_last:
-                return [(project_last, 1)]
-            if f is store and a[0] == last:
-                return [(finish_last, a[2] // P - 1)]
-            if f is store:
-                return [(add_bias if a[0] in HELPED else finish,) + a]
-            if f is add_bias:
-                return [(evacuate, a[0])] + [(gate, a[0] + 3, 1)]
-            if f is finish or f is evacuate:
-                return [("projected", a[0])]
-            return []
-
-        def gives(step):
-            f, a = step[0], step[1:]
-            if (f is relu or f is square) and a[1:] == (P // 2, P):
-                return [step, (f, a[0])]
-            if f is weave_v or f is weave_g:
-                return [("woven", a[0], n) for n in range(a[1], a[2])]
-            if f is quant_part:
-                return [("coded", a[0], n) for n in range(a[1], a[2])]
-            if f is widen_v or f is widen_s:
-                return [("widen",) + a]
-            if f is copy_gated:
-                return [step] + [("copied", a[0], g) for g in range(a[1], a[2])]
-            if f is quant_gated:
-                return [("quantised", a[0], g) for g in range(a[1], a[2])]
-            if f is project and a[2] == G:
-                return [("projected", a[0])]
-            return [step]
-
-        def bank_of(step):
-            f, a = step[0], step[1:]
-            if f is turn:
-                return ("tr", 2, (copy_turned,) + a)
-            if f is turn_gated:
-                return ("tr", 2, (copy_gated,) + a)
-            if f is scores:
-                return ("qk", 2, (relu,) + a)
-            if f is mix:
-                return ("av", 3, (gate,) + a)
-            if f is project and a[1] == 0:
-                reader = (evacuate if a[0] in HELPED else finish, a[0])
-                return ("o", 1, reader) if a[0] < NT - 1 else ("qk", 2, reader)
-            return None
-
-        def issue(queues):
-            done, taken = set(), {}
-            heads = [0] * len(queues)
-            for sweep in range(sum(len(x) for x in queues)):
-                for e, queue in enumerate(queues):
-                    if heads[e] == len(queue):
-                        continue
-                    step = queue[heads[e]]
-                    wait = needs(step)
-                    bank = bank_of(step)
-                    if bank and len(taken.get(bank[0], [])) >= bank[1]:
-                        wait = wait + [taken[bank[0]][-bank[1]]]
-                    if all(w in done for w in wait):
-                        step[0](*step[1:])
-                        for w in gives(step):
-                            done.add(w)
-                        if bank:
-                            taken.setdefault(bank[0], []).append(bank[2])
-                        heads[e] = heads[e] + 1
-            assert heads == [len(x) for x in queues], [x[h] for x, h in zip(queues, heads) if h < len(x)]
+        def finish(j, d0=0, d1=D):
+            add_bias(banks["o", j][:, d0:d1], j, d0, d1)
+            store(j, d0, d1)
 
         make_identity(nc, id_bf[:])
         with tc.manual_schedule():
@@ -359,50 +248,148 @@ def tile_gatedattentionunit_pb_w4_kernel(tc, q, k, u, v_bytes, v_scale, W_o_word
             nc.scalar.activation(id_f[:], id_bf[:], ACT.Copy)
 
             nc.sync.dma_start(out=vs[:], in_=v_scale.rearrange("o (p t) x -> p (o t x)", t=T))
-            load_v(0, 0)
-            load_v(0, 1)
-            load_kq(0)
-            load_v(1, 0)
-            load_v(1, 1)
-            load_kq(1)
-            load_u(0, 0)
+            for b in range(B):
+                load_v(b)
+                load_kq(b)
+            load_u(0, 2)
             load_w()
-            load_u(0, 1)
+            load_u(2, NT)
             nc.sync.dma_start(out=b_bc[:], in_=b_o.partition_broadcast(P))
-            load_u(1, 0)
-            load_u(1, 1)
+            load_u(NT, TILES)
 
-            vector = [(widen_v, 0, 0, t) for t in range(T)] + [(widen_v, 0, 1, 3)]
-            vector += [(interleave, 0, 0), (interleave, 0, 1), (quant_v, 0, 0), (widen_v, 1, 0, 2), (widen_v, 1, 0, 3)]
-            vector += [(quant_attn, 0), (quant_v, 0, 1), (weave_v, 0, 0, 2)]
-            blocks = [
-                [(quant_attn, 1), (widen_v, 1, 1, 2), (widen_v, 1, 1, 3), (quant_part, 0, 0, 2)],
-                [(quant_attn, 2), (weave_v, 0, 3, 4), (quant_gated, 0, 0, G), (quant_part, 0, 2, 4)],
-                [(quant_attn, 3), (quant_gated, 1, 0, G), (finish, 0)],
-                [(quant_attn, 4), (quant_part, 1, 0, 1), (quant_part, 1, 1, 2), (quant_part, 1, 2, 4), (quant_gated, 2, 0, G), (quant_attn, 5)],
-                [(quant_gated, 3, 0, G)],
-                [(finish, 2), (quant_gated, 4, 0, G), (quant_attn, 7)],
-                [(quant_gated, 5, 0, G), (finish, 4)],
-                [(quant_gated, 6, 0, G), (finish, 5)],
-            ]
-            for j in range(TILES):
-                vector += [(gate, j, 0)] + [(quant_attn, 6)] * (j == 4) + [(gate, j, 1)] + blocks[j]
-            vector += [(quant_gated, last, 0, 1), (quant_gated, last, 1, G), (finish, last - 1, 0, D // 2), (finish, last - 1, D // 2, D)] + [(finish_last, c) for c in range(D // P)]
+            for t in range(T):
+                widen_on_vector(0, 0, t)
+            for t in range(T - 1):
+                widen_on_scalar(0, 1, t)
+            widen_on_vector(0, 1, T - 1)
+            turn_kq(0)
+            copy_kq(0)
+            copy_q(0)
+            scores(0)
+            scores(1)
+            turn_kq(1)
+            weave_first(0)
+            weave_first(1)
+            quant_first(0)
+            for t in range(2):
+                widen_on_scalar(1, 0, t)
+            for step in (relu, square):
+                step(0, 0, P // 2)
+                step(0, P // 2, P)
+            scores(2)
+            for t in range(2, T):
+                widen_on_vector(1, 0, t)
+            quant_attn(0)
+            mix(0, 0)
+            quant_first(1)
+            mix(0, 1)
+            weave_second(0, 0, 2)
+            weave_second_on_gpsimd(0, 2, 3)
+            widen_on_scalar(1, 1, 0)
+            relu(1)
+            scores(3)
+            widen_on_scalar(1, 1, 1)
+            square(1)
+            relu(2)
+            copy_kq(1)
+            relu(3)
+            copy_q(1)
+            square(2)
 
-            scalar = [(widen_s, 0, 1, t) for t in range(3)] + [(copy_turned, "k", 0), (copy_turned, "q", 0)]
-            scalar += [(widen_s, 1, 0, 0), (widen_s, 1, 0, 1), (relu, 0, 0, P // 2), (relu, 0, P // 2, P), (square, 0, 0, P // 2), (square, 0, P // 2, P)]
-            scalar += [(widen_s, 1, 1, 0), (relu, 1), (widen_s, 1, 1, 1), (square, 1), (relu, 2), (copy_turned, "k", 1), (relu, 3), (copy_turned, "q", 1), (square, 2)]
-            scalar += [(copy_gated, 0, 0, G), (square, 3), (copy_gated, 1, 0, G), (relu, 4), (relu, 5), (square, 4), (square, 5), (copy_gated, 2, 0, G)]
-            scalar += [(relu, 6), (square, 6), (copy_gated, 3, 0, G), (evacuate, 1), (relu, 7)]
-            scalar += [(copy_gated, 4, 0, G), (square, 7), (copy_gated, 5, 0, G), (evacuate, 3), (copy_gated, 6, 0, G)]
-            scalar += [(copy_gated, last, 0, 1), (copy_gated, last, 1, G)]
+            for j in range(NT):
+                gate(j, 0)
+                gate(j, 1)
+                if j == 2:
+                    weave_second_on_gpsimd(1, 2, 4)
+                if j % 2 == 1:
+                    turn_gated(j)
+                quant_attn(j + 1)
+                if j == NT - 1:
+                    quant_second(1, 0, 1)
+                    quant_second(1, 1, 2)
+                    quant_second(1, 2, 4)
+                mix(j + 1, 0)
+                mix(j + 1, 1)
+                if j % 2 == 0:
+                    turn_gated(j)
+                copy_gated(j)
+                if j == 0:
+                    widen_on_vector(1, 1, 2)
+                    widen_on_vector(1, 1, 3)
+                    weave_second_on_gpsimd(1, 0, 1)
+                    quant_second(0, 0, 2)
+                    scores(4)
+                    scores(5)
+                    square(3)
+                elif j == 1:
+                    weave_second(0, 3, 4)
+                    quant_gated(0)
+                    weave_second_on_gpsimd(1, 1, 2)
+                    quant_second(0, 2, 4)
+                    project(0)
+                    for step in (relu, square):
+                        step(4)
+                        step(5)
+                    scores(6)
+                    relu(6)
+                elif j == 2:
+                    scores(7)
+                    quant_gated(1)
+                    finish(0)
+                    project(1)
+                    relu(7)
+                    square(6)
+                else:
+                    quant_gated(2)
+                    project(2)
+                    quant_attn(5)
+                    mix(5, 0)
+                    evacuate(1)
+                    square(7)
 
-            tensor = [(turn, "k", 0), (turn, "q", 0), (scores, 0), (scores, 1), (turn, "k", 1), (turn, "q", 1), (scores, 2), (mix, 0, 0), (mix, 0, 1), (scores, 3)]
-            tensor += [(mix, 1, 0), (mix, 1, 1), (turn_gated, 0, 0, G), (scores, 4), (scores, 5), (turn_gated, 1, 0, G), (mix, 2, 0), (mix, 2, 1), (project, 0, 0, G), (mix, 3, 0), (mix, 3, 1)]
-            tensor += [(turn_gated, 2, 0, G), (scores, 6), (project, 1, 0, G), (turn_gated, 3, 0, G)]
-            tensor += [(mix, 4, 0), (mix, 4, 1), (scores, 7), (mix, 5, 0), (mix, 5, 1), (turn_gated, 4, 0, G), (project, 2, 0, G), (mix, 6, 0), (mix, 6, 1), (turn_gated, 5, 0, G), (project, 3, 0, G)]
-            tensor += [(project, 4, 0, G), (mix, 7, 0), (mix, 7, 1), (turn_gated, 6, 0, G), (project, 5, 0, G)]
-            tensor += [(turn_gated, last, 0, 1), (turn_gated, last, 1, G), (project, last - 1, 0, G), (project_last, 0), (project_last, 1)]
-            gpsimd = [(weave_g, 0, 2, 3), (weave_g, 1, 0, 1), (weave_g, 1, 1, 2), (weave_g, 1, 2, 4)] + [(add_bias, j) for j in HELPED]
-            sync = [(store, j) for j in (0, 1, 2, 4, 3, 5)] + [(store, j, d, d + D // 2) for j in (last - 1, last) for d in (0, D // 2)]
-            issue([tensor, scalar, gpsimd, vector, sync])
+            for j in range(NT, LAST):
+                gate(j, 0)
+                mix(j + 1, 1)
+                if j == NT:
+                    quant_attn(j + 2)
+                gate(j, 1)
+                if j - HELP_LAG in HELPED:
+                    add_bias_on_gpsimd(j - HELP_LAG)
+                turn_gated(j)
+                copy_gated(j)
+                if j == NT:
+                    quant_gated(3)
+                    project(3)
+                    store(1)
+                    mix(6, 0)
+                    evacuate(3)
+                elif j == NT + 1:
+                    finish(2)
+                    quant_gated(4)
+                    quant_attn(7)
+                    project(4)
+                    mix(7, 0)
+                else:
+                    quant_gated(5)
+                    project(5)
+                    finish(4, 0, D // 2)
+                    store(3)
+
+            for g in range(G):
+                gate(LAST, g)
+                turn_gated(LAST, g, g + 1)
+                copy_gated(LAST, g, g + 1)
+            quant_gated(LAST - 1)
+            project(LAST - 1)
+            finish(LAST - 2)
+            quant_gated(LAST, 0, 1)
+            finish(4, D // 2, D)
+            project_last(0)
+            quant_gated(LAST, 1, G)
+            project_last(1)
+            for d in range(0, D, D // 2):
+                finish(LAST - 1, d, d + D // 2)
+            for c in range(D // P):
+                add_bias(banks["last", c][:], LAST, P * c, P * (c + 1))
+                if c % 2 == 1:
+                    store(LAST, P * (c - 1), P * (c + 1))

@@ -25,8 +25,8 @@ TILES = B * NT
 LAST = TILES - 1
 KP = P * T
 G = H // KP
-HELPED = (1, 3)
-HELP_LAG = 3
+HELPED = {1: 2, 2: 5, 3: 6}
+LASTN = 4
 QK_SCALE = 1.0 / math.sqrt(S)
 
 
@@ -70,7 +70,7 @@ def tile_gatedattentionunit_pb_w4_kernel(tc, q, k, u, v_bytes, v_scale, W_o_word
         id_f = kt([P, P], F32, "id_f")
 
         banks = {}
-        result = {j: u_sb[j + HELP_LAG][:].bitcast(F32) if j in HELPED else o_sb[j][:] for j in range(TILES)}
+        result = {j: u_sb[HELPED[j]][:].bitcast(F32) if j in HELPED else o_sb[j][:] for j in range(TILES)}
         woven = {
             (0, 0): v_il[1][0][:].rearrange("p c t -> p (c t)"),
             (0, 2): v_il[0][1][:].rearrange("p c t -> p (c t)"),
@@ -89,8 +89,11 @@ def tile_gatedattentionunit_pb_w4_kernel(tc, q, k, u, v_bytes, v_scale, W_o_word
 
         def load_v(b):
             rows = v_bytes[b].rearrange("(p t) h -> p t h", t=T)
-            for c in range(2):
-                nc.sync.dma_start(out=vb[b][c][:], in_=rows[:, 2 * c : 2 * c + 2, :])
+            for t in range(T):
+                if b == 0:
+                    nc.sync.dma_start(out=vb[b][t // 2][:, t % 2, :], in_=rows[:, t, :])
+                elif t % 2 == 0:
+                    nc.sync.dma_start(out=vb[b][t // 2][:], in_=rows[:, t : t + 2, :])
 
         def load_u(j0, j1):
             for j in range(j0, j1):
@@ -110,6 +113,8 @@ def tile_gatedattentionunit_pb_w4_kernel(tc, q, k, u, v_bytes, v_scale, W_o_word
 
         def turn_kq(b):
             turn(("kq", b), [k_sb[b][:, t, :] for t in range(T)] + [q_sb[b][:, 0, :]])
+
+        def turn_q(b):
             turn(("q", b), [q_sb[b][:, i, :] for i in range(1, NT)])
 
         def copy_kq(b):
@@ -209,45 +214,41 @@ def tile_gatedattentionunit_pb_w4_kernel(tc, q, k, u, v_bytes, v_scale, W_o_word
                 stop=(g == G - 1),
             )
 
-        def project(j):
-            if j < 2 or j == LAST - 1:
-                banks["o", j] = ps_o.tile([P, D], F32, name="o_bank")
-            else:
-                banks["o", j] = ps_qk.tile([P, D], F32, name="qk_bank")
+        def project(j, pool, name):
+            banks["o", j] = pool.tile([P, D], F32, name=name)
             for g in range(G):
                 project_pass(banks["o", j], j, g, 0, D)
 
         def project_last(g):
-            for c in range(D // P):
-                if g == 0 and c < D // P - 1:
-                    banks["last", c] = ps_av.tile([P, P], F32, name="av_bank")
-                elif g == 0:
-                    banks["last", c] = ps_qk.tile([P, P], F32, name="qk_bank")
-                project_pass(banks["last", c], LAST, g, P * c, P * (c + 1))
+            for c in range(LASTN):
+                if g == 0:
+                    pool, name = ((ps_av, "av_bank"), (ps_qk, "qk_bank"))[c // 3]
+                    banks["last", c] = pool.tile([P, D // LASTN], F32, name=name)
+                project_pass(banks["last", c], LAST, g, D // LASTN * c, D // LASTN * (c + 1))
 
-        def add_bias(bank, j, d0=0, d1=D):
-            nc.vector.tensor_tensor(out=result[j][:, d0:d1], in0=bank, in1=b_bc[:, d0:d1], op=ALU.add)
+        def add_bias(j, d0=0, d1=D):
+            nc.vector.tensor_tensor(out=result[j][:, d0:d1], in0=banks["o", j][:, d0:d1], in1=b_bc[:, d0:d1], op=ALU.add)
 
-        def evacuate(j):
-            nc.scalar.copy(out=o_raw[j][:], in_=banks["o", j][:])
+        def add_last(c):
+            cols = slice(D // LASTN * c, D // LASTN * (c + 1))
+            nc.vector.tensor_tensor(out=result[LAST][:, cols], in0=banks["last", c][:], in1=b_bc[:, cols], op=ALU.add)
 
-        def add_bias_on_gpsimd(j):
-            nc.gpsimd.tensor_tensor(out=result[j], in0=o_raw[j][:], in1=b_bc[:], op=ALU.add)
+        def evacuate(j, d0=0, d1=D):
+            nc.scalar.copy(out=o_raw[j][:, d0:d1], in_=banks["o", j][:, d0:d1])
+
+        def add_on_gpsimd(j, d0=0, d1=D):
+            nc.gpsimd.tensor_tensor(out=result[j][:, d0:d1], in0=o_raw[j][:, d0:d1], in1=b_bc[:, d0:d1], op=ALU.add)
 
         def store(j, d0=0, d1=D):
             b, i = divmod(j, NT)
             nc.sync.dma_start(out=out[b].rearrange("(p i) d -> p i d", i=NT)[:, i, d0:d1], in_=result[j][:, d0:d1])
 
-        def finish(j, d0=0, d1=D):
-            add_bias(banks["o", j][:, d0:d1], j, d0, d1)
-            store(j, d0, d1)
-
         make_identity(nc, id_bf[:])
         with tc.manual_schedule():
             nc.vector.memset(ws_sb[:].bitcast(I32), 0)
-            nc.scalar.activation(id_f[:], id_bf[:], ACT.Copy)
 
-            nc.sync.dma_start(out=vs[:], in_=v_scale.rearrange("o (p t) x -> p (o t x)", t=T))
+            nc.scalar.dma_start(out=vs[:], in_=v_scale.rearrange("o (p t) x -> p (o t x)", t=T))
+            nc.scalar.activation(id_f[:], id_bf[:], ACT.Copy)
             for b in range(B):
                 load_v(b)
                 load_kq(b)
@@ -257,139 +258,172 @@ def tile_gatedattentionunit_pb_w4_kernel(tc, q, k, u, v_bytes, v_scale, W_o_word
             nc.sync.dma_start(out=b_bc[:], in_=b_o.partition_broadcast(P))
             load_u(NT, TILES)
 
-            for t in range(T):
-                widen_on_vector(0, 0, t)
-            for t in range(T - 1):
-                widen_on_scalar(0, 1, t)
-            widen_on_vector(0, 1, T - 1)
+            widen_on_vector(0, 0, 0)
+            widen_on_scalar(0, 1, 0)
             turn_kq(0)
+            widen_on_vector(0, 0, 1)
+            widen_on_scalar(0, 1, 1)
+            turn_q(0)
+            widen_on_vector(0, 0, 2)
+            widen_on_scalar(0, 1, 2)
+            widen_on_vector(0, 0, 3)
             copy_kq(0)
-            copy_q(0)
             scores(0)
+            widen_on_vector(0, 1, 3)
+            copy_q(0)
             scores(1)
-            turn_kq(1)
             weave_first(0)
+            widen_on_scalar(1, 0, 0)
+            turn_kq(1)
             weave_first(1)
+            widen_on_scalar(1, 0, 1)
+            turn_q(1)
             quant_first(0)
-            for t in range(2):
-                widen_on_scalar(1, 0, t)
-            for step in (relu, square):
-                step(0, 0, P // 2)
-                step(0, P // 2, P)
+            relu(0, 0, P // 2)
+            widen_on_vector(1, 0, 2)
+            relu(0, P // 2, P)
             scores(2)
-            for t in range(2, T):
-                widen_on_vector(1, 0, t)
+            widen_on_vector(1, 0, 3)
+            square(0, 0, P // 2)
+            square(0, P // 2, P)
             quant_attn(0)
+            widen_on_scalar(1, 1, 0)
             mix(0, 0)
             quant_first(1)
-            mix(0, 1)
-            weave_second(0, 0, 2)
-            weave_second_on_gpsimd(0, 2, 3)
-            widen_on_scalar(1, 1, 0)
             relu(1)
-            scores(3)
+            mix(0, 1)
+            weave_second_on_gpsimd(0, 2, 3)
+            weave_second(0, 0, 2)
             widen_on_scalar(1, 1, 1)
+            scores(3)
+            gate(0, 0)
             square(1)
+            gate(0, 1)
             relu(2)
+            quant_attn(1)
             copy_kq(1)
+            mix(1, 0)
+            widen_on_vector(1, 1, 2)
             relu(3)
+            mix(1, 1)
+            widen_on_vector(1, 1, 3)
             copy_q(1)
+            turn_gated(0)
+            weave_second_on_gpsimd(1, 0, 1)
+            quant_second(0, 0, 2)
             square(2)
-
-            for j in range(NT):
-                gate(j, 0)
-                gate(j, 1)
-                if j == 2:
-                    weave_second_on_gpsimd(1, 2, 4)
-                if j % 2 == 1:
-                    turn_gated(j)
-                quant_attn(j + 1)
-                if j == NT - 1:
-                    quant_second(1, 0, 1)
-                    quant_second(1, 1, 2)
-                    quant_second(1, 2, 4)
-                mix(j + 1, 0)
-                mix(j + 1, 1)
-                if j % 2 == 0:
-                    turn_gated(j)
-                copy_gated(j)
-                if j == 0:
-                    widen_on_vector(1, 1, 2)
-                    widen_on_vector(1, 1, 3)
-                    weave_second_on_gpsimd(1, 0, 1)
-                    quant_second(0, 0, 2)
-                    scores(4)
-                    scores(5)
-                    square(3)
-                elif j == 1:
-                    weave_second(0, 3, 4)
-                    quant_gated(0)
-                    weave_second_on_gpsimd(1, 1, 2)
-                    quant_second(0, 2, 4)
-                    project(0)
-                    for step in (relu, square):
-                        step(4)
-                        step(5)
-                    scores(6)
-                    relu(6)
-                elif j == 2:
-                    scores(7)
-                    quant_gated(1)
-                    finish(0)
-                    project(1)
-                    relu(7)
-                    square(6)
-                else:
-                    quant_gated(2)
-                    project(2)
-                    quant_attn(5)
-                    mix(5, 0)
-                    evacuate(1)
-                    square(7)
-
-            for j in range(NT, LAST):
-                gate(j, 0)
-                mix(j + 1, 1)
-                if j == NT:
-                    quant_attn(j + 2)
-                gate(j, 1)
-                if j - HELP_LAG in HELPED:
-                    add_bias_on_gpsimd(j - HELP_LAG)
-                turn_gated(j)
-                copy_gated(j)
-                if j == NT:
-                    quant_gated(3)
-                    project(3)
-                    store(1)
-                    mix(6, 0)
-                    evacuate(3)
-                elif j == NT + 1:
-                    finish(2)
-                    quant_gated(4)
-                    quant_attn(7)
-                    project(4)
-                    mix(7, 0)
-                else:
-                    quant_gated(5)
-                    project(5)
-                    finish(4, 0, D // 2)
-                    store(3)
-
-            for g in range(G):
-                gate(LAST, g)
-                turn_gated(LAST, g, g + 1)
-                copy_gated(LAST, g, g + 1)
-            quant_gated(LAST - 1)
-            project(LAST - 1)
-            finish(LAST - 2)
-            quant_gated(LAST, 0, 1)
-            finish(4, D // 2, D)
+            scores(4)
+            gate(1, 0)
+            copy_gated(0)
+            scores(5)
+            gate(1, 1)
+            square(3)
+            turn_gated(1)
+            quant_attn(2)
+            copy_gated(1)
+            mix(2, 0)
+            weave_second(0, 3, 4)
+            relu(4)
+            mix(2, 1)
+            quant_gated(0)
+            relu(5)
+            project(0, ps_o, "o_bank")
+            weave_second_on_gpsimd(1, 1, 2)
+            quant_second(0, 2, 4)
+            square(4)
+            scores(6)
+            gate(2, 0)
+            square(5)
+            gate(2, 1)
+            relu(6)
+            weave_second_on_gpsimd(1, 2, 4)
+            quant_attn(3)
+            mix(3, 0)
+            quant_gated(1)
+            mix(3, 1)
+            add_bias(0)
+            turn_gated(2)
+            store(0)
+            gate(3, 0)
+            copy_gated(2)
+            project(1, ps_o, "o_bank")
+            gate(3, 1)
+            evacuate(1)
+            scores(7)
+            quant_attn(4)
+            square(6)
+            turn_gated(3)
+            quant_second(1, 0, 1)
+            copy_gated(3)
+            mix(4, 0)
+            quant_second(1, 1, 2)
+            relu(7)
+            quant_second(1, 2, 4)
+            mix(4, 1)
+            add_on_gpsimd(1)
+            store(1)
+            quant_attn(5)
+            mix(5, 0)
+            quant_gated(2)
+            project(2, ps_qk, "qk_bank")
+            gate(4, 0)
+            evacuate(2, 0, 256)
+            mix(5, 1)
+            gate(4, 1)
+            square(7)
+            turn_gated(4)
+            quant_gated(3)
+            copy_gated(4)
+            project(3, ps_o, "o_bank")
+            quant_attn(6)
+            evacuate(2, 256, 512)
+            mix(6, 0)
+            gate(5, 0)
+            evacuate(3)
+            mix(6, 1)
+            gate(5, 1)
+            turn_gated(5)
+            add_on_gpsimd(2)
+            store(2)
+            quant_attn(7)
+            copy_gated(5)
+            mix(7, 0)
+            quant_gated(4)
+            project(4, ps_qk, "qk_bank")
+            gate(6, 0)
+            mix(7, 1)
+            gate(6, 1)
+            turn_gated(6)
+            add_on_gpsimd(3)
+            quant_gated(5)
+            copy_gated(6)
+            project(5, ps_qk, "qk_bank")
+            add_bias(4, 0, 256)
+            store(4, 0, 256)
+            gate(7, 0)
+            turn_gated(7, 0, 1)
+            store(3)
+            gate(7, 1)
+            copy_gated(7, 0, 1)
+            turn_gated(7, 1, 2)
+            quant_gated(6)
+            copy_gated(7, 1, 2)
+            project(6, ps_o, "o_bank")
+            add_bias(5)
+            store(5)
+            quant_gated(7, 0, 1)
+            add_bias(4, 256, 512)
             project_last(0)
-            quant_gated(LAST, 1, G)
+            store(4, 256, 512)
+            quant_gated(7, 1, 2)
             project_last(1)
-            for d in range(0, D, D // 2):
-                finish(LAST - 1, d, d + D // 2)
-            for c in range(D // P):
-                add_bias(banks["last", c][:], LAST, P * c, P * (c + 1))
-                if c % 2 == 1:
-                    store(LAST, P * (c - 1), P * (c + 1))
+            add_bias(6, 0, 256)
+            store(6, 0, 256)
+            add_bias(6, 256, 512)
+            store(6, 256, 512)
+            add_last(0)
+            add_last(1)
+            store(7, 0, 256)
+            add_last(2)
+            add_last(3)
+            store(7, 256, 512)

@@ -243,6 +243,11 @@ def tile_gatedattentionunit_pb_w4_kernel(tc, q, k, u, v_bytes, v_scale, W_o_word
             b, i = divmod(j, NT)
             nc.sync.dma_start(out=out[b].rearrange("(p i) d -> p i d", i=NT)[:, i, d0:d1], in_=result[j][:, d0:d1])
 
+        def warm_up():
+            bank = ps_av.tile([P, T, P], F32, name="av_bank")
+            for n in range(4):
+                nc.tensor.matmul(bank[:], lhsT=id_bf[:], rhs=id_bf[:].unsqueeze(1).to_broadcast([P, T, P]), start=True, stop=True)
+
         make_identity(nc, id_bf[:])
         with tc.manual_schedule():
             nc.vector.memset(ws_sb[:].bitcast(I32), 0)
@@ -260,12 +265,13 @@ def tile_gatedattentionunit_pb_w4_kernel(tc, q, k, u, v_bytes, v_scale, W_o_word
 
             widen_on_vector(0, 0, 0)
             widen_on_scalar(0, 1, 0)
-            turn_kq(0)
+            warm_up()
             widen_on_vector(0, 0, 1)
             widen_on_scalar(0, 1, 1)
-            turn_q(0)
+            turn_kq(0)
             widen_on_vector(0, 0, 2)
             widen_on_scalar(0, 1, 2)
+            turn_q(0)
             widen_on_vector(0, 0, 3)
             copy_kq(0)
             scores(0)

@@ -25,8 +25,11 @@ TILES = B * NT
 LAST = TILES - 1
 KP = P * T
 G = H // KP
-HELPED = {1: 2, 2: 5, 3: 6}
-LASTN = 4
+CUTS = (0, 384, 784)
+HELPED = (0, 1, 2, 4,)
+HELP_LAG = 3
+STEPS = [((j, 0), (j, 1)) for j in range(TILES)]
+PLACE = {unit: (s, n) for s, pair in enumerate(STEPS) for n, unit in enumerate(pair)}
 QK_SCALE = 1.0 / math.sqrt(S)
 
 
@@ -43,14 +46,21 @@ def tile_gatedattentionunit_pb_w4_kernel(tc, q, k, u, v_bytes, v_scale, W_o_word
             return keep.tile(shape, dt, name=name, align_bytes=64)
 
         k_sb = [kt([P, T, S], BF16, "k_sb%d" % b) for b in range(B)]
-        q_sb = [kt([P, NT, S], BF16, "q_sb%d" % b) for b in range(B)]
+        q_all = kt([P, NT, S], BF16, "q_all")
+        q_first = q_all[:, 0, :]
+        q_rest = q_all[:, 1:, :]
+        q_second = kt([P, NT, S], BF16, "q_second")
         kqT = [kt([P, T + 1, P], BF16, "kqT%d" % b) for b in range(B)]
         qT = [kt([P, NT - 1, P], BF16, "qT%d" % b) for b in range(B)]
-        vb = [[kt([P, 2, H], U8, "vb%d_%d" % (b, c)) for c in range(2)] for b in range(B)]
-        v_bf = [[kt([P, T, KP], BF16, "v_bf%d_%d" % (b, g)) for g in range(G)] for b in range(B)]
-        v_il = [[kt([P, KP, T], BF16, "v_il%d_%d" % (b, g)) for g in range(G)] for b in range(B)]
-        v_c = [[kt([P, KP], U32, "v_c%d_%d" % (b, g)) for g in range(G)] for b in range(B)]
-        v_s = [[kt([P, KP], U8, "v_s%d_%d" % (b, g)) for g in range(G)] for b in range(B)]
+        vb0 = [kt([P, H], U8, "vb0_%d" % t) for t in range(T)]
+        vb1 = [kt([P, 2, H], U8, "vb1_%d" % c) for c in range(2)]
+        v_bf0 = [kt([P, T, KP], BF16, "v_bf0_%d" % g) for g in range(G)]
+        ends = CUTS[1:] + (H,)
+        v_bf1 = [kt([P, T, ends[c] - CUTS[c]], BF16, "v_bf1_%d" % c) for c in range(len(CUTS))]
+        v_il1 = kt([P, H * T], BF16, "v_il")
+        v_il0 = [kt([P, KP * T], BF16, "v_il0_%d" % g)[:] for g in range(G)]
+        v_c = [kt([P, H], U32, "v_c%d" % b) for b in range(B)]
+        v_s = [kt([P, H], U8, "v_s%d" % b) for b in range(B)]
         u_sb = [kt([P, H], BF16, "u_sb%d" % j) for j in range(TILES)]
         r_sb = [kt([P, P, T], F32, "r_sb%d" % j) for j in range(TILES)]
         at_il = [kt([P, P, T], BF16, "at_il%d" % j) for j in range(TILES)]
@@ -60,7 +70,7 @@ def tile_gatedattentionunit_pb_w4_kernel(tc, q, k, u, v_bytes, v_scale, W_o_word
         gT = [kt([P, G, P, T], BF16, "gT%d" % j) for j in range(TILES)]
         gc = [kt([P, G, P], U32, "gc%d" % j) for j in range(TILES)]
         gs = [kt([P, G, P], U8, "gs%d" % j) for j in range(TILES)]
-        o_sb = [kt([P, D], F32, "o_sb%d" % j) for j in range(TILES)]
+        o_sb = {j: kt([P, D], F32, "o_sb%d" % j) for j in range(TILES) if j not in HELPED}
         o_raw = {j: kt([P, D], F32, "o_raw%d" % j) for j in HELPED}
         vs = kt([P, T], F32, "vs")
         w_sb = kt([P, G, 2 * D], U8, "w_sb")
@@ -70,30 +80,11 @@ def tile_gatedattentionunit_pb_w4_kernel(tc, q, k, u, v_bytes, v_scale, W_o_word
         id_f = kt([P, P], F32, "id_f")
 
         banks = {}
-        result = {j: u_sb[HELPED[j]][:].bitcast(F32) if j in HELPED else o_sb[j][:] for j in range(TILES)}
-        woven = {
-            (0, 0): v_il[1][0][:].rearrange("p c t -> p (c t)"),
-            (0, 2): v_il[0][1][:].rearrange("p c t -> p (c t)"),
-            (1, 0): v_il[1][1][:].rearrange("p c t -> p (c t)"),
-            (1, 1): gT[0][:].rearrange("p g n t -> p (g n t)"),
-            (1, 2): u_sb[2][:],
-        }
-
-        def quarters(g, q0, q1):
-            first = max(s for (h, s) in woven if h == g and s <= q0)
-            return woven[g, first][:, (q0 - first) * P * T : (q1 - first) * P * T]
-
-        def load_kq(b):
-            nc.sync.dma_start(out=k_sb[b][:], in_=k[b].rearrange("(p t) s -> p t s", t=T))
-            nc.sync.dma_start(out=q_sb[b][:], in_=q[b].rearrange("(p i) s -> p i s", i=NT))
-
-        def load_v(b):
-            rows = v_bytes[b].rearrange("(p t) h -> p t h", t=T)
-            for t in range(T):
-                if b == 0:
-                    nc.sync.dma_start(out=vb[b][t // 2][:, t % 2, :], in_=rows[:, t, :])
-                elif t % 2 == 0:
-                    nc.sync.dma_start(out=vb[b][t // 2][:], in_=rows[:, t : t + 2, :])
+        result = {j: o_sb[j][:] for j in o_sb}
+        result[0] = v_il1[:, 768 * T :].bitcast(F32)
+        result[1] = v_il1[:, 512 * T : 768 * T].bitcast(F32)
+        result[2] = gT[4][:].rearrange("p g n t -> p (g n t)").bitcast(F32)
+        result[4] = gT[5][:].rearrange("p g n t -> p (g n t)").bitcast(F32)
 
         def load_u(j0, j1):
             for j in range(j0, j1):
@@ -112,10 +103,11 @@ def tile_gatedattentionunit_pb_w4_kernel(tc, q, k, u, v_bytes, v_scale, W_o_word
                 nc.tensor.transpose(bank[:, n, :], src, id_bf[:])
 
         def turn_kq(b):
-            turn(("kq", b), [k_sb[b][:, t, :] for t in range(T)] + [q_sb[b][:, 0, :]])
+            first = q_first[:] if b == 0 else q_second[:, 0, :]
+            turn(("kq", b), [k_sb[b][:, t, :] for t in range(T)] + [first])
 
         def turn_q(b):
-            turn(("q", b), [q_sb[b][:, i, :] for i in range(1, NT)])
+            turn(("q", b), [q_rest[:, i, :] if b == 0 else q_second[:, i + 1, :] for i in range(NT - 1)])
 
         def copy_kq(b):
             nc.scalar.copy(out=kqT[b][:], in_=banks["kq", b][:])
@@ -123,34 +115,38 @@ def tile_gatedattentionunit_pb_w4_kernel(tc, q, k, u, v_bytes, v_scale, W_o_word
         def copy_q(b):
             nc.scalar.copy(out=qT[b][:], in_=banks["q", b][:])
 
-        def widen_on_vector(b, g, t):
-            src = vb[b][t // 2][:, t % 2, KP * g : KP * (g + 1)].bitcast(FP8)
-            nc.vector.tensor_scalar(out=v_bf[b][g][:, t, :], in0=src, scalar1=vs[:, t : t + 1], scalar2=None, op0=ALU.mult)
+        def widen_on_vector(dst, src, t):
+            nc.vector.tensor_scalar(out=dst, in0=src.bitcast(FP8), scalar1=vs[:, t : t + 1], scalar2=None, op0=ALU.mult)
 
-        def widen_on_scalar(b, g, t):
-            src = vb[b][t // 2][:, t % 2, KP * g : KP * (g + 1)].bitcast(FP8)
-            nc.scalar.activation(v_bf[b][g][:, t, :], src, ACT.Copy, scale=vs[:, t : t + 1])
+        def widen_on_scalar(dst, src, t):
+            nc.scalar.activation(dst, src.bitcast(FP8), ACT.Copy, scale=vs[:, t : t + 1])
+
+        def widen_first(widen, g, t):
+            widen(v_bf0[g][:, t, :], vb0[t][:, KP * g : KP * (g + 1)], t)
+
+        def widen_second(widen, c, t):
+            widen(v_bf1[c][:, t, :], vb1[t // 2][:, t % 2, CUTS[c] : ends[c]], t)
 
         def weave(dst, src):
             nc.vector.tensor_copy(out=dst.rearrange("p (c i t) -> p c t i", i=4, t=T), in_=src.rearrange("p t (c i) -> p c t i", i=4))
 
         def weave_first(g):
-            weave(v_il[0][g][:].rearrange("p c t -> p (c t)"), v_bf[0][g][:])
+            weave(v_il0[g], v_bf0[g][:])
 
         def quant_first(g):
-            nc.vector.quantize_mx(out=v_c[0][g][:].bitcast(FP8X4), scales=v_s[0][g][:], in_=v_il[0][g][:].rearrange("p c t -> p (c t)"))
+            cols = slice(KP * g, KP * (g + 1))
+            nc.vector.quantize_mx(out=v_c[0][:, cols].bitcast(FP8X4), scales=v_s[0][:, cols], in_=v_il0[g])
 
-        def weave_second(g, q0, q1):
-            weave(quarters(g, q0, q1), v_bf[1][g][:, :, P * q0 : P * q1])
+        def weave_rest():
+            weave(v_il1[:, CUTS[-1] * T :], v_bf1[-1][:])
 
-        def weave_second_on_gpsimd(g, q0, q1):
-            dst = quarters(g, q0, q1).rearrange("p (c t) -> p c t", t=T)
-            src = v_bf[1][g][:, :, P * q0 : P * q1].rearrange("p t c -> p c t")
+        def weave_on_gpsimd(c):
+            dst = v_il1[:, CUTS[c] * T : CUTS[c + 1] * T].rearrange("p (c t) -> p c t", t=T)
+            src = v_bf1[c][:, :, : CUTS[c + 1] - CUTS[c]].rearrange("p t c -> p c t")
             nc.gpsimd.tensor_scalar(out=dst, in0=src, scalar1=1.0, scalar2=0.0, op0=ALU.mult, op1=ALU.add)
 
-        def quant_second(g, q0, q1):
-            cols = slice(P * q0, P * q1)
-            nc.vector.quantize_mx(out=v_c[1][g][:, cols].bitcast(FP8X4), scales=v_s[1][g][:, cols], in_=quarters(g, q0, q1))
+        def quant_second(c0, c1):
+            nc.vector.quantize_mx(out=v_c[1][:, c0:c1].bitcast(FP8X4), scales=v_s[1][:, c0:c1], in_=v_il1[:, c0 * T : c1 * T])
 
         def scores(j):
             b, i = divmod(j, NT)
@@ -168,15 +164,15 @@ def tile_gatedattentionunit_pb_w4_kernel(tc, q, k, u, v_bytes, v_scale, W_o_word
         def quant_attn(j):
             nc.vector.quantize_mx(out=at_c[j][:].bitcast(FP8X4), scales=at_s[j][:], in_=at_il[j][:].rearrange("p n t -> p (n t)"))
 
-        def mix(j, g):
-            b = j // NT
-            bank = banks["av", j, g] = ps_av.tile([P, KP], F32, name="av_bank")
+        def mix(j, g, pool=ps_av, name="av_bank"):
+            cols = slice(KP * g, KP * (g + 1))
+            bank = banks["av", j, g] = pool.tile([P, KP], F32, name=name)
             nc.tensor.matmul_mx(
                 out=bank[:],
                 lhsT=at_c[j][:].bitcast(FP8X4),
                 lhsT_scale=at_s[j][:],
-                rhs=v_c[b][g][:].bitcast(FP8X4),
-                rhs_scale=v_s[b][g][:],
+                rhs=v_c[j // NT][:, cols].bitcast(FP8X4),
+                rhs_scale=v_s[j // NT][:, cols],
                 start=True,
                 stop=True,
             )
@@ -189,7 +185,7 @@ def tile_gatedattentionunit_pb_w4_kernel(tc, q, k, u, v_bytes, v_scale, W_o_word
         def turn_gated(j, g0=0, g1=G):
             bank = banks["tg", j, g0] = ps_tr.tile([P, g1 - g0, 2, P], F32, name="tr_bank")
             for g in range(g0, g1):
-                words = gt[j][g][:].bitcast(F32)
+                words = gt[STEPS[j][g][0]][STEPS[j][g][1]][:].bitcast(F32)
                 for w in range(2):
                     nc.tensor.transpose(bank[:, g - g0, w, :], words[:, P * w : P * (w + 1)], id_f[:])
 
@@ -206,8 +202,8 @@ def tile_gatedattentionunit_pb_w4_kernel(tc, q, k, u, v_bytes, v_scale, W_o_word
         def project_pass(bank, j, g, d0, d1):
             nc.tensor.matmul_mx(
                 out=bank[:],
-                lhsT=gc[j][:, g, :].bitcast(FP8X4),
-                lhsT_scale=gs[j][:, g, :],
+                lhsT=gc[PLACE[j, g][0]][:, PLACE[j, g][1], :].bitcast(FP8X4),
+                lhsT_scale=gs[PLACE[j, g][0]][:, PLACE[j, g][1], :],
                 rhs=w_sb[:, g, 2 * d0 : 2 * d1].bitcast(FP4X4),
                 rhs_scale=ws_sb[:, g, d0:d1],
                 start=(g == 0),
@@ -219,18 +215,24 @@ def tile_gatedattentionunit_pb_w4_kernel(tc, q, k, u, v_bytes, v_scale, W_o_word
             for g in range(G):
                 project_pass(banks["o", j], j, g, 0, D)
 
+        def project_open(j, pool, name):
+            banks["o", j] = pool.tile([P, D], F32, name=name)
+            project_pass(banks["o", j], j, 0, 0, D)
+
+        def project_close(j):
+            project_pass(banks["o", j], j, 1, 0, D)
+
         def project_last(g):
-            for c in range(LASTN):
+            for c in range(2):
                 if g == 0:
-                    pool, name = ((ps_av, "av_bank"), (ps_qk, "qk_bank"))[c // 3]
-                    banks["last", c] = pool.tile([P, D // LASTN], F32, name=name)
-                project_pass(banks["last", c], LAST, g, D // LASTN * c, D // LASTN * (c + 1))
+                    banks["last", c] = ps_av.tile([P, D // 2], F32, name="av_bank")
+                project_pass(banks["last", c], LAST, g, D // 2 * c, D // 2 * (c + 1))
 
         def add_bias(j, d0=0, d1=D):
             nc.vector.tensor_tensor(out=result[j][:, d0:d1], in0=banks["o", j][:, d0:d1], in1=b_bc[:, d0:d1], op=ALU.add)
 
         def add_last(c):
-            cols = slice(D // LASTN * c, D // LASTN * (c + 1))
+            cols = slice(D // 2 * c, D // 2 * (c + 1))
             nc.vector.tensor_tensor(out=result[LAST][:, cols], in0=banks["last", c][:], in1=b_bc[:, cols], op=ALU.add)
 
         def evacuate(j, d0=0, d1=D):
@@ -250,177 +252,184 @@ def tile_gatedattentionunit_pb_w4_kernel(tc, q, k, u, v_bytes, v_scale, W_o_word
 
         make_identity(nc, id_bf[:])
         with tc.manual_schedule():
-            nc.vector.memset(ws_sb[:].bitcast(I32), 0)
-
             nc.scalar.dma_start(out=vs[:], in_=v_scale.rearrange("o (p t) x -> p (o t x)", t=T))
-            nc.scalar.activation(id_f[:], id_bf[:], ACT.Copy)
-            for b in range(B):
-                load_v(b)
-                load_kq(b)
+            nc.vector.memset(ws_sb[:].bitcast(I32), 0)
+            rows0 = v_bytes[0].rearrange("(p t) h -> p t h", t=T)
+            rows1 = v_bytes[1].rearrange("(p t) h -> p t h", t=T)
+            q_rows = q[0].rearrange("(p i) s -> p i s", i=NT)
+            for t in range(T):
+                nc.sync.dma_start(out=vb0[t][:], in_=rows0[:, t, :])
+            nc.sync.dma_start(out=k_sb[0][:], in_=k[0].rearrange("(p t) s -> p t s", t=T))
+            nc.sync.dma_start(out=q_all[:], in_=q_rows)
+            for c in range(2):
+                nc.sync.dma_start(out=vb1[c][:], in_=rows1[:, 2 * c : 2 * c + 2, :])
+            nc.sync.dma_start(out=k_sb[1][:], in_=k[1].rearrange("(p t) s -> p t s", t=T))
+            nc.sync.dma_start(out=q_second[:], in_=q[1].rearrange("(p i) s -> p i s", i=NT))
             load_u(0, 2)
             load_w()
             load_u(2, NT)
             nc.sync.dma_start(out=b_bc[:], in_=b_o.partition_broadcast(P))
             load_u(NT, TILES)
+            nc.scalar.activation(id_f[:], id_bf[:], ACT.Copy)
 
-            widen_on_vector(0, 0, 0)
-            widen_on_scalar(0, 1, 0)
+            widen_first(widen_on_vector, 0, 0)
+            widen_first(widen_on_scalar, 1, 0)
             warm_up()
-            widen_on_vector(0, 0, 1)
-            widen_on_scalar(0, 1, 1)
+            widen_first(widen_on_vector, 0, 1)
+            widen_first(widen_on_scalar, 1, 1)
             turn_kq(0)
-            widen_on_vector(0, 0, 2)
-            widen_on_scalar(0, 1, 2)
+            widen_first(widen_on_vector, 0, 2)
+            widen_first(widen_on_scalar, 1, 2)
             turn_q(0)
-            widen_on_vector(0, 0, 3)
+            widen_first(widen_on_vector, 0, 3)
             copy_kq(0)
             scores(0)
-            widen_on_vector(0, 1, 3)
+            widen_first(widen_on_vector, 1, 3)
             copy_q(0)
             scores(1)
             weave_first(0)
-            widen_on_scalar(1, 0, 0)
+            widen_second(widen_on_scalar, 0, 0)
             turn_kq(1)
             weave_first(1)
-            widen_on_scalar(1, 0, 1)
+            widen_second(widen_on_scalar, 0, 1)
             turn_q(1)
             quant_first(0)
             relu(0, 0, P // 2)
-            widen_on_vector(1, 0, 2)
+            widen_second(widen_on_vector, 0, 2)
             relu(0, P // 2, P)
             scores(2)
-            widen_on_vector(1, 0, 3)
             square(0, 0, P // 2)
             square(0, P // 2, P)
             quant_attn(0)
-            widen_on_scalar(1, 1, 0)
+            relu(1, 0, P // 2)
             mix(0, 0)
-            quant_first(1)
-            relu(1)
-            mix(0, 1)
-            weave_second_on_gpsimd(0, 2, 3)
-            weave_second(0, 0, 2)
-            widen_on_scalar(1, 1, 1)
+            widen_second(widen_on_vector, 1, 2)
+            relu(1, P // 2, P)
             scores(3)
-            gate(0, 0)
-            square(1)
-            gate(0, 1)
-            relu(2)
+            quant_first(1)
+            square(1, 0, P // 2)
+            mix(0, 1)
+            square(1, P // 2, P)
             quant_attn(1)
-            copy_kq(1)
+            relu(2)
             mix(1, 0)
-            widen_on_vector(1, 1, 2)
+            widen_second(widen_on_vector, 0, 3)
+            copy_kq(1)
+            weave_on_gpsimd(0)
+            widen_second(widen_on_vector, 1, 1)
+            square(2)
+            gate(0, 0)
             relu(3)
             mix(1, 1)
-            widen_on_vector(1, 1, 3)
+            gate(0, 1)
             copy_q(1)
             turn_gated(0)
-            weave_second_on_gpsimd(1, 0, 1)
-            quant_second(0, 0, 2)
-            square(2)
-            scores(4)
             gate(1, 0)
-            copy_gated(0)
-            scores(5)
-            gate(1, 1)
             square(3)
+            scores(4)
+            gate(1, 1)
+            copy_gated(0)
             turn_gated(1)
             quant_attn(2)
-            copy_gated(1)
+            widen_second(widen_on_scalar, 1, 0)
             mix(2, 0)
-            weave_second(0, 3, 4)
+            quant_attn(3)
             relu(4)
             mix(2, 1)
-            quant_gated(0)
-            relu(5)
-            project(0, ps_o, "o_bank")
-            weave_second_on_gpsimd(1, 1, 2)
-            quant_second(0, 2, 4)
-            square(4)
-            scores(6)
-            gate(2, 0)
-            square(5)
-            gate(2, 1)
-            relu(6)
-            weave_second_on_gpsimd(1, 2, 4)
-            quant_attn(3)
+            widen_second(widen_on_vector, 2, 1)
+            copy_gated(1)
             mix(3, 0)
-            quant_gated(1)
+            widen_second(widen_on_vector, 2, 2)
+            square(4)
+            scores(5)
+            widen_second(widen_on_vector, 2, 3)
+            relu(5)
+            scores(6)
+            quant_gated(0)
+            widen_second(widen_on_scalar, 2, 0)
+            widen_second(widen_on_vector, 1, 3)
+            square(5)
+            weave_on_gpsimd(1)
+            quant_second(0, 384)
+            relu(6)
+            gate(2, 0)
             mix(3, 1)
-            add_bias(0)
+            gate(2, 1)
             turn_gated(2)
-            store(0)
             gate(3, 0)
             copy_gated(2)
-            project(1, ps_o, "o_bank")
+            project(0, ps_o, "o_bank")
             gate(3, 1)
-            evacuate(1)
-            scores(7)
-            quant_attn(4)
             square(6)
             turn_gated(3)
-            quant_second(1, 0, 1)
-            copy_gated(3)
-            mix(4, 0)
-            quant_second(1, 1, 2)
+            weave_rest()
+            evacuate(0)
+            scores(7)
+            quant_gated(1)
+            project(1, ps_qk, "qk_bank")
+            quant_attn(4)
+            evacuate(1)
+            quant_second(384, 512)
             relu(7)
-            quant_second(1, 2, 4)
+            mix(4, 0)
+            quant_attn(5)
+            copy_gated(3)
+            quant_second(512, 1024)
+            square(7)
             mix(4, 1)
+            add_on_gpsimd(0)
+            store(0)
+            quant_attn(6)
+            mix(5, 0)
             add_on_gpsimd(1)
             store(1)
-            quant_attn(5)
-            mix(5, 0)
             quant_gated(2)
-            project(2, ps_qk, "qk_bank")
+            project(2, ps_o, "o_bank")
             gate(4, 0)
-            evacuate(2, 0, 256)
             mix(5, 1)
             gate(4, 1)
-            square(7)
             turn_gated(4)
-            quant_gated(3)
-            copy_gated(4)
-            project(3, ps_o, "o_bank")
-            quant_attn(6)
-            evacuate(2, 256, 512)
-            mix(6, 0)
             gate(5, 0)
-            evacuate(3)
-            mix(6, 1)
+            copy_gated(4)
+            mix(6, 0)
             gate(5, 1)
+            evacuate(2)
             turn_gated(5)
+            quant_gated(3)
+            copy_gated(5)
+            mix(6, 1)
+            quant_attn(7)
+            project(3, ps_qk, "qk_bank")
+            quant_gated(4)
+            mix(7, 0)
             add_on_gpsimd(2)
             store(2)
-            quant_attn(7)
-            copy_gated(5)
-            mix(7, 0)
-            quant_gated(4)
-            project(4, ps_qk, "qk_bank")
             gate(6, 0)
-            mix(7, 1)
+            project(4, ps_qk, "qk_bank")
             gate(6, 1)
+            evacuate(4, 0, 256)
+            mix(7, 1)
+            add_bias(3)
             turn_gated(6)
-            add_on_gpsimd(3)
+            store(3)
             quant_gated(5)
             copy_gated(6)
-            project(5, ps_qk, "qk_bank")
-            add_bias(4, 0, 256)
-            store(4, 0, 256)
+            project(5, ps_o, "o_bank")
+            add_on_gpsimd(4, 0, 256)
             gate(7, 0)
             turn_gated(7, 0, 1)
-            store(3)
             gate(7, 1)
             copy_gated(7, 0, 1)
             turn_gated(7, 1, 2)
-            quant_gated(6)
+            add_bias(4, 256, 512)
             copy_gated(7, 1, 2)
-            project(6, ps_o, "o_bank")
+            store(4)
+            quant_gated(6)
+            project(6, ps_qk, "qk_bank")
             add_bias(5)
             store(5)
             quant_gated(7, 0, 1)
-            add_bias(4, 256, 512)
             project_last(0)
-            store(4, 256, 512)
             quant_gated(7, 1, 2)
             project_last(1)
             add_bias(6, 0, 256)
@@ -428,8 +437,6 @@ def tile_gatedattentionunit_pb_w4_kernel(tc, q, k, u, v_bytes, v_scale, W_o_word
             add_bias(6, 256, 512)
             store(6, 256, 512)
             add_last(0)
-            add_last(1)
             store(7, 0, 256)
-            add_last(2)
-            add_last(3)
+            add_last(1)
             store(7, 256, 512)

@@ -25,7 +25,7 @@ TILES = B * NT
 LAST = TILES - 1
 KP = P * T
 G = H // KP
-CUTS = (0, 384, 784)
+CUTS = (0, 304, 656)
 HELPED = (0, 1, 2, 4,)
 HELP_LAG = 3
 STEPS = [((j, 0), (j, 1)) for j in range(TILES)]
@@ -55,8 +55,7 @@ def tile_gatedattentionunit_pb_w4_kernel(tc, q, k, u, v_bytes, v_scale, W_o_word
         vb0 = [kt([P, H], U8, "vb0_%d" % t) for t in range(T)]
         vb1 = [kt([P, 2, H], U8, "vb1_%d" % c) for c in range(2)]
         v_bf0 = [kt([P, T, KP], BF16, "v_bf0_%d" % g) for g in range(G)]
-        ends = CUTS[1:] + (H,)
-        v_bf1 = [kt([P, T, ends[c] - CUTS[c]], BF16, "v_bf1_%d" % c) for c in range(len(CUTS))]
+        v_bf1 = kt([P, T, H], BF16, "v_bf1")
         v_il1 = kt([P, H * T], BF16, "v_il")
         v_il0 = [kt([P, KP * T], BF16, "v_il0_%d" % g)[:] for g in range(G)]
         v_c = [kt([P, H], U32, "v_c%d" % b) for b in range(B)]
@@ -68,6 +67,7 @@ def tile_gatedattentionunit_pb_w4_kernel(tc, q, k, u, v_bytes, v_scale, W_o_word
         at_s = [kt([P, P], U8, "at_s%d" % j) for j in range(TILES)]
         gt = [[kt([P, KP], BF16, "gt%d_%d" % (j, g)) for g in range(G)] for j in range(TILES)]
         gT = [kt([P, G, P, T], BF16, "gT%d" % j) for j in range(TILES)]
+        gT = [v_il1[:, 384 * T : 640 * T].rearrange("p (g n t) -> p g n t", g=G, t=T)] + gT[1:]
         gc = [kt([P, G, P], U32, "gc%d" % j) for j in range(TILES)]
         gs = [kt([P, G, P], U8, "gs%d" % j) for j in range(TILES)]
         o_sb = {j: kt([P, D], F32, "o_sb%d" % j) for j in range(TILES) if j not in HELPED}
@@ -125,7 +125,7 @@ def tile_gatedattentionunit_pb_w4_kernel(tc, q, k, u, v_bytes, v_scale, W_o_word
             widen(v_bf0[g][:, t, :], vb0[t][:, KP * g : KP * (g + 1)], t)
 
         def widen_second(widen, c, t):
-            widen(v_bf1[c][:, t, :], vb1[t // 2][:, t % 2, CUTS[c] : ends[c]], t)
+            widen(v_bf1[:, t, :], vb1[t // 2][:, t % 2, :], t)
 
         def weave(dst, src):
             nc.vector.tensor_copy(out=dst.rearrange("p (c i t) -> p c t i", i=4, t=T), in_=src.rearrange("p t (c i) -> p c t i", i=4))
@@ -138,11 +138,19 @@ def tile_gatedattentionunit_pb_w4_kernel(tc, q, k, u, v_bytes, v_scale, W_o_word
             nc.vector.quantize_mx(out=v_c[0][:, cols].bitcast(FP8X4), scales=v_s[0][:, cols], in_=v_il0[g])
 
         def weave_rest():
-            weave(v_il1[:, CUTS[-1] * T :], v_bf1[-1][:])
+            weave(v_il1[:, CUTS[-1] * T :], v_bf1[:, :, CUTS[-1] :])
+
+        def weave_part(engine, c0, c1):
+            dst = v_il1[:, c0 * T : c1 * T].rearrange("p (c i t) -> p c t i", i=4, t=T)
+            src = v_bf1[:, :, c0:c1].rearrange("p t (c i) -> p c t i", i=4)
+            if engine == "scalar":
+                nc.scalar.copy(out=dst, in_=src)
+            else:
+                nc.vector.tensor_copy(out=dst, in_=src)
 
         def weave_on_gpsimd(c):
             dst = v_il1[:, CUTS[c] * T : CUTS[c + 1] * T].rearrange("p (c t) -> p c t", t=T)
-            src = v_bf1[c][:, :, : CUTS[c + 1] - CUTS[c]].rearrange("p t c -> p c t")
+            src = v_bf1[:, :, CUTS[c] : CUTS[c + 1]].rearrange("p t c -> p c t")
             nc.gpsimd.tensor_scalar(out=dst, in0=src, scalar1=1.0, scalar2=0.0, op0=ALU.mult, op1=ALU.add)
 
         def quant_second(c0, c1):
@@ -291,22 +299,21 @@ def tile_gatedattentionunit_pb_w4_kernel(tc, q, k, u, v_bytes, v_scale, W_o_word
             widen_second(widen_on_scalar, 0, 0)
             turn_kq(1)
             weave_first(1)
-            widen_second(widen_on_scalar, 0, 1)
+            relu(0, 0, P // 2)
             turn_q(1)
             quant_first(0)
-            relu(0, 0, P // 2)
-            widen_second(widen_on_vector, 0, 2)
             relu(0, P // 2, P)
             scores(2)
+            widen_second(widen_on_vector, 0, 1)
             square(0, 0, P // 2)
             square(0, P // 2, P)
             quant_attn(0)
             relu(1, 0, P // 2)
             mix(0, 0)
-            widen_second(widen_on_vector, 1, 2)
+            quant_first(1)
             relu(1, P // 2, P)
             scores(3)
-            quant_first(1)
+            widen_second(widen_on_vector, 0, 2)
             square(1, 0, P // 2)
             mix(0, 1)
             square(1, P // 2, P)
@@ -315,62 +322,57 @@ def tile_gatedattentionunit_pb_w4_kernel(tc, q, k, u, v_bytes, v_scale, W_o_word
             mix(1, 0)
             widen_second(widen_on_vector, 0, 3)
             copy_kq(1)
+            scores(4)
             weave_on_gpsimd(0)
-            widen_second(widen_on_vector, 1, 1)
-            square(2)
             gate(0, 0)
             relu(3)
             mix(1, 1)
             gate(0, 1)
-            copy_q(1)
+            square(2)
             turn_gated(0)
             gate(1, 0)
-            square(3)
-            scores(4)
+            copy_q(1)
+            scores(5)
             gate(1, 1)
-            copy_gated(0)
+            square(3)
             turn_gated(1)
             quant_attn(2)
-            widen_second(widen_on_scalar, 1, 0)
+            copy_gated(0)
             mix(2, 0)
             quant_attn(3)
             relu(4)
             mix(2, 1)
-            widen_second(widen_on_vector, 2, 1)
-            copy_gated(1)
+            weave_part("vector", 736, 832)
+            weave_part("scalar", 656, 736)
             mix(3, 0)
-            widen_second(widen_on_vector, 2, 2)
-            square(4)
-            scores(5)
-            widen_second(widen_on_vector, 2, 3)
-            relu(5)
-            scores(6)
             quant_gated(0)
-            widen_second(widen_on_scalar, 2, 0)
-            widen_second(widen_on_vector, 1, 3)
-            square(5)
+            square(4)
             weave_on_gpsimd(1)
-            quant_second(0, 384)
-            relu(6)
+            quant_second(0, 256)
+            relu(5)
             gate(2, 0)
+            copy_gated(1)
             mix(3, 1)
             gate(2, 1)
-            turn_gated(2)
+            square(5)
+            scores(6)
             gate(3, 0)
+            relu(6)
+            turn_gated(2)
+            gate(3, 1)
             copy_gated(2)
             project(0, ps_o, "o_bank")
-            gate(3, 1)
+            weave_part("vector", 832, 1024)
             square(6)
             turn_gated(3)
-            weave_rest()
+            quant_gated(1)
             evacuate(0)
             scores(7)
-            quant_gated(1)
-            project(1, ps_qk, "qk_bank")
             quant_attn(4)
-            evacuate(1)
-            quant_second(384, 512)
             relu(7)
+            project(1, ps_qk, "qk_bank")
+            quant_second(256, 512)
+            evacuate(1, 0, 416)
             mix(4, 0)
             quant_attn(5)
             copy_gated(3)
@@ -381,8 +383,7 @@ def tile_gatedattentionunit_pb_w4_kernel(tc, q, k, u, v_bytes, v_scale, W_o_word
             store(0)
             quant_attn(6)
             mix(5, 0)
-            add_on_gpsimd(1)
-            store(1)
+            add_on_gpsimd(1, 0, 416)
             quant_gated(2)
             project(2, ps_o, "o_bank")
             gate(4, 0)
@@ -395,25 +396,27 @@ def tile_gatedattentionunit_pb_w4_kernel(tc, q, k, u, v_bytes, v_scale, W_o_word
             gate(5, 1)
             evacuate(2)
             turn_gated(5)
-            quant_gated(3)
+            add_bias(1, 416, 512)
             copy_gated(5)
             mix(6, 1)
-            quant_attn(7)
+            store(1)
+            quant_gated(3)
             project(3, ps_qk, "qk_bank")
-            quant_gated(4)
+            quant_attn(7)
             mix(7, 0)
+            quant_gated(4)
+            project(4, ps_qk, "qk_bank")
             add_on_gpsimd(2)
             store(2)
             gate(6, 0)
-            project(4, ps_qk, "qk_bank")
-            gate(6, 1)
             evacuate(4, 0, 256)
             mix(7, 1)
-            add_bias(3)
+            gate(6, 1)
             turn_gated(6)
+            add_bias(3)
+            copy_gated(6)
             store(3)
             quant_gated(5)
-            copy_gated(6)
             project(5, ps_o, "o_bank")
             add_on_gpsimd(4, 0, 256)
             gate(7, 0)

@@ -25,7 +25,7 @@ TILES = B * NT
 LAST = TILES - 1
 KP = P * T
 G = H // KP
-CUTS = (0, 304, 656)
+CUTS = (0, 320, 672)
 HELPED = (0, 1, 2, 4,)
 HELP_LAG = 3
 STEPS = [((j, 0), (j, 1)) for j in range(TILES)]
@@ -52,6 +52,9 @@ def tile_gatedattentionunit_pb_w4_kernel(tc, q, k, u, v_bytes, v_scale, W_o_word
         q_second = kt([P, NT, S], BF16, "q_second")
         kqT = [kt([P, T + 1, P], BF16, "kqT%d" % b) for b in range(B)]
         qT = [kt([P, NT - 1, P], BF16, "qT%d" % b) for b in range(B)]
+        both = kt([P, T + NT, P], BF16, "both")
+        kqT = [kqT[0], both[:, : T + 1]]
+        qT = [qT[0], both[:, T + 1 :]]
         vb0 = [kt([P, H], U8, "vb0_%d" % t) for t in range(T)]
         vb1 = [kt([P, 2, H], U8, "vb1_%d" % c) for c in range(2)]
         v_bf0 = [kt([P, T, KP], BF16, "v_bf0_%d" % g) for g in range(G)]
@@ -61,10 +64,14 @@ def tile_gatedattentionunit_pb_w4_kernel(tc, q, k, u, v_bytes, v_scale, W_o_word
         v_c = [kt([P, H], U32, "v_c%d" % b) for b in range(B)]
         v_s = [kt([P, H], U8, "v_s%d" % b) for b in range(B)]
         u_sb = [kt([P, H], BF16, "u_sb%d" % j) for j in range(TILES)]
-        r_sb = [kt([P, P, T], F32, "r_sb%d" % j) for j in range(TILES)]
-        at_il = [kt([P, P, T], BF16, "at_il%d" % j) for j in range(TILES)]
-        at_c = [kt([P, P], U32, "at_c%d" % j) for j in range(TILES)]
-        at_s = [kt([P, P], U8, "at_s%d" % j) for j in range(TILES)]
+        r_two = [kt([P, 2, P, T], F32, "r_two%d" % j) for j in range(TILES // 2)]
+        il_two = [kt([P, 2, P, T], BF16, "il_two%d" % j) for j in range(TILES // 2)]
+        c_two = [kt([P, 2, P], U32, "c_two%d" % j) for j in range(TILES // 2)]
+        s_two = [kt([P, 2, P], U8, "s_two%d" % j) for j in range(TILES // 2)]
+        r_sb = [r_two[j // 2][:, j % 2] for j in range(TILES)]
+        at_il = [il_two[j // 2][:, j % 2] for j in range(TILES)]
+        at_c = [c_two[j // 2][:, j % 2] for j in range(TILES)]
+        at_s = [s_two[j // 2][:, j % 2] for j in range(TILES)]
         gt = [[kt([P, KP], BF16, "gt%d_%d" % (j, g)) for g in range(G)] for j in range(TILES)]
         gT = [kt([P, G, P, T], BF16, "gT%d" % j) for j in range(TILES)]
         gT = [v_il1[:, 384 * T : 640 * T].rearrange("p (g n t) -> p g n t", g=G, t=T)] + gT[1:]
@@ -168,6 +175,22 @@ def tile_gatedattentionunit_pb_w4_kernel(tc, q, k, u, v_bytes, v_scale, W_o_word
 
         def square(j, n0=0, n1=P):
             nc.scalar.activation(at_il[j][:, n0:n1], r_sb[j][:, n0:n1], ACT.Square, scale=QK_SCALE)
+
+        def square_pair(j):
+            nc.scalar.activation(il_two[j // 2][:], r_two[j // 2][:], ACT.Square, scale=QK_SCALE)
+
+        def quant_pair(j):
+            nc.vector.quantize_mx(
+                out=c_two[j // 2][:].rearrange("p a n -> p (a n)").bitcast(FP8X4),
+                scales=s_two[j // 2][:].rearrange("p a n -> p (a n)"),
+                in_=il_two[j // 2][:].rearrange("p a n t -> p (a n t)"),
+            )
+
+        def turn_all(b):
+            turn(("kq", b), [k_sb[b][:, t, :] for t in range(T)] + [q_second[:, i, :] for i in range(NT)])
+
+        def copy_all(b):
+            nc.scalar.copy(out=both[:], in_=banks["kq", b][:])
 
         def quant_attn(j):
             nc.vector.quantize_mx(out=at_c[j][:].bitcast(FP8X4), scales=at_s[j][:], in_=at_il[j][:].rearrange("p n t -> p (n t)"))
@@ -297,94 +320,84 @@ def tile_gatedattentionunit_pb_w4_kernel(tc, q, k, u, v_bytes, v_scale, W_o_word
             scores(1)
             weave_first(0)
             widen_second(widen_on_scalar, 0, 0)
-            turn_kq(1)
+            turn_all(1)
             weave_first(1)
-            relu(0, 0, P // 2)
-            turn_q(1)
-            quant_first(0)
-            relu(0, P // 2, P)
+            relu(0)
             scores(2)
-            widen_second(widen_on_vector, 0, 1)
-            square(0, 0, P // 2)
-            square(0, P // 2, P)
-            quant_attn(0)
-            relu(1, 0, P // 2)
-            mix(0, 0)
-            quant_first(1)
-            relu(1, P // 2, P)
+            quant_first(0)
+            relu(1)
             scores(3)
-            widen_second(widen_on_vector, 0, 2)
-            square(1, 0, P // 2)
-            mix(0, 1)
-            square(1, P // 2, P)
-            quant_attn(1)
+            widen_second(widen_on_vector, 0, 1)
+            square(0)
+            quant_first(1)
+            square(1)
+            quant_attn(0)
             relu(2)
-            mix(1, 0)
-            widen_second(widen_on_vector, 0, 3)
-            copy_kq(1)
-            scores(4)
-            weave_on_gpsimd(0)
-            gate(0, 0)
+            mix(0, 0)
+            widen_second(widen_on_vector, 0, 2)
             relu(3)
-            mix(1, 1)
+            mix(0, 1)
+            widen_second(widen_on_vector, 0, 3)
+            copy_all(1)
+            weave_on_gpsimd(0)
+            quant_attn(1)
+            square_pair(2)
+            mix(1, 0)
+            gate(0, 0)
+            scores(4)
             gate(0, 1)
-            square(2)
-            turn_gated(0)
-            gate(1, 0)
-            copy_q(1)
-            scores(5)
-            gate(1, 1)
-            square(3)
-            turn_gated(1)
-            quant_attn(2)
-            copy_gated(0)
-            mix(2, 0)
-            quant_attn(3)
             relu(4)
-            mix(2, 1)
-            weave_part("vector", 736, 832)
-            weave_part("scalar", 656, 736)
-            mix(3, 0)
+            mix(1, 1)
+            gate(1, 0)
+            turn_gated(0)
+            gate(1, 1)
+            copy_gated(0)
+            scores(5)
+            quant_pair(2)
+            relu(5)
+            turn_gated(1)
+            weave_part("vector", 800, 928)
+            weave_part("scalar", 672, 800)
+            mix(2, 0)
             quant_gated(0)
-            square(4)
+            copy_gated(1)
+            mix(2, 1)
             weave_on_gpsimd(1)
             quant_second(0, 256)
-            relu(5)
+            square_pair(4)
+            mix(3, 0)
             gate(2, 0)
-            copy_gated(1)
-            mix(3, 1)
-            gate(2, 1)
-            square(5)
             scores(6)
-            gate(3, 0)
+            gate(2, 1)
             relu(6)
+            mix(3, 1)
+            gate(3, 0)
             turn_gated(2)
             gate(3, 1)
             copy_gated(2)
             project(0, ps_o, "o_bank")
-            weave_part("vector", 832, 1024)
+            weave_part("vector", 928, 1024)
             square(6)
             turn_gated(3)
             quant_gated(1)
             evacuate(0)
             scores(7)
-            quant_attn(4)
+            quant_pair(4)
             relu(7)
             project(1, ps_qk, "qk_bank")
             quant_second(256, 512)
             evacuate(1, 0, 416)
             mix(4, 0)
-            quant_attn(5)
-            copy_gated(3)
             quant_second(512, 1024)
-            square(7)
+            copy_gated(3)
             mix(4, 1)
             add_on_gpsimd(0)
             store(0)
-            quant_attn(6)
+            quant_gated(2)
+            square(7)
             mix(5, 0)
             add_on_gpsimd(1, 0, 416)
-            quant_gated(2)
+            quant_attn(6)
             project(2, ps_o, "o_bank")
             gate(4, 0)
             mix(5, 1)

@@ -135,7 +135,7 @@ def tile_gatedattentionunit_pb_w4_kernel(tc, q, k, u, v_bytes, v_scale, W_o_word
             widen(v_bf1[:, t, :], vb1[t // 2][:, t % 2, :], t)
 
         def weave(dst, src):
-            nc.vector.tensor_copy(out=dst.rearrange("p (c i t) -> p c t i", i=4, t=T), in_=src.rearrange("p t (c i) -> p c t i", i=4))
+            nc.vector.tensor_copy(out=dst.rearrange("p (c i t) -> p c t i", i=2, t=T), in_=src.rearrange("p t (c i) -> p c t i", i=2))
 
         def weave_first(g):
             weave(v_il0[g], v_bf0[g][:])
@@ -148,8 +148,8 @@ def tile_gatedattentionunit_pb_w4_kernel(tc, q, k, u, v_bytes, v_scale, W_o_word
             weave(v_il1[:, CUTS[-1] * T :], v_bf1[:, :, CUTS[-1] :])
 
         def weave_part(engine, c0, c1):
-            dst = v_il1[:, c0 * T : c1 * T].rearrange("p (c i t) -> p c t i", i=4, t=T)
-            src = v_bf1[:, :, c0:c1].rearrange("p t (c i) -> p c t i", i=4)
+            dst = v_il1[:, c0 * T : c1 * T].rearrange("p (c i t) -> p c t i", i=2, t=T)
+            src = v_bf1[:, :, c0:c1].rearrange("p t (c i) -> p c t i", i=2)
             if engine == "scalar":
                 nc.scalar.copy(out=dst, in_=src)
             else:

@@ -25,12 +25,11 @@ TILES = B * NT
 LAST = TILES - 1
 KP = P * T
 G = H // KP
-CUTS = (0, 320, 672)
-HELPED = (0, 1, 2, 4,)
-HELP_LAG = 3
-STEPS = [((j, 0), (j, 1)) for j in range(TILES)]
-PLACE = {unit: (s, n) for s, pair in enumerate(STEPS) for n, unit in enumerate(pair)}
+BANK_COLS = 256
 QK_SCALE = 1.0 / math.sqrt(S)
+HELPED = (0, 1, 2, 3)
+C0, C1, C2 = 320, 704, 896
+D1 = 256
 
 
 def tile_gatedattentionunit_pb_w4_kernel(tc, q, k, u, v_bytes, v_scale, W_o_words, W_o_scales, b_o, out):
@@ -46,21 +45,13 @@ def tile_gatedattentionunit_pb_w4_kernel(tc, q, k, u, v_bytes, v_scale, W_o_word
             return keep.tile(shape, dt, name=name, align_bytes=64)
 
         k_sb = [kt([P, T, S], BF16, "k_sb%d" % b) for b in range(B)]
-        q_all = kt([P, NT, S], BF16, "q_all")
-        q_first = q_all[:, 0, :]
-        q_rest = q_all[:, 1:, :]
-        q_second = kt([P, NT, S], BF16, "q_second")
-        kqT = [kt([P, T + 1, P], BF16, "kqT%d" % b) for b in range(B)]
-        qT = [kt([P, NT - 1, P], BF16, "qT%d" % b) for b in range(B)]
-        both = kt([P, T + NT, P], BF16, "both")
-        kqT = [kqT[0], both[:, : T + 1]]
-        qT = [qT[0], both[:, T + 1 :]]
+        q_sb = [kt([P, NT, S], BF16, "q_sb%d" % b) for b in range(B)]
+        kqT = [kt([P, T + NT, P], BF16, "kqT%d" % b) for b in range(B)]
         vb0 = [kt([P, H], U8, "vb0_%d" % t) for t in range(T)]
         vb1 = [kt([P, 2, H], U8, "vb1_%d" % c) for c in range(2)]
-        v_bf0 = [kt([P, T, KP], BF16, "v_bf0_%d" % g) for g in range(G)]
-        v_bf1 = kt([P, T, H], BF16, "v_bf1")
-        v_il1 = kt([P, H * T], BF16, "v_il")
-        v_il0 = [kt([P, KP * T], BF16, "v_il0_%d" % g)[:] for g in range(G)]
+        v_raw = [[vb0[t][:] for t in range(T)], [vb1[t // 2][:, t % 2, :] for t in range(T)]]
+        v_bf = [kt([P, T, H], BF16, "v_bf%d" % b) for b in range(B)]
+        v_il = [kt([P, H * T], BF16, "v_il%d" % b) for b in range(B)]
         v_c = [kt([P, H], U32, "v_c%d" % b) for b in range(B)]
         v_s = [kt([P, H], U8, "v_s%d" % b) for b in range(B)]
         u_sb = [kt([P, H], BF16, "u_sb%d" % j) for j in range(TILES)]
@@ -68,13 +59,8 @@ def tile_gatedattentionunit_pb_w4_kernel(tc, q, k, u, v_bytes, v_scale, W_o_word
         il_two = [kt([P, 2, P, T], BF16, "il_two%d" % j) for j in range(TILES // 2)]
         c_two = [kt([P, 2, P], U32, "c_two%d" % j) for j in range(TILES // 2)]
         s_two = [kt([P, 2, P], U8, "s_two%d" % j) for j in range(TILES // 2)]
-        r_sb = [r_two[j // 2][:, j % 2] for j in range(TILES)]
-        at_il = [il_two[j // 2][:, j % 2] for j in range(TILES)]
-        at_c = [c_two[j // 2][:, j % 2] for j in range(TILES)]
-        at_s = [s_two[j // 2][:, j % 2] for j in range(TILES)]
         gt = [[kt([P, KP], BF16, "gt%d_%d" % (j, g)) for g in range(G)] for j in range(TILES)]
         gT = [kt([P, G, P, T], BF16, "gT%d" % j) for j in range(TILES)]
-        gT = [v_il1[:, 384 * T : 640 * T].rearrange("p (g n t) -> p g n t", g=G, t=T)] + gT[1:]
         gc = [kt([P, G, P], U32, "gc%d" % j) for j in range(TILES)]
         gs = [kt([P, G, P], U8, "gs%d" % j) for j in range(TILES)]
         o_sb = {j: kt([P, D], F32, "o_sb%d" % j) for j in range(TILES) if j not in HELPED}
@@ -88,10 +74,11 @@ def tile_gatedattentionunit_pb_w4_kernel(tc, q, k, u, v_bytes, v_scale, W_o_word
 
         banks = {}
         result = {j: o_sb[j][:] for j in o_sb}
-        result[0] = v_il1[:, 768 * T :].bitcast(F32)
-        result[1] = v_il1[:, 512 * T : 768 * T].bitcast(F32)
-        result[2] = gT[4][:].rearrange("p g n t -> p (g n t)").bitcast(F32)
-        result[4] = gT[5][:].rearrange("p g n t -> p (g n t)").bitcast(F32)
+        gT[0] = v_il[1][:, 384 * T : 640 * T].rearrange("p (g n t) -> p g n t", g=G, t=T)
+        result[0] = v_il[1][:, 768 * T :].bitcast(F32)
+        result[1] = v_il[1][:, 512 * T : 768 * T].bitcast(F32)
+        result[2] = il_two[3][:].rearrange("p a n t -> p (a n t)").bitcast(F32)
+        result[3] = u_sb[6][:].bitcast(F32)
 
         def load_u(j0, j1):
             for j in range(j0, j1):
@@ -104,104 +91,96 @@ def tile_gatedattentionunit_pb_w4_kernel(tc, q, k, u, v_bytes, v_scale, W_o_word
             for r in range(4):
                 nc.sync.dma_start(out=ws_i[r:P:32, :, :], in_=rows[r])
 
-        def turn(name, srcs):
+        def load_k(b):
+            nc.sync.dma_start(out=k_sb[b][:], in_=k[b].rearrange("(p t) s -> p t s", t=T))
+
+        def load_q(b):
+            nc.sync.dma_start(out=q_sb[b][:], in_=q[b].rearrange("(p i) s -> p i s", i=NT))
+
+        def load_q_first(i0, i1):
+            nc.sync.dma_start(out=q_sb[0][:, i0:i1, :], in_=q[0].rearrange("(p i) s -> p i s", i=NT)[:, i0:i1, :])
+
+        def turn_first(name, srcs):
             bank = banks[name] = ps_tr.tile([P, len(srcs), P], BF16, name="tr_bank")
             for n, src in enumerate(srcs):
                 nc.tensor.transpose(bank[:, n, :], src, id_bf[:])
 
-        def turn_kq(b):
-            first = q_first[:] if b == 0 else q_second[:, 0, :]
-            turn(("kq", b), [k_sb[b][:, t, :] for t in range(T)] + [first])
+        def copy_first(name, n0, n1):
+            nc.scalar.copy(out=kqT[0][:, n0:n1, :], in_=banks[name][:])
 
-        def turn_q(b):
-            turn(("q", b), [q_rest[:, i, :] if b == 0 else q_second[:, i + 1, :] for i in range(NT - 1)])
+        def turn_kq(b):
+            bank = banks["kq", b] = ps_tr.tile([P, T + NT, P], BF16, name="tr_bank")
+            for t in range(T):
+                nc.tensor.transpose(bank[:, t, :], k_sb[b][:, t, :], id_bf[:])
+            for i in range(NT):
+                nc.tensor.transpose(bank[:, T + i, :], q_sb[b][:, i, :], id_bf[:])
 
         def copy_kq(b):
             nc.scalar.copy(out=kqT[b][:], in_=banks["kq", b][:])
 
-        def copy_q(b):
-            nc.scalar.copy(out=qT[b][:], in_=banks["q", b][:])
+        def widen_on_vector(b, t, c0=0, c1=H):
+            nc.vector.tensor_scalar(out=v_bf[b][:, t, c0:c1], in0=v_raw[b][t][:, c0:c1].bitcast(FP8), scalar1=vs[:, t : t + 1], scalar2=None, op0=ALU.mult)
 
-        def widen_on_vector(dst, src, t):
-            nc.vector.tensor_scalar(out=dst, in0=src.bitcast(FP8), scalar1=vs[:, t : t + 1], scalar2=None, op0=ALU.mult)
+        def widen_on_scalar(b, t, c0=0, c1=H):
+            nc.scalar.activation(v_bf[b][:, t, c0:c1], v_raw[b][t][:, c0:c1].bitcast(FP8), ACT.Copy, scale=vs[:, t : t + 1])
 
-        def widen_on_scalar(dst, src, t):
-            nc.scalar.activation(dst, src.bitcast(FP8), ACT.Copy, scale=vs[:, t : t + 1])
+        def weave_on_vector(b, c0, c1):
+            dst = v_il[b][:, c0 * T : c1 * T].rearrange("p (c i t) -> p c t i", i=2, t=T)
+            nc.vector.tensor_copy(out=dst, in_=v_bf[b][:, :, c0:c1].rearrange("p t (c i) -> p c t i", i=2))
 
-        def widen_first(widen, g, t):
-            widen(v_bf0[g][:, t, :], vb0[t][:, KP * g : KP * (g + 1)], t)
+        def weave_on_scalar(b, c0, c1):
+            dst = v_il[b][:, c0 * T : c1 * T].rearrange("p (c i t) -> p c t i", i=2, t=T)
+            nc.scalar.copy(out=dst, in_=v_bf[b][:, :, c0:c1].rearrange("p t (c i) -> p c t i", i=2))
 
-        def widen_second(widen, c, t):
-            widen(v_bf1[:, t, :], vb1[t // 2][:, t % 2, :], t)
-
-        def weave(dst, src):
-            nc.vector.tensor_copy(out=dst.rearrange("p (c i t) -> p c t i", i=2, t=T), in_=src.rearrange("p t (c i) -> p c t i", i=2))
-
-        def weave_first(g):
-            weave(v_il0[g], v_bf0[g][:])
-
-        def quant_first(g):
-            cols = slice(KP * g, KP * (g + 1))
-            nc.vector.quantize_mx(out=v_c[0][:, cols].bitcast(FP8X4), scales=v_s[0][:, cols], in_=v_il0[g])
-
-        def weave_rest():
-            weave(v_il1[:, CUTS[-1] * T :], v_bf1[:, :, CUTS[-1] :])
-
-        def weave_part(engine, c0, c1):
-            dst = v_il1[:, c0 * T : c1 * T].rearrange("p (c i t) -> p c t i", i=2, t=T)
-            src = v_bf1[:, :, c0:c1].rearrange("p t (c i) -> p c t i", i=2)
-            if engine == "scalar":
-                nc.scalar.copy(out=dst, in_=src)
-            else:
-                nc.vector.tensor_copy(out=dst, in_=src)
-
-        def weave_on_gpsimd(c):
-            dst = v_il1[:, CUTS[c] * T : CUTS[c + 1] * T].rearrange("p (c t) -> p c t", t=T)
-            src = v_bf1[:, :, CUTS[c] : CUTS[c + 1]].rearrange("p t c -> p c t")
+        def weave_on_gpsimd(b, c0, c1):
+            dst = v_il[b][:, c0 * T : c1 * T].rearrange("p (c t) -> p c t", t=T)
+            src = v_bf[b][:, :, c0:c1].rearrange("p t c -> p c t")
             nc.gpsimd.tensor_scalar(out=dst, in0=src, scalar1=1.0, scalar2=0.0, op0=ALU.mult, op1=ALU.add)
 
-        def quant_second(c0, c1):
-            nc.vector.quantize_mx(out=v_c[1][:, c0:c1].bitcast(FP8X4), scales=v_s[1][:, c0:c1], in_=v_il1[:, c0 * T : c1 * T])
+        def weave_on_tensor(b, c0, c1, half, pool, name, parts=2):
+            if half == 0:
+                banks["v", b, c0] = pool.tile([P, (c1 - c0) * T], BF16, name=name)
+            slots = slice(T // parts * half, T // parts * (half + 1))
+            dst = banks["v", b, c0][:].rearrange("p (c t) -> p t c", t=T)[:, slots, :]
+            nc.tensor.matmul(dst, lhsT=id_bf[:], rhs=v_bf[b][:, slots, c0:c1], start=True, stop=True)
+
+        def copy_woven(b, c0, c1):
+            nc.scalar.copy(out=v_il[b][:, c0 * T : c1 * T], in_=banks["v", b, c0][:])
+
+        def copy_woven_on_vector(b, c0, c1):
+            nc.vector.tensor_copy(out=v_il[b][:, c0 * T : c1 * T], in_=banks["v", b, c0][:])
+
+        def quant_v(b, c0, c1):
+            nc.vector.quantize_mx(out=v_c[b][:, c0:c1].bitcast(FP8X4), scales=v_s[b][:, c0:c1], in_=v_il[b][:, c0 * T : c1 * T])
 
         def scores(j):
             b, i = divmod(j, NT)
             bank = banks["qk", j] = ps_qk.tile([P, T, P], F32, name="qk_bank")
-            queries = kqT[b][:, T, :] if i == 0 else qT[b][:, i - 1, :]
             for t in range(T):
-                nc.tensor.matmul(bank[:, t, :], lhsT=kqT[b][:, t, :], rhs=queries, start=True, stop=True)
+                nc.tensor.matmul(bank[:, t, :], lhsT=kqT[b][:, t, :], rhs=kqT[b][:, T + i, :], start=True, stop=True)
 
-        def relu(j, n0=0, n1=P):
-            nc.scalar.activation(r_sb[j][:, n0:n1], banks["qk", j][:, :, n0:n1].rearrange("p t n -> p n t"), ACT.Relu)
+        def relu(j):
+            nc.scalar.activation(r_two[j // 2][:, j % 2], banks["qk", j][:].rearrange("p t n -> p n t"), ACT.Relu)
 
-        def square(j, n0=0, n1=P):
-            nc.scalar.activation(at_il[j][:, n0:n1], r_sb[j][:, n0:n1], ACT.Square, scale=QK_SCALE)
+        def square(j, n=1):
+            a = slice(j % 2, j % 2 + n)
+            nc.scalar.activation(il_two[j // 2][:, a], r_two[j // 2][:, a], ACT.Square, scale=QK_SCALE)
 
-        def square_pair(j):
-            nc.scalar.activation(il_two[j // 2][:], r_two[j // 2][:], ACT.Square, scale=QK_SCALE)
-
-        def quant_pair(j):
+        def quant_attn(j, n=1):
+            a = slice(j % 2, j % 2 + n)
             nc.vector.quantize_mx(
-                out=c_two[j // 2][:].rearrange("p a n -> p (a n)").bitcast(FP8X4),
-                scales=s_two[j // 2][:].rearrange("p a n -> p (a n)"),
-                in_=il_two[j // 2][:].rearrange("p a n t -> p (a n t)"),
+                out=c_two[j // 2][:, a].rearrange("p a n -> p (a n)").bitcast(FP8X4),
+                scales=s_two[j // 2][:, a].rearrange("p a n -> p (a n)"),
+                in_=il_two[j // 2][:, a].rearrange("p a n t -> p (a n t)"),
             )
 
-        def turn_all(b):
-            turn(("kq", b), [k_sb[b][:, t, :] for t in range(T)] + [q_second[:, i, :] for i in range(NT)])
-
-        def copy_all(b):
-            nc.scalar.copy(out=both[:], in_=banks["kq", b][:])
-
-        def quant_attn(j):
-            nc.vector.quantize_mx(out=at_c[j][:].bitcast(FP8X4), scales=at_s[j][:], in_=at_il[j][:].rearrange("p n t -> p (n t)"))
-
-        def mix(j, g, pool=ps_av, name="av_bank"):
+        def mix(j, g):
             cols = slice(KP * g, KP * (g + 1))
-            bank = banks["av", j, g] = pool.tile([P, KP], F32, name=name)
+            bank = banks["av", j, g] = ps_av.tile([P, KP], F32, name="av_bank")
             nc.tensor.matmul_mx(
                 out=bank[:],
-                lhsT=at_c[j][:].bitcast(FP8X4),
-                lhsT_scale=at_s[j][:],
+                lhsT=c_two[j // 2][:, j % 2].bitcast(FP8X4),
+                lhsT_scale=s_two[j // 2][:, j % 2],
                 rhs=v_c[j // NT][:, cols].bitcast(FP8X4),
                 rhs_scale=v_s[j // NT][:, cols],
                 start=True,
@@ -216,7 +195,7 @@ def tile_gatedattentionunit_pb_w4_kernel(tc, q, k, u, v_bytes, v_scale, W_o_word
         def turn_gated(j, g0=0, g1=G):
             bank = banks["tg", j, g0] = ps_tr.tile([P, g1 - g0, 2, P], F32, name="tr_bank")
             for g in range(g0, g1):
-                words = gt[STEPS[j][g][0]][STEPS[j][g][1]][:].bitcast(F32)
+                words = gt[j][g][:].bitcast(F32)
                 for w in range(2):
                     nc.tensor.transpose(bank[:, g - g0, w, :], words[:, P * w : P * (w + 1)], id_f[:])
 
@@ -233,8 +212,8 @@ def tile_gatedattentionunit_pb_w4_kernel(tc, q, k, u, v_bytes, v_scale, W_o_word
         def project_pass(bank, j, g, d0, d1):
             nc.tensor.matmul_mx(
                 out=bank[:],
-                lhsT=gc[PLACE[j, g][0]][:, PLACE[j, g][1], :].bitcast(FP8X4),
-                lhsT_scale=gs[PLACE[j, g][0]][:, PLACE[j, g][1], :],
+                lhsT=gc[j][:, g, :].bitcast(FP8X4),
+                lhsT_scale=gs[j][:, g, :],
                 rhs=w_sb[:, g, 2 * d0 : 2 * d1].bitcast(FP4X4),
                 rhs_scale=ws_sb[:, g, d0:d1],
                 start=(g == 0),
@@ -245,13 +224,6 @@ def tile_gatedattentionunit_pb_w4_kernel(tc, q, k, u, v_bytes, v_scale, W_o_word
             banks["o", j] = pool.tile([P, D], F32, name=name)
             for g in range(G):
                 project_pass(banks["o", j], j, g, 0, D)
-
-        def project_open(j, pool, name):
-            banks["o", j] = pool.tile([P, D], F32, name=name)
-            project_pass(banks["o", j], j, 0, 0, D)
-
-        def project_close(j):
-            project_pass(banks["o", j], j, 1, 0, D)
 
         def project_last(g):
             for c in range(2):
@@ -276,9 +248,9 @@ def tile_gatedattentionunit_pb_w4_kernel(tc, q, k, u, v_bytes, v_scale, W_o_word
             b, i = divmod(j, NT)
             nc.sync.dma_start(out=out[b].rearrange("(p i) d -> p i d", i=NT)[:, i, d0:d1], in_=result[j][:, d0:d1])
 
-        def warm_up():
+        def warm_up(count):
             bank = ps_av.tile([P, T, P], F32, name="av_bank")
-            for n in range(4):
+            for n in range(count):
                 nc.tensor.matmul(bank[:], lhsT=id_bf[:], rhs=id_bf[:].unsqueeze(1).to_broadcast([P, T, P]), start=True, stop=True)
 
         make_identity(nc, id_bf[:])
@@ -287,15 +259,14 @@ def tile_gatedattentionunit_pb_w4_kernel(tc, q, k, u, v_bytes, v_scale, W_o_word
             nc.vector.memset(ws_sb[:].bitcast(I32), 0)
             rows0 = v_bytes[0].rearrange("(p t) h -> p t h", t=T)
             rows1 = v_bytes[1].rearrange("(p t) h -> p t h", t=T)
-            q_rows = q[0].rearrange("(p i) s -> p i s", i=NT)
             for t in range(T):
                 nc.sync.dma_start(out=vb0[t][:], in_=rows0[:, t, :])
-            nc.sync.dma_start(out=k_sb[0][:], in_=k[0].rearrange("(p t) s -> p t s", t=T))
-            nc.sync.dma_start(out=q_all[:], in_=q_rows)
+            load_k(0)
+            load_q(0)
             for c in range(2):
                 nc.sync.dma_start(out=vb1[c][:], in_=rows1[:, 2 * c : 2 * c + 2, :])
-            nc.sync.dma_start(out=k_sb[1][:], in_=k[1].rearrange("(p t) s -> p t s", t=T))
-            nc.sync.dma_start(out=q_second[:], in_=q[1].rearrange("(p i) s -> p i s", i=NT))
+            load_k(1)
+            load_q(1)
             load_u(0, 2)
             load_w()
             load_u(2, NT)
@@ -303,156 +274,159 @@ def tile_gatedattentionunit_pb_w4_kernel(tc, q, k, u, v_bytes, v_scale, W_o_word
             load_u(NT, TILES)
             nc.scalar.activation(id_f[:], id_bf[:], ACT.Copy)
 
-            widen_first(widen_on_vector, 0, 0)
-            widen_first(widen_on_scalar, 1, 0)
-            warm_up()
-            widen_first(widen_on_vector, 0, 1)
-            widen_first(widen_on_scalar, 1, 1)
-            turn_kq(0)
-            widen_first(widen_on_vector, 0, 2)
-            widen_first(widen_on_scalar, 1, 2)
-            turn_q(0)
-            widen_first(widen_on_vector, 0, 3)
-            copy_kq(0)
+            warm_up(2)
+            widen_on_scalar(0, 0, KP, H)
+            turn_first("k", [k_sb[0][:, t, :] for t in range(T)] + [q_sb[0][:, 0, :]])
+            widen_on_scalar(0, 1, KP, H)
+            turn_first("q", [q_sb[0][:, i, :] for i in range(1, NT)])
+            widen_on_scalar(0, 2, KP, H)
+            copy_first("k", 0, T + 1)
             scores(0)
-            widen_first(widen_on_vector, 1, 3)
-            copy_q(0)
+            copy_first("q", T + 1, T + NT)
             scores(1)
-            weave_first(0)
-            widen_second(widen_on_scalar, 0, 0)
-            turn_all(1)
-            weave_first(1)
+            widen_on_scalar(1, 0)
+            turn_kq(1)
             relu(0)
             scores(2)
-            quant_first(0)
             relu(1)
             scores(3)
-            widen_second(widen_on_vector, 0, 1)
             square(0)
-            quant_first(1)
             square(1)
-            quant_attn(0)
             relu(2)
-            mix(0, 0)
-            widen_second(widen_on_vector, 0, 2)
             relu(3)
+            copy_kq(1)
+            square(2, 2)
+            widen_on_vector(0, 0, 0, KP)
+            widen_on_vector(0, 1, 0, KP)
+            widen_on_vector(0, 2, 0, KP)
+            widen_on_vector(0, 3, 0, KP)
+            widen_on_vector(0, 3, KP, H)
+            weave_on_vector(0, 0, KP)
+            weave_on_vector(0, KP, H)
+            quant_v(0, 0, KP)
+            widen_on_vector(1, 1)
+            quant_v(0, KP, H)
+            quant_attn(0)
+            mix(0, 0)
             mix(0, 1)
-            widen_second(widen_on_vector, 0, 3)
-            copy_all(1)
-            weave_on_gpsimd(0)
+            widen_on_vector(1, 2)
+            widen_on_vector(1, 3, 0, C0)
+            weave_on_gpsimd(1, 0, C0)
             quant_attn(1)
-            square_pair(2)
             mix(1, 0)
             gate(0, 0)
-            scores(4)
-            gate(0, 1)
-            relu(4)
             mix(1, 1)
-            gate(1, 0)
+            gate(0, 1)
             turn_gated(0)
-            gate(1, 1)
             copy_gated(0)
+            scores(4)
+            relu(4)
+            weave_on_tensor(1, C1, C2, 0, ps_o, "o_bank")
             scores(5)
-            quant_pair(2)
             relu(5)
+            gate(1, 0)
+            gate(1, 1)
             turn_gated(1)
-            weave_part("vector", 800, 928)
-            weave_part("scalar", 672, 800)
-            mix(2, 0)
-            quant_gated(0)
             copy_gated(1)
+            quant_attn(2, 2)
+            mix(2, 0)
             mix(2, 1)
-            weave_on_gpsimd(1)
-            quant_second(0, 256)
-            square_pair(4)
+            widen_on_vector(1, 3, C0, H)
+            weave_on_tensor(1, C1, C2, 1, ps_o, "o_bank")
+            copy_woven(1, C1, C2)
             mix(3, 0)
+            square(4, 2)
+            weave_on_tensor(1, C2, H, 0, ps_qk, "qk_bank")
+            weave_on_tensor(1, C2, H, 1, ps_qk, "qk_bank")
+            quant_gated(0)
+            weave_on_gpsimd(1, C0, C1)
+            quant_v(1, 0, 256)
             gate(2, 0)
-            scores(6)
-            gate(2, 1)
-            relu(6)
             mix(3, 1)
-            gate(3, 0)
+            scores(6)
+            relu(6)
+            gate(2, 1)
             turn_gated(2)
-            gate(3, 1)
             copy_gated(2)
             project(0, ps_o, "o_bank")
-            weave_part("vector", 928, 1024)
             square(6)
+            evacuate(0)
+            gate(3, 0)
+            copy_woven_on_vector(1, C2, H)
+            scores(7)
+            gate(3, 1)
             turn_gated(3)
             quant_gated(1)
-            evacuate(0)
-            scores(7)
-            quant_pair(4)
-            relu(7)
             project(1, ps_qk, "qk_bank")
-            quant_second(256, 512)
-            evacuate(1, 0, 416)
-            mix(4, 0)
-            quant_second(512, 1024)
+            evacuate(1, 0, D1)
+            relu(7)
             copy_gated(3)
+            square(7)
+            quant_attn(4, 2)
+            quant_v(1, 256, 640)
+            mix(4, 0)
+            quant_v(1, 640, H)
             mix(4, 1)
             add_on_gpsimd(0)
             store(0)
-            quant_gated(2)
-            square(7)
             mix(5, 0)
-            add_on_gpsimd(1, 0, 416)
-            quant_attn(6)
+            add_on_gpsimd(1, 0, D1)
+            quant_gated(2)
             project(2, ps_o, "o_bank")
+            quant_attn(6)
             gate(4, 0)
             mix(5, 1)
             gate(4, 1)
             turn_gated(4)
-            gate(5, 0)
             copy_gated(4)
             mix(6, 0)
-            gate(5, 1)
             evacuate(2)
-            turn_gated(5)
-            add_bias(1, 416, 512)
-            copy_gated(5)
+            gate(5, 0)
             mix(6, 1)
-            store(1)
+            gate(5, 1)
+            turn_gated(5)
+            copy_gated(5)
             quant_gated(3)
             project(3, ps_qk, "qk_bank")
+            evacuate(3)
             quant_attn(7)
             mix(7, 0)
-            quant_gated(4)
-            project(4, ps_qk, "qk_bank")
             add_on_gpsimd(2)
+            quant_gated(4)
+            project(4, ps_o, "o_bank")
+            add_bias(1, D1, D)
+            store(1)
             store(2)
             gate(6, 0)
-            evacuate(4, 0, 256)
             mix(7, 1)
             gate(6, 1)
             turn_gated(6)
-            add_bias(3)
-            copy_gated(6)
+            add_on_gpsimd(3)
             store(3)
+            copy_gated(6)
             quant_gated(5)
-            project(5, ps_o, "o_bank")
-            add_on_gpsimd(4, 0, 256)
+            project(5, ps_qk, "qk_bank")
             gate(7, 0)
             turn_gated(7, 0, 1)
-            gate(7, 1)
             copy_gated(7, 0, 1)
+            gate(7, 1)
             turn_gated(7, 1, 2)
-            add_bias(4, 256, 512)
             copy_gated(7, 1, 2)
-            store(4)
             quant_gated(6)
             project(6, ps_qk, "qk_bank")
-            add_bias(5)
-            store(5)
+            add_bias(4)
+            store(4)
             quant_gated(7, 0, 1)
             project_last(0)
+            add_bias(5)
+            store(5)
             quant_gated(7, 1, 2)
             project_last(1)
             add_bias(6, 0, 256)
             store(6, 0, 256)
-            add_bias(6, 256, 512)
-            store(6, 256, 512)
+            add_bias(6, 256, D)
+            store(6, 256, D)
             add_last(0)
             store(7, 0, 256)
             add_last(1)
-            store(7, 256, 512)
+            store(7, 256, D)

@@ -249,11 +249,11 @@ def tile_gatedattentionunit_pb_w4_kernel(tc, q, k, u, v_bytes, v_scale, W_o_word
             nc.sync.dma_start(out=out[b].rearrange("(p i) d -> p i d", i=NT)[:, i, d0:d1], in_=result[j][:, d0:d1])
 
         def warm_up(count):
-            bank = ps_av.tile([P, T, P], F32, name="av_bank")
+            bank = ps_av.tile([P, 2, P], F32, name="av_bank")
             for n in range(count):
-                nc.tensor.matmul(bank[:], lhsT=id_bf[:], rhs=id_bf[:].unsqueeze(1).to_broadcast([P, T, P]), start=True, stop=True)
+                nc.tensor.matmul(bank[:], lhsT=id_f[:], rhs=id_f[:].unsqueeze(1).to_broadcast([P, 2, P]), start=True, stop=True)
 
-        make_identity(nc, id_bf[:])
+        make_identity(nc, id_f[:])
         with tc.manual_schedule():
             nc.scalar.dma_start(out=vs[:], in_=v_scale.rearrange("o (p t) x -> p (o t x)", t=T))
             nc.vector.memset(ws_sb[:].bitcast(I32), 0)
@@ -272,7 +272,7 @@ def tile_gatedattentionunit_pb_w4_kernel(tc, q, k, u, v_bytes, v_scale, W_o_word
             load_u(2, NT)
             nc.sync.dma_start(out=b_bc[:], in_=b_o.partition_broadcast(P))
             load_u(NT, TILES)
-            nc.scalar.activation(id_f[:], id_bf[:], ACT.Copy)
+            nc.scalar.activation(id_bf[:], id_f[:], ACT.Copy)
 
             warm_up(2)
             widen_on_scalar(0, 0, KP, H)

@@ -28,8 +28,8 @@ G = H // KP
 BANK_COLS = 256
 QK_SCALE = 1.0 / math.sqrt(S)
 HELPED = (0, 1, 2, 3)
-C0, C1, C2 = 320, 704, 896
-D1 = 256
+C0, C1 = 448, 672
+D1, D2 = 416, 448
 
 
 def tile_gatedattentionunit_pb_w4_kernel(tc, q, k, u, v_bytes, v_scale, W_o_words, W_o_scales, b_o, out):
@@ -56,7 +56,8 @@ def tile_gatedattentionunit_pb_w4_kernel(tc, q, k, u, v_bytes, v_scale, W_o_word
         v_s = [kt([P, H], U8, "v_s%d" % b) for b in range(B)]
         u_sb = [kt([P, H], BF16, "u_sb%d" % j) for j in range(TILES)]
         r_two = [kt([P, 2, P, T], F32, "r_two%d" % j) for j in range(TILES // 2)]
-        il_two = [kt([P, 2, P, T], BF16, "il_two%d" % j) for j in range(TILES // 2)]
+        il_late = kt([P, TILES - 1, P, T], BF16, "il_late")
+        il_two = [v_il[1][:, : 2 * KP].rearrange("p (a n t) -> p a n t", a=2, t=T)] + [il_late[:, j - 2 : j] for j in range(2, TILES, 2)]
         c_two = [kt([P, 2, P], U32, "c_two%d" % j) for j in range(TILES // 2)]
         s_two = [kt([P, 2, P], U8, "s_two%d" % j) for j in range(TILES // 2)]
         gt = [[kt([P, KP], BF16, "gt%d_%d" % (j, g)) for g in range(G)] for j in range(TILES)]
@@ -74,10 +75,10 @@ def tile_gatedattentionunit_pb_w4_kernel(tc, q, k, u, v_bytes, v_scale, W_o_word
 
         banks = {}
         result = {j: o_sb[j][:] for j in o_sb}
-        gT[0] = v_il[1][:, 384 * T : 640 * T].rearrange("p (g n t) -> p g n t", g=G, t=T)
-        result[0] = v_il[1][:, 768 * T :].bitcast(F32)
+        gT[0] = v_il[1][:, 672 * T : 928 * T].rearrange("p (g n t) -> p g n t", g=G, t=T)
+        result[0] = il_late[:, 3:5].rearrange("p a n t -> p (a n t)").bitcast(F32)
         result[1] = v_il[1][:, 512 * T : 768 * T].bitcast(F32)
-        result[2] = il_two[3][:].rearrange("p a n t -> p (a n t)").bitcast(F32)
+        result[2] = il_late[:, 5:7].rearrange("p a n t -> p (a n t)").bitcast(F32)
         result[3] = u_sb[6][:].bitcast(F32)
 
         def load_u(j0, j1):
@@ -220,9 +221,10 @@ def tile_gatedattentionunit_pb_w4_kernel(tc, q, k, u, v_bytes, v_scale, W_o_word
                 stop=(g == G - 1),
             )
 
-        def project(j, pool, name):
-            banks["o", j] = pool.tile([P, D], F32, name=name)
-            for g in range(G):
+        def project(j, pool, name, g0=0, g1=G):
+            if g0 == 0:
+                banks["o", j] = pool.tile([P, D], F32, name=name)
+            for g in range(g0, g1):
                 project_pass(banks["o", j], j, g, 0, D)
 
         def project_last(g):
@@ -280,6 +282,7 @@ def tile_gatedattentionunit_pb_w4_kernel(tc, q, k, u, v_bytes, v_scale, W_o_word
             widen_on_scalar(0, 1, KP, H)
             turn_first("q", [q_sb[0][:, i, :] for i in range(1, NT)])
             widen_on_scalar(0, 2, KP, H)
+            warm_up(1)
             copy_first("k", 0, T + 1)
             scores(0)
             copy_first("q", T + 1, T + NT)
@@ -287,100 +290,97 @@ def tile_gatedattentionunit_pb_w4_kernel(tc, q, k, u, v_bytes, v_scale, W_o_word
             widen_on_scalar(1, 0)
             turn_kq(1)
             relu(0)
-            scores(2)
             relu(1)
-            scores(3)
             square(0)
             square(1)
-            relu(2)
-            relu(3)
-            copy_kq(1)
-            square(2, 2)
             widen_on_vector(0, 0, 0, KP)
             widen_on_vector(0, 1, 0, KP)
             widen_on_vector(0, 2, 0, KP)
             widen_on_vector(0, 3, 0, KP)
             widen_on_vector(0, 3, KP, H)
             weave_on_vector(0, 0, KP)
-            weave_on_vector(0, KP, H)
-            quant_v(0, 0, KP)
             widen_on_vector(1, 1)
-            quant_v(0, KP, H)
+            weave_on_tensor(1, C0, C1, 0, ps_o, "o_bank")
+            scores(2)
+            relu(2)
+            scores(3)
+            relu(3)
+            copy_kq(1)
+            square(2, 2)
+            quant_v(0, 0, KP)
+            widen_on_vector(1, 2)
+            weave_on_vector(0, KP, H)
             quant_attn(0)
             mix(0, 0)
-            mix(0, 1)
-            widen_on_vector(1, 2)
-            widen_on_vector(1, 3, 0, C0)
-            weave_on_gpsimd(1, 0, C0)
+            widen_on_vector(1, 3, 0, C1)
+            weave_on_tensor(1, C0, C1, 1, ps_o, "o_bank")
             quant_attn(1)
             mix(1, 0)
+            weave_on_gpsimd(1, 0, C0)
+            quant_v(0, KP, H)
+            mix(0, 1)
             gate(0, 0)
             mix(1, 1)
+            scores(4)
+            relu(4)
+            copy_woven_on_vector(1, C0, C1)
             gate(0, 1)
             turn_gated(0)
             copy_gated(0)
-            scores(4)
-            relu(4)
-            weave_on_tensor(1, C1, C2, 0, ps_o, "o_bank")
             scores(5)
             relu(5)
             gate(1, 0)
             gate(1, 1)
             turn_gated(1)
             copy_gated(1)
+            square(4, 2)
             quant_attn(2, 2)
             mix(2, 0)
             mix(2, 1)
-            widen_on_vector(1, 3, C0, H)
-            weave_on_tensor(1, C1, C2, 1, ps_o, "o_bank")
-            copy_woven(1, C1, C2)
             mix(3, 0)
-            square(4, 2)
-            weave_on_tensor(1, C2, H, 0, ps_qk, "qk_bank")
-            weave_on_tensor(1, C2, H, 1, ps_qk, "qk_bank")
-            quant_gated(0)
-            weave_on_gpsimd(1, C0, C1)
-            quant_v(1, 0, 256)
-            gate(2, 0)
-            mix(3, 1)
             scores(6)
             relu(6)
+            widen_on_vector(1, 3, C1, H)
+            quant_gated(0)
+            project(0, ps_o, "o_bank")
+            weave_on_gpsimd(1, C1, H)
+            evacuate(0)
+            square(6)
+            quant_v(1, 0, KP)
+            gate(2, 0)
+            mix(3, 1)
             gate(2, 1)
             turn_gated(2)
             copy_gated(2)
-            project(0, ps_o, "o_bank")
-            square(6)
-            evacuate(0)
-            gate(3, 0)
-            copy_woven_on_vector(1, C2, H)
             scores(7)
+            relu(7)
+            gate(3, 0)
             gate(3, 1)
             turn_gated(3)
+            quant_attn(4, 2)
+            mix(4, 0)
             quant_gated(1)
             project(1, ps_qk, "qk_bank")
             evacuate(1, 0, D1)
-            relu(7)
             copy_gated(3)
             square(7)
-            quant_attn(4, 2)
-            quant_v(1, 256, 640)
-            mix(4, 0)
-            quant_v(1, 640, H)
+            quant_v(1, KP, H)
             mix(4, 1)
+            mix(5, 0)
+            quant_attn(6)
             add_on_gpsimd(0)
             store(0)
-            mix(5, 0)
             add_on_gpsimd(1, 0, D1)
             quant_gated(2)
-            project(2, ps_o, "o_bank")
-            quant_attn(6)
+            project(2, ps_o, "o_bank", 0, 1)
             gate(4, 0)
             mix(5, 1)
             gate(4, 1)
             turn_gated(4)
             copy_gated(4)
+            project(2, ps_o, "o_bank", 1, 2)
+            evacuate(2, 0, D2)
             mix(6, 0)
-            evacuate(2)
             gate(5, 0)
             mix(6, 1)
             gate(5, 1)
@@ -391,35 +391,37 @@ def tile_gatedattentionunit_pb_w4_kernel(tc, q, k, u, v_bytes, v_scale, W_o_word
             evacuate(3)
             quant_attn(7)
             mix(7, 0)
-            add_on_gpsimd(2)
+            add_on_gpsimd(2, 0, D2)
             quant_gated(4)
-            project(4, ps_o, "o_bank")
             add_bias(1, D1, D)
+            project(4, ps_qk, "qk_bank", 0, 1)
             store(1)
-            store(2)
             gate(6, 0)
             mix(7, 1)
+            add_bias(2, D2, D)
+            store(2)
             gate(6, 1)
             turn_gated(6)
             add_on_gpsimd(3)
             store(3)
             copy_gated(6)
+            project(4, ps_qk, "qk_bank", 1, 2)
             quant_gated(5)
-            project(5, ps_qk, "qk_bank")
+            project(5, ps_o, "o_bank")
             gate(7, 0)
             turn_gated(7, 0, 1)
             copy_gated(7, 0, 1)
             gate(7, 1)
             turn_gated(7, 1, 2)
             copy_gated(7, 1, 2)
-            quant_gated(6)
-            project(6, ps_qk, "qk_bank")
             add_bias(4)
             store(4)
-            quant_gated(7, 0, 1)
-            project_last(0)
+            quant_gated(6)
+            project(6, ps_qk, "qk_bank")
             add_bias(5)
             store(5)
+            quant_gated(7, 0, 1)
+            project_last(0)
             quant_gated(7, 1, 2)
             project_last(1)
             add_bias(6, 0, 256)

@@ -28,21 +28,21 @@ G = H // KP
 BANK_COLS = 256
 QK_SCALE = 1.0 / math.sqrt(S)
 HELPED = (0, 1, 2, 3)
-C0, C1 = 448, 672
-D1, D2 = 416, 448
+C0, C1 = 440, 688
+D1, D2 = 320, 480
 
 
 def tile_gatedattentionunit_pb_w4_kernel(tc, q, k, u, v_bytes, v_scale, W_o_words, W_o_scales, b_o, out):
     nc = tc.nc
     with ExitStack() as ctx:
         keep = ctx.enter_context(tc.tile_pool(name="keep", bufs=1))
-        ps_tr = ctx.enter_context(tc.psum_pool(name="ps_tr", bufs=2))
-        ps_qk = ctx.enter_context(tc.psum_pool(name="ps_qk", bufs=2))
-        ps_av = ctx.enter_context(tc.psum_pool(name="ps_av", bufs=3))
-        ps_o = ctx.enter_context(tc.psum_pool(name="ps_o", bufs=1))
+        ps_mm = ctx.enter_context(tc.psum_pool(name="ps_mm", bufs=1))
 
         def kt(shape, dt, name):
             return keep.tile(shape, dt, name=name, align_bytes=64)
+
+        def in_bank(n, shape, dt):
+            return ps_mm.tile(shape, dt, name="bank%d" % n)
 
         k_sb = [kt([P, T, S], BF16, "k_sb%d" % b) for b in range(B)]
         q_sb = [kt([P, NT, S], BF16, "q_sb%d" % b) for b in range(B)]
@@ -75,11 +75,11 @@ def tile_gatedattentionunit_pb_w4_kernel(tc, q, k, u, v_bytes, v_scale, W_o_word
 
         banks = {}
         result = {j: o_sb[j][:] for j in o_sb}
-        gT[0] = v_il[1][:, 672 * T : 928 * T].rearrange("p (g n t) -> p g n t", g=G, t=T)
+        gT[0] = v_il[1][:, 688 * T : 944 * T].rearrange("p (g n t) -> p g n t", g=G, t=T)
         result[0] = il_late[:, 3:5].rearrange("p a n t -> p (a n t)").bitcast(F32)
         result[1] = v_il[1][:, 512 * T : 768 * T].bitcast(F32)
         result[2] = il_late[:, 5:7].rearrange("p a n t -> p (a n t)").bitcast(F32)
-        result[3] = u_sb[6][:].bitcast(F32)
+        result[3] = gT[4][:].rearrange("p g n t -> p (g n t)").bitcast(F32)
 
         def load_u(j0, j1):
             for j in range(j0, j1):
@@ -101,16 +101,16 @@ def tile_gatedattentionunit_pb_w4_kernel(tc, q, k, u, v_bytes, v_scale, W_o_word
         def load_q_first(i0, i1):
             nc.sync.dma_start(out=q_sb[0][:, i0:i1, :], in_=q[0].rearrange("(p i) s -> p i s", i=NT)[:, i0:i1, :])
 
-        def turn_first(name, srcs):
-            bank = banks[name] = ps_tr.tile([P, len(srcs), P], BF16, name="tr_bank")
-            for n, src in enumerate(srcs):
-                nc.tensor.transpose(bank[:, n, :], src, id_bf[:])
+        def turn_first(name, n, srcs):
+            bank = banks[name] = in_bank(n, [P, len(srcs), P], BF16)
+            for m, src in enumerate(srcs):
+                nc.tensor.transpose(bank[:, m, :], src, id_bf[:])
 
         def copy_first(name, n0, n1):
             nc.scalar.copy(out=kqT[0][:, n0:n1, :], in_=banks[name][:])
 
-        def turn_kq(b):
-            bank = banks["kq", b] = ps_tr.tile([P, T + NT, P], BF16, name="tr_bank")
+        def turn_kq(b, n):
+            bank = banks["kq", b] = in_bank(n, [P, T + NT, P], BF16)
             for t in range(T):
                 nc.tensor.transpose(bank[:, t, :], k_sb[b][:, t, :], id_bf[:])
             for i in range(NT):
@@ -138,9 +138,9 @@ def tile_gatedattentionunit_pb_w4_kernel(tc, q, k, u, v_bytes, v_scale, W_o_word
             src = v_bf[b][:, :, c0:c1].rearrange("p t c -> p c t")
             nc.gpsimd.tensor_scalar(out=dst, in0=src, scalar1=1.0, scalar2=0.0, op0=ALU.mult, op1=ALU.add)
 
-        def weave_on_tensor(b, c0, c1, half, pool, name, parts=2):
+        def weave_on_tensor(b, c0, c1, half, n, parts=2):
             if half == 0:
-                banks["v", b, c0] = pool.tile([P, (c1 - c0) * T], BF16, name=name)
+                banks["v", b, c0] = in_bank(n, [P, (c1 - c0) * T], BF16)
             slots = slice(T // parts * half, T // parts * (half + 1))
             dst = banks["v", b, c0][:].rearrange("p (c t) -> p t c", t=T)[:, slots, :]
             nc.tensor.matmul(dst, lhsT=id_bf[:], rhs=v_bf[b][:, slots, c0:c1], start=True, stop=True)
@@ -154,9 +154,9 @@ def tile_gatedattentionunit_pb_w4_kernel(tc, q, k, u, v_bytes, v_scale, W_o_word
         def quant_v(b, c0, c1):
             nc.vector.quantize_mx(out=v_c[b][:, c0:c1].bitcast(FP8X4), scales=v_s[b][:, c0:c1], in_=v_il[b][:, c0 * T : c1 * T])
 
-        def scores(j):
+        def scores(j, n):
             b, i = divmod(j, NT)
-            bank = banks["qk", j] = ps_qk.tile([P, T, P], F32, name="qk_bank")
+            bank = banks["qk", j] = in_bank(n, [P, T, P], F32)
             for t in range(T):
                 nc.tensor.matmul(bank[:, t, :], lhsT=kqT[b][:, t, :], rhs=kqT[b][:, T + i, :], start=True, stop=True)
 
@@ -175,9 +175,9 @@ def tile_gatedattentionunit_pb_w4_kernel(tc, q, k, u, v_bytes, v_scale, W_o_word
                 in_=il_two[j // 2][:, a].rearrange("p a n t -> p (a n t)"),
             )
 
-        def mix(j, g):
+        def mix(j, g, n):
             cols = slice(KP * g, KP * (g + 1))
-            bank = banks["av", j, g] = ps_av.tile([P, KP], F32, name="av_bank")
+            bank = banks["av", j, g] = in_bank(n, [P, KP], F32)
             nc.tensor.matmul_mx(
                 out=bank[:],
                 lhsT=c_two[j // 2][:, j % 2].bitcast(FP8X4),
@@ -193,8 +193,8 @@ def tile_gatedattentionunit_pb_w4_kernel(tc, q, k, u, v_bytes, v_scale, W_o_word
             gate_in = u_sb[j][:, KP * g : KP * (g + 1)].rearrange("n (p w e) -> n w p e", w=2, e=2)
             nc.vector.tensor_tensor(out=gt[j][g][:].rearrange("n (w p e) -> n w p e", w=2, e=2), in0=av, in1=gate_in, op=ALU.mult)
 
-        def turn_gated(j, g0=0, g1=G):
-            bank = banks["tg", j, g0] = ps_tr.tile([P, g1 - g0, 2, P], F32, name="tr_bank")
+        def turn_gated(j, n, g0=0, g1=G):
+            bank = banks["tg", j, g0] = in_bank(n, [P, g1 - g0, 2, P], F32)
             for g in range(g0, g1):
                 words = gt[j][g][:].bitcast(F32)
                 for w in range(2):
@@ -221,16 +221,16 @@ def tile_gatedattentionunit_pb_w4_kernel(tc, q, k, u, v_bytes, v_scale, W_o_word
                 stop=(g == G - 1),
             )
 
-        def project(j, pool, name, g0=0, g1=G):
+        def project(j, n, g0=0, g1=G):
             if g0 == 0:
-                banks["o", j] = pool.tile([P, D], F32, name=name)
+                banks["o", j] = in_bank(n, [P, D], F32)
             for g in range(g0, g1):
                 project_pass(banks["o", j], j, g, 0, D)
 
-        def project_last(g):
-            for c in range(2):
+        def project_last(g, n, c0=0, c1=2):
+            for c in range(c0, c1):
                 if g == 0:
-                    banks["last", c] = ps_av.tile([P, D // 2], F32, name="av_bank")
+                    banks["last", c] = in_bank(n + c, [P, D // 2], F32)
                 project_pass(banks["last", c], LAST, g, D // 2 * c, D // 2 * (c + 1))
 
         def add_bias(j, d0=0, d1=D):
@@ -250,9 +250,9 @@ def tile_gatedattentionunit_pb_w4_kernel(tc, q, k, u, v_bytes, v_scale, W_o_word
             b, i = divmod(j, NT)
             nc.sync.dma_start(out=out[b].rearrange("(p i) d -> p i d", i=NT)[:, i, d0:d1], in_=result[j][:, d0:d1])
 
-        def warm_up(count):
-            bank = ps_av.tile([P, 2, P], F32, name="av_bank")
-            for n in range(count):
+        def warm_up(count, n):
+            bank = in_bank(n, [P, 2, P], F32)
+            for _ in range(count):
                 nc.tensor.matmul(bank[:], lhsT=id_f[:], rhs=id_f[:].unsqueeze(1).to_broadcast([P, 2, P]), start=True, stop=True)
 
         make_identity(nc, id_f[:])
@@ -276,19 +276,19 @@ def tile_gatedattentionunit_pb_w4_kernel(tc, q, k, u, v_bytes, v_scale, W_o_word
             load_u(NT, TILES)
             nc.scalar.activation(id_bf[:], id_f[:], ACT.Copy)
 
-            warm_up(2)
+            warm_up(2, 0)
             widen_on_scalar(0, 0, KP, H)
-            turn_first("k", [k_sb[0][:, t, :] for t in range(T)] + [q_sb[0][:, 0, :]])
+            turn_first("k", 6, [k_sb[0][:, t, :] for t in range(T)] + [q_sb[0][:, 0, :]])
             widen_on_scalar(0, 1, KP, H)
-            turn_first("q", [q_sb[0][:, i, :] for i in range(1, NT)])
+            turn_first("q", 7, [q_sb[0][:, i, :] for i in range(1, NT)])
             widen_on_scalar(0, 2, KP, H)
-            warm_up(1)
+            warm_up(1, 3)
             copy_first("k", 0, T + 1)
-            scores(0)
+            scores(0, 0)
             copy_first("q", T + 1, T + NT)
-            scores(1)
+            scores(1, 1)
             widen_on_scalar(1, 0)
-            turn_kq(1)
+            turn_kq(1, 6)
             relu(0)
             relu(1)
             square(0)
@@ -300,10 +300,10 @@ def tile_gatedattentionunit_pb_w4_kernel(tc, q, k, u, v_bytes, v_scale, W_o_word
             widen_on_vector(0, 3, KP, H)
             weave_on_vector(0, 0, KP)
             widen_on_vector(1, 1)
-            weave_on_tensor(1, C0, C1, 0, ps_o, "o_bank")
-            scores(2)
+            weave_on_tensor(1, C0, C1, 0, 2)
+            scores(2, 0)
             relu(2)
-            scores(3)
+            scores(3, 1)
             relu(3)
             copy_kq(1)
             square(2, 2)
@@ -311,119 +311,120 @@ def tile_gatedattentionunit_pb_w4_kernel(tc, q, k, u, v_bytes, v_scale, W_o_word
             widen_on_vector(1, 2)
             weave_on_vector(0, KP, H)
             quant_attn(0)
-            mix(0, 0)
+            mix(0, 0, 3)
             widen_on_vector(1, 3, 0, C1)
-            weave_on_tensor(1, C0, C1, 1, ps_o, "o_bank")
+            weave_on_tensor(1, C0, C1, 1, 2)
             quant_attn(1)
-            mix(1, 0)
+            mix(1, 0, 4)
             weave_on_gpsimd(1, 0, C0)
             quant_v(0, KP, H)
-            mix(0, 1)
+            mix(0, 1, 5)
             gate(0, 0)
-            mix(1, 1)
-            scores(4)
+            mix(1, 1, 3)
+            scores(4, 0)
             relu(4)
+            scores(5, 1)
             copy_woven_on_vector(1, C0, C1)
             gate(0, 1)
-            turn_gated(0)
+            turn_gated(0, 7)
             copy_gated(0)
-            scores(5)
+            scores(7, 2)
             relu(5)
             gate(1, 0)
             gate(1, 1)
-            turn_gated(1)
+            turn_gated(1, 6)
             copy_gated(1)
             square(4, 2)
             quant_attn(2, 2)
-            mix(2, 0)
-            mix(2, 1)
-            mix(3, 0)
-            scores(6)
+            mix(2, 0, 5)
+            mix(2, 1, 4)
+            mix(3, 0, 3)
+            scores(6, 0)
             relu(6)
+            mix(3, 1, 7)
             widen_on_vector(1, 3, C1, H)
             quant_gated(0)
-            project(0, ps_o, "o_bank")
+            project(0, 1)
             weave_on_gpsimd(1, C1, H)
             evacuate(0)
             square(6)
             quant_v(1, 0, KP)
             gate(2, 0)
-            mix(3, 1)
             gate(2, 1)
-            turn_gated(2)
+            turn_gated(2, 6)
             copy_gated(2)
-            scores(7)
             relu(7)
             gate(3, 0)
             gate(3, 1)
-            turn_gated(3)
+            turn_gated(3, 5)
             quant_attn(4, 2)
-            mix(4, 0)
+            mix(4, 0, 4)
             quant_gated(1)
-            project(1, ps_qk, "qk_bank")
+            project(1, 1)
             evacuate(1, 0, D1)
             copy_gated(3)
             square(7)
             quant_v(1, KP, H)
-            mix(4, 1)
-            mix(5, 0)
+            mix(4, 1, 3)
+            mix(5, 0, 7)
+            mix(5, 1, 0)
             quant_attn(6)
             add_on_gpsimd(0)
             store(0)
             add_on_gpsimd(1, 0, D1)
             quant_gated(2)
-            project(2, ps_o, "o_bank", 0, 1)
-            gate(4, 0)
-            mix(5, 1)
-            gate(4, 1)
-            turn_gated(4)
-            copy_gated(4)
-            project(2, ps_o, "o_bank", 1, 2)
+            project(2, 6)
             evacuate(2, 0, D2)
-            mix(6, 0)
+            mix(6, 0, 2)
+            gate(4, 0)
+            mix(6, 1, 4)
+            gate(4, 1)
+            turn_gated(4, 5)
+            copy_gated(4)
             gate(5, 0)
-            mix(6, 1)
             gate(5, 1)
-            turn_gated(5)
+            turn_gated(5, 3)
             copy_gated(5)
-            quant_gated(3)
-            project(3, ps_qk, "qk_bank")
-            evacuate(3)
             quant_attn(7)
-            mix(7, 0)
             add_on_gpsimd(2, 0, D2)
-            quant_gated(4)
+            quant_gated(3)
+            project(3, 0)
+            evacuate(3)
+            mix(7, 0, 7)
             add_bias(1, D1, D)
-            project(4, ps_qk, "qk_bank", 0, 1)
+            mix(7, 1, 1)
             store(1)
             gate(6, 0)
-            mix(7, 1)
             add_bias(2, D2, D)
             store(2)
             gate(6, 1)
-            turn_gated(6)
+            turn_gated(6, 2)
+            copy_gated(6)
+            quant_gated(4)
+            project(4, 5)
             add_on_gpsimd(3)
             store(3)
-            copy_gated(6)
-            project(4, ps_qk, "qk_bank", 1, 2)
             quant_gated(5)
-            project(5, ps_o, "o_bank")
+            project(5, 6)
             gate(7, 0)
-            turn_gated(7, 0, 1)
+            turn_gated(7, 3, 0, 1)
             copy_gated(7, 0, 1)
             gate(7, 1)
-            turn_gated(7, 1, 2)
+            turn_gated(7, 4, 1, 2)
             copy_gated(7, 1, 2)
-            add_bias(4)
-            store(4)
+            add_bias(4, 0, 256)
             quant_gated(6)
-            project(6, ps_qk, "qk_bank")
+            project(6, 7)
+            add_bias(4, 256, D)
+            store(4)
             add_bias(5)
             store(5)
             quant_gated(7, 0, 1)
-            project_last(0)
+            project_last(0, 0, 0, 1)
             quant_gated(7, 1, 2)
-            project_last(1)
+            project_last(1, 0, 0, 1)
+            project_last(0, 0, 1, 2)
+            project_last(1, 0, 1, 2)
             add_bias(6, 0, 256)
             store(6, 0, 256)
             add_bias(6, 256, D)

@@ -28,8 +28,8 @@ G = H // KP
 BANK_COLS = 256
 QK_SCALE = 1.0 / math.sqrt(S)
 HELPED = (0, 1, 2, 3)
-C0, C1 = 440, 688
-D1, D2 = 320, 480
+C0, C1 = 448, 680
+D1, D2 = 352, 480
 
 
 def tile_gatedattentionunit_pb_w4_kernel(tc, q, k, u, v_bytes, v_scale, W_o_words, W_o_scales, b_o, out):
@@ -39,7 +39,7 @@ def tile_gatedattentionunit_pb_w4_kernel(tc, q, k, u, v_bytes, v_scale, W_o_word
         ps_mm = ctx.enter_context(tc.psum_pool(name="ps_mm", bufs=1))
 
         def kt(shape, dt, name):
-            return keep.tile(shape, dt, name=name, align_bytes=64)
+            return keep.tile(shape, dt, name=name, align_bytes=256)
 
         def in_bank(n, shape, dt):
             return ps_mm.tile(shape, dt, name="bank%d" % n)
@@ -75,7 +75,7 @@ def tile_gatedattentionunit_pb_w4_kernel(tc, q, k, u, v_bytes, v_scale, W_o_word
 
         banks = {}
         result = {j: o_sb[j][:] for j in o_sb}
-        gT[0] = v_il[1][:, 688 * T : 944 * T].rearrange("p (g n t) -> p g n t", g=G, t=T)
+        gT[0] = v_il[1][:, 680 * T : 936 * T].rearrange("p (g n t) -> p g n t", g=G, t=T)
         result[0] = il_late[:, 3:5].rearrange("p a n t -> p (a n t)").bitcast(F32)
         result[1] = v_il[1][:, 512 * T : 768 * T].bitcast(F32)
         result[2] = il_late[:, 5:7].rearrange("p a n t -> p (a n t)").bitcast(F32)

import math
from contextlib import ExitStack

import concourse.mybir as mybir
from concourse.masks import make_identity

B, N, D, H, S = 2, 512, 512, 1024, 128
FLOPS = B * (2 * N * N * S + 2 * N * N * H + 2 * N * H * D)

F32 = mybir.dt.float32
BF16 = mybir.dt.bfloat16
U32 = mybir.dt.uint32
I32 = mybir.dt.int32
U8 = mybir.dt.uint8
FP8 = mybir.dt.float8_e4m3fn
FP8X4 = mybir.dt.float8_e4m3fn_x4
FP4X4 = mybir.dt.float4_e2m1fn_x4
ACT = mybir.ActivationFunctionType
ALU = mybir.AluOpType

P = 128
T = 4
NT = N // P
TILES = B * NT
LAST = TILES - 1
KP = P * T
G = H // KP
BANK_COLS = 256
QK_SCALE = 1.0 / math.sqrt(S)
HELPED = (0, 1, 2, 3)
C0, C1 = 448, 680
D1, D2 = 352, 480


def tile_gatedattentionunit_pb_w4_kernel(tc, q, k, u, v_bytes, v_scale, W_o_words, W_o_scales, b_o, out):
    nc = tc.nc
    with ExitStack() as ctx:
        keep = ctx.enter_context(tc.tile_pool(name="keep", bufs=1))
        ps_mm = ctx.enter_context(tc.psum_pool(name="ps_mm", bufs=1))

        def kt(shape, dt, name):
            return keep.tile(shape, dt, name=name, align_bytes=256)

        def in_bank(n, shape, dt):
            return ps_mm.tile(shape, dt, name="bank%d" % n)

        k_sb = [kt([P, T, S], BF16, "k_sb%d" % b) for b in range(B)]
        q_sb = [kt([P, NT, S], BF16, "q_sb%d" % b) for b in range(B)]
        kqT = [kt([P, T + NT, P], BF16, "kqT%d" % b) for b in range(B)]
        vb0 = [kt([P, H], U8, "vb0_%d" % t) for t in range(T)]
        vb1 = [kt([P, 2, H], U8, "vb1_%d" % c) for c in range(2)]
        v_raw = [[vb0[t][:] for t in range(T)], [vb1[t // 2][:, t % 2, :] for t in range(T)]]
        v_bf = [kt([P, T, H], BF16, "v_bf%d" % b) for b in range(B)]
        v_il = [kt([P, H * T], BF16, "v_il%d" % b) for b in range(B)]
        v_c = [kt([P, H], U32, "v_c%d" % b) for b in range(B)]
        v_s = [kt([P, H], U8, "v_s%d" % b) for b in range(B)]
        u_sb = [kt([P, H], BF16, "u_sb%d" % j) for j in range(TILES)]
        r_two = [kt([P, 2, P, T], F32, "r_two%d" % j) for j in range(TILES // 2)]
        il_late = kt([P, TILES - 1, P, T], BF16, "il_late")
        il_two = [v_il[1][:, : 2 * KP].rearrange("p (a n t) -> p a n t", a=2, t=T)] + [il_late[:, j - 2 : j] for j in range(2, TILES, 2)]
        c_two = [kt([P, 2, P], U32, "c_two%d" % j) for j in range(TILES // 2)]
        s_two = [kt([P, 2, P], U8, "s_two%d" % j) for j in range(TILES // 2)]
        gt = [[kt([P, KP], BF16, "gt%d_%d" % (j, g)) for g in range(G)] for j in range(TILES)]
        gT = [kt([P, G, P, T], BF16, "gT%d" % j) for j in range(TILES)]
        gc = [kt([P, G, P], U32, "gc%d" % j) for j in range(TILES)]
        gs = [kt([P, G, P], U8, "gs%d" % j) for j in range(TILES)]
        o_sb = {j: kt([P, D], F32, "o_sb%d" % j) for j in range(TILES) if j not in HELPED}
        o_raw = {j: kt([P, D], F32, "o_raw%d" % j) for j in HELPED}
        vs = kt([P, T], F32, "vs")
        w_sb = kt([P, G, 2 * D], U8, "w_sb")
        ws_sb = kt([P, G, D], U8, "ws_sb")
        b_bc = kt([P, D], BF16, "b_bc")
        id_bf = kt([P, P], BF16, "id_bf")
        id_f = kt([P, P], F32, "id_f")

        banks = {}
        result = {j: o_sb[j][:] for j in o_sb}
        gT[0] = v_il[1][:, 680 * T : 936 * T].rearrange("p (g n t) -> p g n t", g=G, t=T)
        result[0] = il_late[:, 3:5].rearrange("p a n t -> p (a n t)").bitcast(F32)
        result[1] = v_il[1][:, 512 * T : 768 * T].bitcast(F32)
        result[2] = il_late[:, 5:7].rearrange("p a n t -> p (a n t)").bitcast(F32)
        result[3] = gT[4][:].rearrange("p g n t -> p (g n t)").bitcast(F32)

        def load_u(j0, j1):
            for j in range(j0, j1):
                nc.sync.dma_start(out=u_sb[j][:], in_=u[j // NT].rearrange("(p i) h -> p i h", i=NT)[:, j % NT, :])

        def load_w():
            nc.sync.dma_start(out=w_sb[:], in_=W_o_words.rearrange("g p n -> p g n"))
            rows = W_o_scales.bitcast(I32).rearrange("g (q r) n -> r q g n", r=4)
            ws_i = ws_sb[:].bitcast(I32)
            for r in range(4):
                nc.sync.dma_start(out=ws_i[r:P:32, :, :], in_=rows[r])

        def load_k(b):
            nc.sync.dma_start(out=k_sb[b][:], in_=k[b].rearrange("(p t) s -> p t s", t=T))

        def load_q(b):
            nc.sync.dma_start(out=q_sb[b][:], in_=q[b].rearrange("(p i) s -> p i s", i=NT))

        def load_q_first(i0, i1):
            nc.sync.dma_start(out=q_sb[0][:, i0:i1, :], in_=q[0].rearrange("(p i) s -> p i s", i=NT)[:, i0:i1, :])

        def turn_first(name, n, srcs):
            bank = banks[name] = in_bank(n, [P, len(srcs), P], BF16)
            for m, src in enumerate(srcs):
                nc.tensor.transpose(bank[:, m, :], src, id_bf[:])

        def copy_first(name, n0, n1):
            nc.scalar.copy(out=kqT[0][:, n0:n1, :], in_=banks[name][:])

        def turn_kq(b, n):
            bank = banks["kq", b] = in_bank(n, [P, T + NT, P], BF16)
            for t in range(T):
                nc.tensor.transpose(bank[:, t, :], k_sb[b][:, t, :], id_bf[:])
            for i in range(NT):
                nc.tensor.transpose(bank[:, T + i, :], q_sb[b][:, i, :], id_bf[:])

        def copy_kq(b):
            nc.scalar.copy(out=kqT[b][:], in_=banks["kq", b][:])

        def widen_on_vector(b, t, c0=0, c1=H):
            nc.vector.tensor_scalar(out=v_bf[b][:, t, c0:c1], in0=v_raw[b][t][:, c0:c1].bitcast(FP8), scalar1=vs[:, t : t + 1], scalar2=None, op0=ALU.mult)

        def widen_on_scalar(b, t, c0=0, c1=H):
            nc.scalar.activation(v_bf[b][:, t, c0:c1], v_raw[b][t][:, c0:c1].bitcast(FP8), ACT.Copy, scale=vs[:, t : t + 1])

        def weave_on_vector(b, c0, c1):
            dst = v_il[b][:, c0 * T : c1 * T].rearrange("p (c i t) -> p c t i", i=2, t=T)
            nc.vector.tensor_copy(out=dst, in_=v_bf[b][:, :, c0:c1].rearrange("p t (c i) -> p c t i", i=2))

        def weave_on_scalar(b, c0, c1):
            dst = v_il[b][:, c0 * T : c1 * T].rearrange("p (c i t) -> p c t i", i=2, t=T)
            nc.scalar.copy(out=dst, in_=v_bf[b][:, :, c0:c1].rearrange("p t (c i) -> p c t i", i=2))

        def weave_on_gpsimd(b, c0, c1):
            dst = v_il[b][:, c0 * T : c1 * T].rearrange("p (c t) -> p c t", t=T)
            src = v_bf[b][:, :, c0:c1].rearrange("p t c -> p c t")
            nc.gpsimd.tensor_scalar(out=dst, in0=src, scalar1=1.0, scalar2=0.0, op0=ALU.mult, op1=ALU.add)

        def weave_on_tensor(b, c0, c1, half, n, parts=2):
            if half == 0:
                banks["v", b, c0] = in_bank(n, [P, (c1 - c0) * T], BF16)
            slots = slice(T // parts * half, T // parts * (half + 1))
            dst = banks["v", b, c0][:].rearrange("p (c t) -> p t c", t=T)[:, slots, :]
            nc.tensor.matmul(dst, lhsT=id_bf[:], rhs=v_bf[b][:, slots, c0:c1], start=True, stop=True)

        def copy_woven(b, c0, c1):
            nc.scalar.copy(out=v_il[b][:, c0 * T : c1 * T], in_=banks["v", b, c0][:])

        def copy_woven_on_vector(b, c0, c1):
            nc.vector.tensor_copy(out=v_il[b][:, c0 * T : c1 * T], in_=banks["v", b, c0][:])

        def quant_v(b, c0, c1):
            nc.vector.quantize_mx(out=v_c[b][:, c0:c1].bitcast(FP8X4), scales=v_s[b][:, c0:c1], in_=v_il[b][:, c0 * T : c1 * T])

        def scores(j, n):
            b, i = divmod(j, NT)
            bank = banks["qk", j] = in_bank(n, [P, T, P], F32)
            for t in range(T):
                nc.tensor.matmul(bank[:, t, :], lhsT=kqT[b][:, t, :], rhs=kqT[b][:, T + i, :], start=True, stop=True)

        def relu(j):
            nc.scalar.activation(r_two[j // 2][:, j % 2], banks["qk", j][:].rearrange("p t n -> p n t"), ACT.Relu)

        def square(j, n=1):
            a = slice(j % 2, j % 2 + n)
            nc.scalar.activation(il_two[j // 2][:, a], r_two[j // 2][:, a], ACT.Square, scale=QK_SCALE)

        def quant_attn(j, n=1):
            a = slice(j % 2, j % 2 + n)
            nc.vector.quantize_mx(
                out=c_two[j // 2][:, a].rearrange("p a n -> p (a n)").bitcast(FP8X4),
                scales=s_two[j // 2][:, a].rearrange("p a n -> p (a n)"),
                in_=il_two[j // 2][:, a].rearrange("p a n t -> p (a n t)"),
            )

        def mix(j, g, n):
            cols = slice(KP * g, KP * (g + 1))
            bank = banks["av", j, g] = in_bank(n, [P, KP], F32)
            nc.tensor.matmul_mx(
                out=bank[:],
                lhsT=c_two[j // 2][:, j % 2].bitcast(FP8X4),
                lhsT_scale=s_two[j // 2][:, j % 2],
                rhs=v_c[j // NT][:, cols].bitcast(FP8X4),
                rhs_scale=v_s[j // NT][:, cols],
                start=True,
                stop=True,
            )

        def gate(j, g):
            av = banks["av", j, g][:].rearrange("n (p w e) -> n w p e", w=2, e=2)
            gate_in = u_sb[j][:, KP * g : KP * (g + 1)].rearrange("n (p w e) -> n w p e", w=2, e=2)
            nc.vector.tensor_tensor(out=gt[j][g][:].rearrange("n (w p e) -> n w p e", w=2, e=2), in0=av, in1=gate_in, op=ALU.mult)

        def turn_gated(j, n, g0=0, g1=G):
            bank = banks["tg", j, g0] = in_bank(n, [P, g1 - g0, 2, P], F32)
            for g in range(g0, g1):
                words = gt[j][g][:].bitcast(F32)
                for w in range(2):
                    nc.tensor.transpose(bank[:, g - g0, w, :], words[:, P * w : P * (w + 1)], id_f[:])

        def copy_gated(j, g0=0, g1=G):
            nc.scalar.copy(out=gT[j][:, g0:g1].bitcast(F32), in_=banks["tg", j, g0][:].rearrange("p g w n -> p g n w"))

        def quant_gated(j, g0=0, g1=G):
            nc.vector.quantize_mx(
                out=gc[j][:, g0:g1].rearrange("p g n -> p (g n)").bitcast(FP8X4),
                scales=gs[j][:, g0:g1].rearrange("p g n -> p (g n)"),
                in_=gT[j][:, g0:g1].rearrange("p g n t -> p (g n t)"),
            )

        def project_pass(bank, j, g, d0, d1):
            nc.tensor.matmul_mx(
                out=bank[:],
                lhsT=gc[j][:, g, :].bitcast(FP8X4),
                lhsT_scale=gs[j][:, g, :],
                rhs=w_sb[:, g, 2 * d0 : 2 * d1].bitcast(FP4X4),
                rhs_scale=ws_sb[:, g, d0:d1],
                start=(g == 0),
                stop=(g == G - 1),
            )

        def project(j, n, g0=0, g1=G):
            if g0 == 0:
                banks["o", j] = in_bank(n, [P, D], F32)
            for g in range(g0, g1):
                project_pass(banks["o", j], j, g, 0, D)

        def project_last(g, n, c0=0, c1=2):
            for c in range(c0, c1):
                if g == 0:
                    banks["last", c] = in_bank(n + c, [P, D // 2], F32)
                project_pass(banks["last", c], LAST, g, D // 2 * c, D // 2 * (c + 1))

        def add_bias(j, d0=0, d1=D):
            nc.vector.tensor_tensor(out=result[j][:, d0:d1], in0=banks["o", j][:, d0:d1], in1=b_bc[:, d0:d1], op=ALU.add)

        def add_last(c):
            cols = slice(D // 2 * c, D // 2 * (c + 1))
            nc.vector.tensor_tensor(out=result[LAST][:, cols], in0=banks["last", c][:], in1=b_bc[:, cols], op=ALU.add)

        def evacuate(j, d0=0, d1=D):
            nc.scalar.copy(out=o_raw[j][:, d0:d1], in_=banks["o", j][:, d0:d1])

        def add_on_gpsimd(j, d0=0, d1=D):
            nc.gpsimd.tensor_tensor(out=result[j][:, d0:d1], in0=o_raw[j][:, d0:d1], in1=b_bc[:, d0:d1], op=ALU.add)

        def store(j, d0=0, d1=D):
            b, i = divmod(j, NT)
            nc.sync.dma_start(out=out[b].rearrange("(p i) d -> p i d", i=NT)[:, i, d0:d1], in_=result[j][:, d0:d1])

        def warm_up(count, n):
            bank = in_bank(n, [P, 2, P], F32)
            for _ in range(count):
                nc.tensor.matmul(bank[:], lhsT=id_f[:], rhs=id_f[:].unsqueeze(1).to_broadcast([P, 2, P]), start=True, stop=True)

        make_identity(nc, id_f[:])
        with tc.manual_schedule():
            nc.scalar.dma_start(out=vs[:], in_=v_scale.rearrange("o (p t) x -> p (o t x)", t=T))
            nc.vector.memset(ws_sb[:].bitcast(I32), 0)
            rows0 = v_bytes[0].rearrange("(p t) h -> p t h", t=T)
            rows1 = v_bytes[1].rearrange("(p t) h -> p t h", t=T)
            for t in range(T):
                nc.sync.dma_start(out=vb0[t][:], in_=rows0[:, t, :])
            load_k(0)
            load_q(0)
            for c in range(2):
                nc.sync.dma_start(out=vb1[c][:], in_=rows1[:, 2 * c : 2 * c + 2, :])
            load_k(1)
            load_q(1)
            load_u(0, 2)
            load_w()
            load_u(2, NT)
            nc.sync.dma_start(out=b_bc[:], in_=b_o.partition_broadcast(P))
            load_u(NT, TILES)
            nc.scalar.activation(id_bf[:], id_f[:], ACT.Copy)

            warm_up(2, 0)
            widen_on_scalar(0, 0, KP, H)
            turn_first("k", 6, [k_sb[0][:, t, :] for t in range(T)] + [q_sb[0][:, 0, :]])
            widen_on_scalar(0, 1, KP, H)
            turn_first("q", 7, [q_sb[0][:, i, :] for i in range(1, NT)])
            widen_on_scalar(0, 2, KP, H)
            warm_up(1, 3)
            copy_first("k", 0, T + 1)
            scores(0, 0)
            copy_first("q", T + 1, T + NT)
            scores(1, 1)
            widen_on_scalar(1, 0)
            turn_kq(1, 6)
            relu(0)
            relu(1)
            square(0)
            square(1)
            widen_on_vector(0, 0, 0, KP)
            widen_on_vector(0, 1, 0, KP)
            widen_on_vector(0, 2, 0, KP)
            widen_on_vector(0, 3, 0, KP)
            widen_on_vector(0, 3, KP, H)
            weave_on_vector(0, 0, KP)
            widen_on_vector(1, 1)
            weave_on_tensor(1, C0, C1, 0, 2)
            scores(2, 0)
            relu(2)
            scores(3, 1)
            relu(3)
            copy_kq(1)
            square(2, 2)
            quant_v(0, 0, KP)
            widen_on_vector(1, 2)
            weave_on_vector(0, KP, H)
            quant_attn(0)
            mix(0, 0, 3)
            widen_on_vector(1, 3, 0, C1)
            weave_on_tensor(1, C0, C1, 1, 2)
            quant_attn(1)
            mix(1, 0, 4)
            weave_on_gpsimd(1, 0, C0)
            quant_v(0, KP, H)
            mix(0, 1, 5)
            gate(0, 0)
            mix(1, 1, 3)
            scores(4, 0)
            relu(4)
            scores(5, 1)
            copy_woven_on_vector(1, C0, C1)
            gate(0, 1)
            turn_gated(0, 7)
            copy_gated(0)
            scores(7, 2)
            relu(5)
            gate(1, 0)
            gate(1, 1)
            turn_gated(1, 6)
            copy_gated(1)
            square(4, 2)
            quant_attn(2, 2)
            mix(2, 0, 5)
            mix(2, 1, 4)
            mix(3, 0, 3)
            scores(6, 0)
            relu(6)
            mix(3, 1, 7)
            widen_on_vector(1, 3, C1, H)
            quant_gated(0)
            project(0, 1)
            weave_on_gpsimd(1, C1, H)
            evacuate(0)
            square(6)
            quant_v(1, 0, KP)
            gate(2, 0)
            gate(2, 1)
            turn_gated(2, 6)
            copy_gated(2)
            relu(7)
            gate(3, 0)
            gate(3, 1)
            turn_gated(3, 5)
            quant_attn(4, 2)
            mix(4, 0, 4)
            quant_gated(1)
            project(1, 1)
            evacuate(1, 0, D1)
            copy_gated(3)
            square(7)
            quant_v(1, KP, H)
            mix(4, 1, 3)
            mix(5, 0, 7)
            mix(5, 1, 0)
            quant_attn(6)
            add_on_gpsimd(0)
            store(0)
            add_on_gpsimd(1, 0, D1)
            quant_gated(2)
            project(2, 6)
            evacuate(2, 0, D2)
            mix(6, 0, 2)
            gate(4, 0)
            mix(6, 1, 4)
            gate(4, 1)
            turn_gated(4, 5)
            copy_gated(4)
            gate(5, 0)
            gate(5, 1)
            turn_gated(5, 3)
            copy_gated(5)
            quant_attn(7)
            add_on_gpsimd(2, 0, D2)
            quant_gated(3)
            project(3, 0)
            evacuate(3)
            mix(7, 0, 7)
            add_bias(1, D1, D)
            mix(7, 1, 1)
            store(1)
            gate(6, 0)
            add_bias(2, D2, D)
            store(2)
            gate(6, 1)
            turn_gated(6, 2)
            copy_gated(6)
            quant_gated(4)
            project(4, 5)
            add_on_gpsimd(3)
            store(3)
            quant_gated(5)
            project(5, 6)
            gate(7, 0)
            turn_gated(7, 3, 0, 1)
            copy_gated(7, 0, 1)
            gate(7, 1)
            turn_gated(7, 4, 1, 2)
            copy_gated(7, 1, 2)
            add_bias(4, 0, 256)
            quant_gated(6)
            project(6, 7)
            add_bias(4, 256, D)
            store(4)
            add_bias(5)
            store(5)
            quant_gated(7, 0, 1)
            project_last(0, 0, 0, 1)
            quant_gated(7, 1, 2)
            project_last(1, 0, 0, 1)
            project_last(0, 0, 1, 2)
            project_last(1, 0, 1, 2)
            add_bias(6, 0, 256)
            store(6, 0, 256)
            add_bias(6, 256, D)
            store(6, 256, D)
            add_last(0)
            store(7, 0, 256)
            add_last(1)
            store(7, 256, D)
